import numpy as np
import ml_dtypes


def mxq(x, axis, fmt="e4m3"):
    dtype, down = {"e4m3": (ml_dtypes.float8_e4m3fn, 7), "e5m2": (ml_dtypes.float8_e5m2, 14)}[fmt]
    v = np.moveaxis(np.asarray(x, np.float32).astype(ml_dtypes.bfloat16).astype(np.float64), axis, -1)
    blocks = v.reshape(v.shape[:-1] + (-1, 32))
    amax = np.abs(blocks).max(-1, keepdims=True)
    byte = np.maximum(np.where(amax > 0, np.frexp(amax)[1] - 1 + 127, 0) - down, 1)
    scale = np.exp2(byte - 127.0)
    codes = (blocks / scale).astype(np.float32).astype(dtype).astype(np.float64)
    return np.moveaxis((codes * scale).reshape(v.shape), -1, axis)


WIDE = False


def mx_kscale(k):
    if not WIDE:
        return np.ones(k)
    levels = np.array([10, -10, 5, -5, 0])
    if k % 512:
        return np.exp2(np.random.permutation(np.resize(levels, k // 32))).repeat(32)
    a = np.empty((k // 512, 16))
    for p in range(k // 512):
        a[p, :8] = np.random.permutation(np.resize(levels, 8))
        for g in range(8):
            far = levels[np.abs(levels - a[p, g]) >= 10]
            a[p, g + 8] = far[np.random.randint(len(far))]
    return np.exp2(a.ravel()).repeat(32)


BF16 = ml_dtypes.bfloat16


def bf(x):
    return np.asarray(x, np.float32).astype(BF16)


def f64(x):
    return np.asarray(x).astype(np.float64)


B, S, D_MODEL, N_H, D_H, D_CQ, D_CKV, D_HR = 4, 1024, 1024, 4, 128, 512, 512, 128
ROPE_BASE = 10000.0


def rope_cos_sin(seq_len, dim):
    inv_freq = 1.0 / (ROPE_BASE ** (np.arange(0, dim, 2) / dim))
    ang = np.arange(seq_len)[:, None] * inv_freq[None, :]
    return np.cos(ang), np.sin(ang)


def rope(t, cos, sin):
    shp = t.shape
    d2 = shp[-1] // 2
    tr = t.reshape(shp[:-1] + (d2, 2))
    x0, x1 = tr[..., 0], tr[..., 1]
    bshape = (1, shp[1]) + (1,) * (x0.ndim - 3) + (d2,)
    cs, sn = cos.reshape(bshape), sin.reshape(bshape)
    return np.stack([x0 * cs - x1 * sn, x0 * sn + x1 * cs], axis=-1).reshape(shp)


def draw0():
    s, t = mx_kscale(D_MODEL), mx_kscale(D_CQ)
    return {"h": bf(np.random.standard_normal((B, S, D_MODEL)) * s),
            "w_cq": bf(np.random.standard_normal((D_MODEL, D_CQ)) / np.sqrt(D_MODEL) / s[:, None] * t),
            "w_q": bf(np.random.standard_normal((D_CQ, N_H * D_H)) / np.sqrt(D_CQ) / t[:, None]),
            "w_qr": bf(np.random.standard_normal((D_CQ, N_H * D_HR)) / np.sqrt(D_CQ) / t[:, None])}


def core(h, w_cq, w_q, w_qr):
    cos, sin = rope_cos_sin(S, D_HR)
    c_q = mxq(f64(h), 2, "e4m3") @ mxq(f64(w_cq), 0, "e4m3")
    cq = mxq(c_q, 2, "e4m3")
    q_c = (cq @ mxq(f64(w_q), 0, "e4m3")).reshape(B, S, N_H, D_H).transpose(0, 2, 1, 3)
    q_r = rope((cq @ mxq(f64(w_qr), 0, "e4m3")).reshape(B, S, N_H, D_HR), cos, sin).transpose(0, 2, 1, 3)
    return np.concatenate([q_c, q_r], axis=-1)


def e4m3fn_bytes(y):
    return np.clip(np.asarray(y, np.float64), -448.0, 448.0).astype(np.float32).astype(ml_dtypes.float8_e4m3fn).view(np.uint8)


def e4m3fn_values(b):
    return np.asarray(b, np.uint8).view(ml_dtypes.float8_e4m3fn).astype(np.float64)


def setup_inputs():
    d = draw0()
    x0 = np.asarray(d['h']).astype(np.float64)
    s = (np.max(np.abs(x0), axis=(0, 1), keepdims=True) / 448.0).astype(np.float32)
    out = {}
    for k, v in d.items():
        if k == 'h':
            out['h_bytes'] = e4m3fn_bytes(x0 / s.astype(np.float64))
            out['h_scale'] = s
        else:
            out[k] = v
    return out


def reference(h_bytes, h_scale, w_cq, w_q, w_qr):
    return core(e4m3fn_values(h_bytes) * h_scale.astype(np.float64), w_cq, w_q, w_qr)

@@ -1,0 +1,342 @@
+from contextlib import ExitStack
+import math
+
+import concourse.mybir as mybir
+from concourse.masks import make_identity
+
+F32 = mybir.dt.float32
+BF16 = mybir.dt.bfloat16
+U32 = mybir.dt.uint32
+I32 = mybir.dt.int32
+U8 = mybir.dt.uint8
+E4M3 = mybir.dt.float8_e4m3fn
+FP8X4 = mybir.dt.float8_e4m3fn_x4
+ALU = mybir.AluOpType
+ACT = mybir.ActivationFunctionType
+
+B, S, D, H, DH, CQ = 4, 1024, 1024, 4, 128, 512
+P = 128
+NT = B * S // P
+NC = NT // 4
+
+
+def WT(s):
+    return s + 3
+
+
+FLOPS = 2 * B * S * (D * CQ + 2 * CQ * H * DH) + 3 * B * S * H * DH
+
+
+def tile_mla_pa_t_kernel(tc, h_bytes, h_scale, w_cq, w_q, w_qr, out):
+    nc = tc.nc
+    V = nc.vector.tensor_copy
+    A = nc.scalar.copy
+    with ExitStack() as ctx:
+        keep = ctx.enter_context(tc.tile_pool(name="keep", bufs=1))
+        work = ctx.enter_context(tc.tile_pool(name="work", bufs=3))
+        psum = ctx.enter_context(tc.psum_pool(name="psum", bufs=2))
+        ctx.enter_context(tc.manual_schedule())
+
+        hb = [keep.tile([P, 4, D], U8, name=f"hb{c}", align_bytes=64) for c in range(NC)]
+
+        def load_h(c, j0, j1):
+            b, half = c // 2, c % 2
+            nc.sync.dma_start(
+                out=hb[c][:, j0:j1, :],
+                in_=h_bytes[b, half * 512 : (half + 1) * 512, :].rearrange("(p j) k -> p j k", j=4)[:, j0:j1, :])
+
+        sv = keep.tile([P, 8], F32, name="sv")
+        nc.sync.dma_start(out=sv[:], in_=h_scale.rearrange("a b (p c) -> p (a b c)", c=8))
+        wcq_raw = [keep.tile([P, 4, CQ], BF16, name=f"wcq_raw{g}", align_bytes=64) for g in range(2)]
+        wq_raw = keep.tile([P, 4, H * DH], BF16, name="wq_raw", align_bytes=64)
+        wqr_raw = keep.tile([P, 4, H * DH], BF16, name="wqr_raw", align_bytes=64)
+
+        def load_wcq(g):
+            nc.sync.dma_start(out=wcq_raw[g][:],
+                              in_=w_cq[g * 512 : (g + 1) * 512, :].rearrange("(p j) c -> p j c", j=4))
+
+        load_h(0, 0, 2)
+        load_wcq(0)
+        load_wcq(1)
+        load_h(0, 2, 4)
+        nc.sync.dma_start(out=wqr_raw[:], in_=w_qr.rearrange("(p j) c -> p j c", j=4))
+        nc.sync.dma_start(out=wq_raw[:], in_=w_q.rearrange("(p j) c -> p j c", j=4))
+        for c in range(1, NC):
+            load_h(c, 0, 4)
+
+        ident = keep.tile([P, P], F32, name="ident", align_bytes=64)
+        make_identity(nc, ident[:])
+        warm = keep.tile([P, 1], F32, name="warm")
+        nc.gpsimd.memset(warm[:], 0.0)
+        warm2 = keep.tile([P, 1], F32, name="warm2")
+        nc.scalar.activation(out=warm2[:], in_=warm[:], func=ACT.Sin)
+        s_row = keep.tile([P, S], F32, name="s_row", align_bytes=64)
+        nc.gpsimd.iota(s_row[:].rearrange("p (c j q) -> p c j q", c=2, j=4), pattern=[[512, 2], [1, 4], [4, 128]],
+                       base=0, channel_multiplier=0, allow_small_or_imprecise_dtypes=True)
+        th = keep.tile([P, 64], F32, name="th")
+        nc.vector.memset(th[:, 0:1], 1.0)
+        w = 1
+        while w < 64:
+            nc.vector.tensor_scalar(out=th[:, w : 2 * w], in0=th[:, 0:w], scalar1=10000.0 ** (-w / 64.0),
+                                    scalar2=None, op0=ALU.mult)
+            w *= 2
+        th2 = keep.tile([P, P], F32, name="th2", align_bytes=64)
+        for e in range(2):
+            nc.vector.tensor_scalar(out=th2[:].rearrange("p (i two) -> p two i", two=2)[:, e, :], in0=th[:],
+                                    scalar1=(1.0 - 2.0 * e) / (2.0 * math.pi), scalar2=None, op0=ALU.mult)
+        hpi = keep.tile([P, 1], F32, name="hpi")
+        nc.gpsimd.memset(hpi[:], 1.0)
+        hpi2 = keep.tile([P, 1], F32, name="hpi2")
+        nc.gpsimd.tensor_scalar(out=hpi2[:], in0=hpi[:], scalar1=math.pi / 2, scalar2=None, op0=ALU.mult)
+        perm = keep.tile([P, P], F32, name="perm", align_bytes=64)
+        for e in range(2):
+            nc.gpsimd.tensor_copy(out=perm[:].rearrange("p (i two) -> p two i", two=2)[:, e, :],
+                                  in_=ident[:].rearrange("p (i two) -> p two i", two=2)[:, 1 - e, :])
+        th_ps = psum.tile([P, P], F32, name="th_ps", tag="ra")
+        nc.tensor.transpose(th_ps[:], th2[:], ident[:])
+
+        scale = keep.tile([P, D], F32, name="scale", align_bytes=64)
+        sc_ps = [psum.tile([P, 4, P], F32, name=f"sc_ps{k}", tag="ht") for k in range(2)]
+        for k in range(8):
+            nc.tensor.transpose(sc_ps[k // 4][:, k % 4, :], sv[:, k : k + 1].to_broadcast([P, P]), ident[:])
+        scv = scale[:].rearrange("p (q k c) -> p k q c", k=2, c=4)
+        nc.scalar.copy(out=scv[:, 1], in_=sc_ps[1][:].rearrange("p c q -> p q c"))
+        thc = keep.tile([P, 1], F32, name="thc")
+        nc.vector.tensor_copy(out=thc[:], in_=th_ps[:, 0:1])
+        turns = keep.tile([P, S], F32, name="turns", align_bytes=64)
+        whole = keep.tile([P, S], I32, name="whole", align_bytes=64)
+        frac = keep.tile([P, S], F32, name="frac", align_bytes=64)
+        fabs = keep.tile([P, S], F32, name="fabs", align_bytes=64)
+        tab = keep.tile([P, 2, 2, 512], F32, name="tab", align_bytes=64)
+
+        def turns_v(h):
+            cols = slice(512 * h, 512 * (h + 1))
+            nc.vector.tensor_scalar(out=turns[:, cols], in0=s_row[:, cols], scalar1=thc[:, 0:1], scalar2=None,
+                                    op0=ALU.mult)
+        def whole_v(h):
+            cols = slice(512 * h, 512 * (h + 1))
+            nc.vector.tensor_copy(out=whole[:, cols], in_=turns[:, cols])
+
+        def frac_v(h):
+            cols = slice(512 * h, 512 * (h + 1))
+            nc.vector.tensor_tensor(out=frac[:, cols], in0=turns[:, cols], in1=whole[:, cols], op=ALU.subtract)
+
+        def tables_s(h):
+            cols = slice(512 * h, 512 * (h + 1))
+            nc.scalar.activation(out=tab[:, h, 1, :], in_=frac[:, cols], func=ACT.Sin, scale=2.0 * math.pi)
+            nc.scalar.activation(out=fabs[:, cols], in_=frac[:, cols], func=ACT.Abs)
+            nc.scalar.activation(out=tab[:, h, 0, :], in_=fabs[:, cols], func=ACT.Sin, scale=-2.0 * math.pi,
+                                 bias=hpi2[:, 0:1])
+        turns_v(0)
+        turns_v(1)
+        nc.vector.tensor_copy(out=scv[:, 0], in_=sc_ps[0][:].rearrange("p c q -> p q c"))
+
+
+        wcq_codes = keep.tile([P, 2, CQ], U32, name="wcq_codes", align_bytes=64)
+        wcq_sc = keep.tile([P, 2, CQ], U8, name="wcq_sc", align_bytes=64)
+        wq_codes = keep.tile([P, 512], U32, name="wq_codes", align_bytes=64)
+        wq_sc = keep.tile([P, 512], U8, name="wq_sc", align_bytes=64)
+        wqr_codes = keep.tile([P, 512], U32, name="wqr_codes", align_bytes=64)
+        wqr_sc = keep.tile([P, 512], U8, name="wqr_sc", align_bytes=64)
+        wcq_g = [keep.tile([P, 4 * CQ], BF16, name=f"wcq_g{g}", align_bytes=64) for g in range(2)]
+        wq_g = keep.tile([P, 2048], BF16, name="wq_g", align_bytes=64)
+        wqr_g = keep.tile([P, 2048], BF16, name="wqr_g", align_bytes=64)
+
+        def wcq_copy(copy, g):
+            copy(out=wcq_g[g][:].rearrange("p (t m j) -> p t m j", t=4, j=4),
+                 in_=wcq_raw[g][:].rearrange("p j (m t) -> p t m j", t=4))
+
+        def wcq_quant(g):
+            nc.vector.quantize_mx(out=wcq_codes[:, g, :].bitcast(FP8X4), scales=wcq_sc[:, g, :], in_=wcq_g[g][:])
+
+        def w_copy(copy, grouped, raw):
+            copy(out=grouped[:].rearrange("p (n j) -> p n j", j=4), in_=raw[:].rearrange("p j n -> p n j"))
+
+        xb, hps, grp, hq, cps, cgs, cq, ups, ts, rps, aps, osb, u3s = ({} for k in range(13))
+
+        def widen_to(n):
+            while len(xb) < min(n, NT):
+                i = len(xb)
+                x = work.tile([P, D], BF16, name=f"x{i}", tag="x", bufs=8, align_bytes=64)
+                nc.vector.tensor_tensor(out=x[:], in0=hb[i // 4][:, i % 4, :].bitcast(E4M3), in1=scale[:], op=ALU.mult)
+                xb[i] = x
+
+        def h_transpose(i):
+            ht = psum.tile([P, 2, 2, P], F32, name=f"ht{i}", tag="ht")
+            words = xb[i][:].bitcast(F32)
+            for g in range(2):
+                for u in range(2):
+                    nc.tensor.transpose(ht[:, g, u, :], words[:, 256 * g + u : 256 * (g + 1) : 2], ident[:])
+            hps[i] = ht
+
+        def h_copy(i):
+            gt = work.tile([P, D], BF16, name=f"g{i}", tag="g", align_bytes=64)
+            nc.scalar.copy(out=gt[:].bitcast(F32).rearrange("p (g n u) -> p g n u", g=2, u=2),
+                           in_=hps[i][:].rearrange("p g u n -> p g n u"))
+            grp[i] = gt
+
+        def h_quant(i):
+            codes = work.tile([P, 256], U32, name=f"hc{i}", tag="hc", align_bytes=64)
+            sc = work.tile([P, 256], U8, name=f"hs{i}", tag="hs", align_bytes=64)
+            nc.vector.quantize_mx(out=codes[:].bitcast(FP8X4), scales=sc[:], in_=grp[i][:])
+            hq[i] = (codes, sc)
+
+        def mm1(i):
+            codes, sc = hq[i]
+            cp = psum.tile([P, 4, P], F32, name=f"cp{i}", tag="cp")
+            for t in range(4):
+                for g in range(2):
+                    cols = slice(g * P, (g + 1) * P)
+                    nc.tensor.matmul_mx(
+                        out=cp[:, t, :],
+                        lhsT=wcq_codes[:, g, t * P : (t + 1) * P].bitcast(FP8X4),
+                        lhsT_scale=wcq_sc[:, g, t * P : (t + 1) * P],
+                        rhs=codes[:, cols].bitcast(FP8X4), rhs_scale=sc[:, cols],
+                        start=(g == 0), stop=(g == 1))
+            cps[i] = cp
+
+        def c_copy(i):
+            cg = work.tile([P, 512], BF16, name=f"cg{i}", tag="cg", align_bytes=64)
+            nc.scalar.copy(out=cg[:].rearrange("p (n t) -> p n t", t=4), in_=cps[i][:].rearrange("p t n -> p n t"))
+            cgs[i] = cg
+
+        def c_quant(i):
+            codes = work.tile([P, P], U32, name=f"cc{i}", tag="cc", align_bytes=64)
+            sc = work.tile([P, P], U8, name=f"cs{i}", tag="cs", align_bytes=64)
+            nc.vector.quantize_mx(out=codes[:].bitcast(FP8X4), scales=sc[:], in_=cgs[i][:])
+            cq[i] = (codes, sc)
+
+        def mm2u(i):
+            codes, sc = cq[i]
+            up = psum.tile([P, H, P], F32, name=f"up{i}", tag="up")
+            for n in range(H):
+                nc.tensor.matmul_mx(out=up[:, n, :], lhsT=wqr_codes[:, n * P : (n + 1) * P].bitcast(FP8X4),
+                                    lhsT_scale=wqr_sc[:, n * P : (n + 1) * P],
+                                    rhs=codes[:].bitcast(FP8X4), rhs_scale=sc[:], start=True, stop=True)
+            ups[i] = up
+
+        def mm2a(i):
+            codes, sc = cq[i]
+            ap_ = psum.tile([P, 512], F32, name=f"ap{i}", tag="ra")
+            nc.tensor.matmul_mx(out=ap_[:], lhsT=codes[:].bitcast(FP8X4), lhsT_scale=sc[:],
+                                rhs=wq_codes[:].bitcast(FP8X4), rhs_scale=wq_sc[:], start=True, stop=True)
+            aps[i] = ap_
+
+        def a_copy(i):
+            if i % 2 == 0:
+                o = work.tile([P, H, 2, 2 * DH], F32, name=f"o{i}", tag="o", bufs=4, align_bytes=64)
+                osb[i // 2] = o
+            nc.scalar.copy(out=osb[i // 2][:, :, i % 2, 0:DH], in_=aps[i][:].rearrange("p (n d) -> p n d", n=H))
+
+        def rope_mul(i):
+            t = work.tile([P, 2, H, P], F32, name=f"t{i}", tag="t", align_bytes=64)
+            k = i % 8
+            cs = tab[:, k // 4, :, P * (k % 4) : P * (k % 4 + 1)]
+            G = H - 1
+            nc.vector.tensor_tensor(out=t[:, :, 0:G, :], in0=ups[i][:, 0:G, :].unsqueeze(1).to_broadcast([P, 2, G, P]),
+                                    in1=cs.unsqueeze(2).to_broadcast([P, 2, G, P]), op=ALU.mult)
+            nc.gpsimd.tensor_tensor(out=t[:, :, G, :], in0=u3s[i][:].unsqueeze(1).to_broadcast([P, 2, P]), in1=cs,
+                                    op=ALU.mult)
+            ts[i] = t
+
+        def tick(i):
+            word = work.tile([P, 1], U32, name=f"tick{i}", tag="tick")
+            nc.gpsimd.tensor_copy(out=word[:], in_=cq[i][0][:, 0:1])
+
+        def u3_copy(i):
+            u3 = work.tile([P, P], F32, name=f"u3_{i}", tag="u3", align_bytes=64)
+            nc.scalar.copy(out=u3[:], in_=ups[i][:, H - 1, :])
+            u3s[i] = u3
+
+        def r_transpose(i):
+            rp = psum.tile([P, H, P], F32, name=f"rp{i}", tag="ra")
+            for n in range(H):
+                nc.tensor.matmul(rp[:, n, :], lhsT=ts[i][:, 0, n, :], rhs=ident[:], is_transpose=True,
+                                 start=True, stop=False)
+                nc.tensor.matmul(rp[:, n, :], lhsT=ts[i][:, 1, n, :], rhs=perm[:], is_transpose=True,
+                                 start=False, stop=True)
+            rps[i] = rp
+
+        def r_copy(i):
+            nc.scalar.copy(out=osb[i // 2][:, :, i % 2, DH : 2 * DH], in_=rps[i][:])
+
+        def store(i):
+            c = i // 4
+            b, half = c // 2, c % 2
+            if i < NT - 4:
+                if i % 2 == 0:
+                    return
+                j0, j1, k0, k1 = i % 4 - 1, i % 4 + 1, 0, 2
+            else:
+                j0, j1, k0, k1 = i % 4, i % 4 + 1, i % 2, i % 2 + 1
+            for n in range(H):
+                nc.sync.dma_start(
+                    out=out[b, n, half * 512 : (half + 1) * 512, :].rearrange("(p j) d -> p j d", j=4)[:, j0:j1, :],
+                    in_=osb[i // 2][:, n, k0:k1, :])
+
+        def ok(i):
+            return 0 <= i < NT
+
+        def step(s):
+            if ok(s - 1):
+                h_quant(s - 1)
+            if ok(s - 2):
+                c_quant(s - 2)
+                tick(s - 2)
+            widen_to(WT(s))
+            if ok(s):
+                h_transpose(s)
+                h_copy(s)
+            if ok(s - 4):
+                r_transpose(s - 4)
+                r_copy(s - 4)
+                store(s - 4)
+            if ok(s - 3):
+                rope_mul(s - 3)
+            if ok(s - 1):
+                mm1(s - 1)
+                c_copy(s - 1)
+
+            if ok(s - 2):
+                mm2u(s - 2)
+                mm2a(s - 2)
+                u3_copy(s - 2)
+                a_copy(s - 2)
+
+        whole_v(0)
+        widen_to(1)
+        frac_v(0)
+        wcq_copy(A, 0)
+        tables_s(0)
+        widen_to(2)
+        h_transpose(0)
+        h_copy(0)
+        h_transpose(1)
+        h_copy(1)
+        wcq_copy(V, 1)
+        wcq_quant(0)
+        wcq_quant(1)
+        h_quant(0)
+        w_copy(A, wqr_g, wqr_raw)
+        mm1(0)
+        widen_to(3)
+        h_quant(1)
+        c_copy(0)
+        nc.vector.quantize_mx(out=wqr_codes[:].bitcast(FP8X4), scales=wqr_sc[:], in_=wqr_g[:])
+        w_copy(A, wq_g, wq_raw)
+        c_quant(0)
+        whole_v(1)
+        h_transpose(2)
+        h_copy(2)
+        mm1(1)
+        c_copy(1)
+        widen_to(4)
+        frac_v(1)
+        nc.vector.quantize_mx(out=wq_codes[:].bitcast(FP8X4), scales=wq_sc[:], in_=wq_g[:])
+        mm2u(0)
+        mm2a(0)
+        u3_copy(0)
+        a_copy(0)
+        tables_s(1)
+        for s in range(3, NT + 4):
+            step(s)

@@ -18,19 +18,19 @@ B, S, D, H, DH, CQ = 4, 1024, 1024, 4, 128, 512
 P = 128
 NT = B * S // P
 NC = NT // 4
-
-
-def WT(s):
-    return s + 3
-
+NP = DH // 2
+LEAD = 5
+V_ADDS = 3
+SINGLE = 6
+HALVES = 2
+SPLIT = NT - 2 * (LEAD - 1) - 1
+KINDS = 8
 
 FLOPS = 2 * B * S * (D * CQ + 2 * CQ * H * DH) + 3 * B * S * H * DH
 
 
 def tile_mla_pa_t_kernel(tc, h_bytes, h_scale, w_cq, w_q, w_qr, out):
     nc = tc.nc
-    V = nc.vector.tensor_copy
-    A = nc.scalar.copy
     with ExitStack() as ctx:
         keep = ctx.enter_context(tc.tile_pool(name="keep", bufs=1))
         work = ctx.enter_context(tc.tile_pool(name="work", bufs=3))
@@ -45,8 +45,7 @@ def tile_mla_pa_t_kernel(tc, h_bytes, h_scale, w_cq, w_q, w_qr, out):
                 out=hb[c][:, j0:j1, :],
                 in_=h_bytes[b, half * 512 : (half + 1) * 512, :].rearrange("(p j) k -> p j k", j=4)[:, j0:j1, :])
 
-        sv = keep.tile([P, 8], F32, name="sv")
-        nc.sync.dma_start(out=sv[:], in_=h_scale.rearrange("a b (p c) -> p (a b c)", c=8))
+        scale = keep.tile([P, 2, 4], F32, name="scale")
         wcq_raw = [keep.tile([P, 4, CQ], BF16, name=f"wcq_raw{g}", align_bytes=64) for g in range(2)]
         wq_raw = keep.tile([P, 4, H * DH], BF16, name="wq_raw", align_bytes=64)
         wqr_raw = keep.tile([P, 4, H * DH], BF16, name="wqr_raw", align_bytes=64)
@@ -55,135 +54,137 @@ def tile_mla_pa_t_kernel(tc, h_bytes, h_scale, w_cq, w_q, w_qr, out):
             nc.sync.dma_start(out=wcq_raw[g][:],
                               in_=w_cq[g * 512 : (g + 1) * 512, :].rearrange("(p j) c -> p j c", j=4))
 
-        load_h(0, 0, 2)
+        load_h(0, 0, 1)
         load_wcq(0)
+        load_h(0, 1, 2)
+        nc.sync.dma_start(out=scale[:], in_=h_scale.rearrange("a b (g p t) -> p (a b g) t", g=2, t=4))
         load_wcq(1)
         load_h(0, 2, 4)
         nc.sync.dma_start(out=wqr_raw[:], in_=w_qr.rearrange("(p j) c -> p j c", j=4))
+        load_h(1, 0, 4)
         nc.sync.dma_start(out=wq_raw[:], in_=w_q.rearrange("(p j) c -> p j c", j=4))
-        for c in range(1, NC):
+        for c in range(2, NC):
             load_h(c, 0, 4)
 
+        pos = keep.tile([P, KINDS], F32, name="pos")
+        nc.gpsimd.iota(pos[:].rearrange("p (c j) -> p c j", c=2), pattern=[[512, 2], [1, 4]],
+                       base=0, channel_multiplier=4, allow_small_or_imprecise_dtypes=True)
         ident = keep.tile([P, P], F32, name="ident", align_bytes=64)
         make_identity(nc, ident[:])
-        warm = keep.tile([P, 1], F32, name="warm")
-        nc.gpsimd.memset(warm[:], 0.0)
-        warm2 = keep.tile([P, 1], F32, name="warm2")
-        nc.scalar.activation(out=warm2[:], in_=warm[:], func=ACT.Sin)
-        s_row = keep.tile([P, S], F32, name="s_row", align_bytes=64)
-        nc.gpsimd.iota(s_row[:].rearrange("p (c j q) -> p c j q", c=2, j=4), pattern=[[512, 2], [1, 4], [4, 128]],
-                       base=0, channel_multiplier=0, allow_small_or_imprecise_dtypes=True)
-        th = keep.tile([P, 64], F32, name="th")
-        nc.vector.memset(th[:, 0:1], 1.0)
-        w = 1
-        while w < 64:
-            nc.vector.tensor_scalar(out=th[:, w : 2 * w], in0=th[:, 0:w], scalar1=10000.0 ** (-w / 64.0),
+        one = keep.tile([P, 1], F32, name="one")
+        nc.vector.memset(one[:], 1.0)
+        th = keep.tile([P, NP], F32, name="th")
+        for a in range(4):
+            nc.vector.tensor_scalar(out=th[:, a : a + 1], in0=one[:], scalar1=10000.0 ** (-a / NP) / (2.0 * math.pi),
                                     scalar2=None, op0=ALU.mult)
-            w *= 2
-        th2 = keep.tile([P, P], F32, name="th2", align_bytes=64)
-        for e in range(2):
-            nc.vector.tensor_scalar(out=th2[:].rearrange("p (i two) -> p two i", two=2)[:, e, :], in0=th[:],
-                                    scalar1=(1.0 - 2.0 * e) / (2.0 * math.pi), scalar2=None, op0=ALU.mult)
         hpi = keep.tile([P, 1], F32, name="hpi")
-        nc.gpsimd.memset(hpi[:], 1.0)
-        hpi2 = keep.tile([P, 1], F32, name="hpi2")
-        nc.gpsimd.tensor_scalar(out=hpi2[:], in0=hpi[:], scalar1=math.pi / 2, scalar2=None, op0=ALU.mult)
-        perm = keep.tile([P, P], F32, name="perm", align_bytes=64)
-        for e in range(2):
-            nc.gpsimd.tensor_copy(out=perm[:].rearrange("p (i two) -> p two i", two=2)[:, e, :],
-                                  in_=ident[:].rearrange("p (i two) -> p two i", two=2)[:, 1 - e, :])
-        th_ps = psum.tile([P, P], F32, name="th_ps", tag="ra")
-        nc.tensor.transpose(th_ps[:], th2[:], ident[:])
+        nc.vector.tensor_scalar(out=hpi[:], in0=one[:], scalar1=math.pi / 2, scalar2=None, op0=ALU.mult)
+        for w in (4, 16):
+            for a in range(1, 4):
+                nc.vector.tensor_scalar(out=th[:, a * w : (a + 1) * w], in0=th[:, 0:w],
+                                        scalar1=10000.0 ** (-a * w / NP), scalar2=None, op0=ALU.mult)
+        M = KINDS * NP
+        turns = keep.tile([P, M], F32, name="turns", align_bytes=64)
+        whole = keep.tile([P, M], I32, name="whole", align_bytes=64)
+        frac = keep.tile([P, M], F32, name="frac", align_bytes=64)
+        fabs = keep.tile([P, M], F32, name="fabs", align_bytes=64)
+        sines = keep.tile([P, 2, M], F32, name="sines", tag="late", align_bytes=64)
+        cos = keep.tile([P, M], F32, name="cos", align_bytes=64)
+        mix = keep.tile([P, M, 2], F32, name="mix", align_bytes=64)
 
-        scale = keep.tile([P, D], F32, name="scale", align_bytes=64)
-        sc_ps = [psum.tile([P, 4, P], F32, name=f"sc_ps{k}", tag="ht") for k in range(2)]
-        for k in range(8):
-            nc.tensor.transpose(sc_ps[k // 4][:, k % 4, :], sv[:, k : k + 1].to_broadcast([P, P]), ident[:])
-        scv = scale[:].rearrange("p (q k c) -> p k q c", k=2, c=4)
-        nc.scalar.copy(out=scv[:, 1], in_=sc_ps[1][:].rearrange("p c q -> p q c"))
-        thc = keep.tile([P, 1], F32, name="thc")
-        nc.vector.tensor_copy(out=thc[:], in_=th_ps[:, 0:1])
-        turns = keep.tile([P, S], F32, name="turns", align_bytes=64)
-        whole = keep.tile([P, S], I32, name="whole", align_bytes=64)
-        frac = keep.tile([P, S], F32, name="frac", align_bytes=64)
-        fabs = keep.tile([P, S], F32, name="fabs", align_bytes=64)
-        tab = keep.tile([P, 2, 2, 512], F32, name="tab", align_bytes=64)
+        def half_cols(f):
+            return slice(f * M // 2, (f + 1) * M // 2)
 
-        def turns_v(h):
-            cols = slice(512 * h, 512 * (h + 1))
-            nc.vector.tensor_scalar(out=turns[:, cols], in0=s_row[:, cols], scalar1=thc[:, 0:1], scalar2=None,
-                                    op0=ALU.mult)
-        def whole_v(h):
-            cols = slice(512 * h, 512 * (h + 1))
-            nc.vector.tensor_copy(out=whole[:, cols], in_=turns[:, cols])
+        def tables_turns(f):
+            nc.vector.tensor_tensor(out=turns[:, half_cols(f)].rearrange("p (k i) -> p k i", k=4),
+                                    in0=pos[:, 4 * f : 4 * f + 4].unsqueeze(2).to_broadcast([P, 4, NP]),
+                                    in1=th[:].unsqueeze(1).to_broadcast([P, 4, NP]), op=ALU.mult)
 
-        def frac_v(h):
-            cols = slice(512 * h, 512 * (h + 1))
+        def tables_whole(f):
+            nc.vector.tensor_copy(out=whole[:, half_cols(f)], in_=turns[:, half_cols(f)])
+
+        def tables_frac(f):
+            cols = half_cols(f)
             nc.vector.tensor_tensor(out=frac[:, cols], in0=turns[:, cols], in1=whole[:, cols], op=ALU.subtract)
 
-        def tables_s(h):
-            cols = slice(512 * h, 512 * (h + 1))
-            nc.scalar.activation(out=tab[:, h, 1, :], in_=frac[:, cols], func=ACT.Sin, scale=2.0 * math.pi)
-            nc.scalar.activation(out=fabs[:, cols], in_=frac[:, cols], func=ACT.Abs)
-            nc.scalar.activation(out=tab[:, h, 0, :], in_=fabs[:, cols], func=ACT.Sin, scale=-2.0 * math.pi,
-                                 bias=hpi2[:, 0:1])
-        turns_v(0)
-        turns_v(1)
-        nc.vector.tensor_copy(out=scv[:, 0], in_=sc_ps[0][:].rearrange("p c q -> p q c"))
+        def tables_sin(f, e):
+            nc.scalar.activation(out=sines[:, e, half_cols(f)], in_=frac[:, half_cols(f)], func=ACT.Sin,
+                                 scale=(2.0 * e - 1.0) * 2.0 * math.pi)
 
+        def tables_cos():
+            nc.scalar.activation(out=fabs[:], in_=frac[:], func=ACT.Abs)
+            nc.scalar.activation(out=cos[:], in_=fabs[:], func=ACT.Sin, scale=-2.0 * math.pi, bias=hpi[:, 0:1])
+
+        def tables_mix():
+            nc.vector.tensor_tensor(out=mix[:], in0=sines[:].rearrange("p e m -> p m e"),
+                                    in1=cos[:].unsqueeze(2).to_broadcast([P, M, 2]), op=ALU.subtract)
 
         wcq_codes = keep.tile([P, 2, CQ], U32, name="wcq_codes", align_bytes=64)
         wcq_sc = keep.tile([P, 2, CQ], U8, name="wcq_sc", align_bytes=64)
-        wq_codes = keep.tile([P, 512], U32, name="wq_codes", align_bytes=64)
-        wq_sc = keep.tile([P, 512], U8, name="wq_sc", align_bytes=64)
-        wqr_codes = keep.tile([P, 512], U32, name="wqr_codes", align_bytes=64)
-        wqr_sc = keep.tile([P, 512], U8, name="wqr_sc", align_bytes=64)
-        wcq_g = [keep.tile([P, 4 * CQ], BF16, name=f"wcq_g{g}", align_bytes=64) for g in range(2)]
-        wq_g = keep.tile([P, 2048], BF16, name="wq_g", align_bytes=64)
-        wqr_g = keep.tile([P, 2048], BF16, name="wqr_g", align_bytes=64)
+        w2_codes = keep.tile([P, 1024], U32, name="w2_codes", align_bytes=64)
+        w2_sc = keep.tile([P, 1024], U8, name="w2_sc", align_bytes=64)
+        wcq_g = keep.tile([P, 2, 4 * CQ], BF16, name="wcq_g", align_bytes=64)
+        early_g = keep.tile([P, 2, 1024], BF16, name="early_g", align_bytes=64)
+
+        def pool_copy(out, in_):
+            nc.gpsimd.tensor_scalar(out=out, in0=in_, scalar1=1.0, scalar2=0.0, op0=ALU.mult, op1=ALU.add)
 
         def wcq_copy(copy, g):
-            copy(out=wcq_g[g][:].rearrange("p (t m j) -> p t m j", t=4, j=4),
+            copy(out=wcq_g[:, g, :].rearrange("p (t m j) -> p t m j", t=4, j=4),
                  in_=wcq_raw[g][:].rearrange("p j (m t) -> p t m j", t=4))
 
-        def wcq_quant(g):
-            nc.vector.quantize_mx(out=wcq_codes[:, g, :].bitcast(FP8X4), scales=wcq_sc[:, g, :], in_=wcq_g[g][:])
+        def wqr_copy(copy, dst, f):
+            copy(out=dst.rearrange("p (m j) -> p m j", j=4),
+                 in_=wqr_raw[:].rearrange("p j (m e) -> p e m j", e=2)[:, 1 - f])
 
-        def w_copy(copy, grouped, raw):
-            copy(out=grouped[:].rearrange("p (n j) -> p n j", j=4), in_=raw[:].rearrange("p j n -> p n j"))
+        def wq_copy(copy, dst, f):
+            copy(out=dst.rearrange("p (n j) -> p n j", j=4),
+                 in_=wq_raw[:, :, 256 * f : 256 * (f + 1)].rearrange("p j n -> p n j"))
 
-        xb, hps, grp, hq, cps, cgs, cq, ups, ts, rps, aps, osb, u3s = ({} for k in range(13))
+        def quant(codes, sc, grouped):
+            nc.vector.quantize_mx(out=codes.bitcast(FP8X4), scales=sc, in_=grouped)
 
-        def widen_to(n):
-            while len(xb) < min(n, NT):
-                i = len(xb)
-                x = work.tile([P, D], BF16, name=f"x{i}", tag="x", bufs=8, align_bytes=64)
-                nc.vector.tensor_tensor(out=x[:], in0=hb[i // 4][:, i % 4, :].bitcast(E4M3), in1=scale[:], op=ALU.mult)
-                xb[i] = x
+        xb, hps, grp, cq, cps, ups, aps, sps, k1s, k23s, osb = ({} for k in range(11))
+
+        def cast(i, copy):
+            x = work.tile([P, D], BF16, name=f"x{i}", tag="x", align_bytes=64)
+            copy(out=x[:], in_=hb[i // 4][:, i % 4, :].bitcast(E4M3))
+            xb[i] = x
 
         def h_transpose(i):
             ht = psum.tile([P, 2, 2, P], F32, name=f"ht{i}", tag="ht")
             words = xb[i][:].bitcast(F32)
             for g in range(2):
                 for u in range(2):
-                    nc.tensor.transpose(ht[:, g, u, :], words[:, 256 * g + u : 256 * (g + 1) : 2], ident[:])
+                    nc.tensor.transpose(ht[:, u, g, :], words[:, 256 * g + u : 256 * (g + 1) : 2], ident[:])
             hps[i] = ht
 
-        def h_copy(i):
-            gt = work.tile([P, D], BF16, name=f"g{i}", tag="g", align_bytes=64)
-            nc.scalar.copy(out=gt[:].bitcast(F32).rearrange("p (g n u) -> p g n u", g=2, u=2),
-                           in_=hps[i][:].rearrange("p g u n -> p g n u"))
-            grp[i] = gt
+        def group(i):
+            if i not in grp:
+                grp[i] = work.tile([P, D + CQ], BF16, name=f"g{i}", tag="g", bufs=LEAD + 3, align_bytes=64)
+            return grp[i]
 
-        def h_quant(i):
-            codes = work.tile([P, 256], U32, name=f"hc{i}", tag="hc", align_bytes=64)
-            sc = work.tile([P, 256], U8, name=f"hs{i}", tag="hs", align_bytes=64)
-            nc.vector.quantize_mx(out=codes[:].bitcast(FP8X4), scales=sc[:], in_=grp[i][:])
-            hq[i] = (codes, sc)
+        def h_scale_mul(i, g0=0, g1=2):
+            halves = hps[i][:].rearrange("p u g n -> p (u g n)").bitcast(BF16)
+            nc.vector.tensor_tensor(
+                out=group(i)[:, 0:D].rearrange("p (g n u e) -> p g n u e", g=2, u=2, e=2)[:, g0:g1],
+                in0=halves.rearrange("p (u g n e) -> p g n u e", u=2, g=2, e=2)[:, g0:g1],
+                in1=scale[:, g0:g1, :].rearrange("p g (u e) -> p g u e", u=2).unsqueeze(2).to_broadcast(
+                    [P, g1 - g0, P, 2, 2]),
+                op=ALU.mult)
+
+        def quant_step(s):
+            codes = work.tile([P, 384], U32, name=f"q{s}", tag="q", align_bytes=64)
+            sc = work.tile([P, 384], U8, name=f"qs{s}", tag="qs", align_bytes=64)
+            lo = 0 if s < NT else 256
+            hi = 384 if s >= 2 else 256
+            quant(codes[:, lo:hi], sc[:, lo:hi], group(s)[:, 4 * lo : 4 * hi])
+            cq[s] = (codes, sc)
 
         def mm1(i):
-            codes, sc = hq[i]
-            cp = psum.tile([P, 4, P], F32, name=f"cp{i}", tag="cp")
+            codes, sc = cq[i]
+            tag, bufs = ("m2", 5) if i == 0 else ("cp", 1)
+            cp = psum.tile([P, 4, P], F32, name=f"cp{i}", tag=tag, bufs=bufs)
             for t in range(4):
                 for g in range(2):
                     cols = slice(g * P, (g + 1) * P)
@@ -196,147 +197,161 @@ def tile_mla_pa_t_kernel(tc, h_bytes, h_scale, w_cq, w_q, w_qr, out):
             cps[i] = cp
 
         def c_copy(i):
-            cg = work.tile([P, 512], BF16, name=f"cg{i}", tag="cg", align_bytes=64)
-            nc.scalar.copy(out=cg[:].rearrange("p (n t) -> p n t", t=4), in_=cps[i][:].rearrange("p t n -> p n t"))
-            cgs[i] = cg
+            nc.scalar.copy(out=group(i + 2)[:, D : D + CQ].rearrange("p (n t) -> p n t", t=4),
+                           in_=cps[i][:].rearrange("p t n -> p n t"))
 
-        def c_quant(i):
-            codes = work.tile([P, P], U32, name=f"cc{i}", tag="cc", align_bytes=64)
-            sc = work.tile([P, P], U8, name=f"cs{i}", tag="cs", align_bytes=64)
-            nc.vector.quantize_mx(out=codes[:].bitcast(FP8X4), scales=sc[:], in_=cgs[i][:])
-            cq[i] = (codes, sc)
+        def mm2(i):
+            codes, sc = cq[i + 2]
 
-        def mm2u(i):
-            codes, sc = cq[i]
-            up = psum.tile([P, H, P], F32, name=f"up{i}", tag="up")
-            for n in range(H):
-                nc.tensor.matmul_mx(out=up[:, n, :], lhsT=wqr_codes[:, n * P : (n + 1) * P].bitcast(FP8X4),
-                                    lhsT_scale=wqr_sc[:, n * P : (n + 1) * P],
-                                    rhs=codes[:].bitcast(FP8X4), rhs_scale=sc[:], start=True, stop=True)
-            ups[i] = up
+            def mm(dst, c0, c1, start, stop):
+                nc.tensor.matmul_mx(out=dst, lhsT=codes[:, 256:384].bitcast(FP8X4), lhsT_scale=sc[:, 256:384],
+                                    rhs=w2_codes[:, c0:c1].bitcast(FP8X4), rhs_scale=w2_sc[:, c0:c1],
+                                    start=start, stop=stop)
 
-        def mm2a(i):
-            codes, sc = cq[i]
-            ap_ = psum.tile([P, 512], F32, name=f"ap{i}", tag="ra")
-            nc.tensor.matmul_mx(out=ap_[:], lhsT=codes[:].bitcast(FP8X4), lhsT_scale=sc[:],
-                                rhs=wq_codes[:].bitcast(FP8X4), rhs_scale=wq_sc[:], start=True, stop=True)
-            aps[i] = ap_
+            aps[i] = psum.tile([P, 512], F32, name=f"ap{i}", tag="m2", bufs=5)
+            mm(aps[i][:], 512, 1024, True, True)
+            ups[i] = psum.tile([P, 512], F32, name=f"up{i}", tag="m2", bufs=5)
+            mm(ups[i][:], 0, 512, True, True)
+            sps[i] = psum.tile([P, 256], F32, name=f"sp{i}", tag="m2", bufs=5)
+            mm(sps[i][:], 0, 256, True, False)
+            mm(sps[i][:], 256, 512, False, True)
+
+        def result(i, part):
+            if i >= NT - HALVES:
+                if (i, part) not in osb:
+                    osb[i, part] = keep.tile([P, H, DH], F32, name=f"last{i}_{part}", align_bytes=64)
+                return osb[i, part][:]
+            if i >= NT - SINGLE:
+                if (i, 0) not in osb:
+                    osb[i, 0] = keep.tile([P, H, 2 * DH], F32, name=f"single{i}", align_bytes=64)
+                return osb[i, 0][:, :, part * DH : (part + 1) * DH]
+            if i // 2 not in osb:
+                osb[i // 2] = work.tile([P, H, 2, 2 * DH], F32, name=f"o{i}", tag="o", bufs=4, align_bytes=64)
+            return osb[i // 2][:, :, i % 2, part * DH : (part + 1) * DH]
 
         def a_copy(i):
-            if i % 2 == 0:
-                o = work.tile([P, H, 2, 2 * DH], F32, name=f"o{i}", tag="o", bufs=4, align_bytes=64)
-                osb[i // 2] = o
-            nc.scalar.copy(out=osb[i // 2][:, :, i % 2, 0:DH], in_=aps[i][:].rearrange("p (n d) -> p n d", n=H))
+            nc.scalar.copy(out=result(i, 0), in_=aps[i][:].rearrange("p (n d) -> p n d", n=H))
 
-        def rope_mul(i):
-            t = work.tile([P, 2, H, P], F32, name=f"t{i}", tag="t", align_bytes=64)
-            k = i % 8
-            cs = tab[:, k // 4, :, P * (k % 4) : P * (k % 4 + 1)]
-            G = H - 1
-            nc.vector.tensor_tensor(out=t[:, :, 0:G, :], in0=ups[i][:, 0:G, :].unsqueeze(1).to_broadcast([P, 2, G, P]),
-                                    in1=cs.unsqueeze(2).to_broadcast([P, 2, G, P]), op=ALU.mult)
-            nc.gpsimd.tensor_tensor(out=t[:, :, G, :], in0=u3s[i][:].unsqueeze(1).to_broadcast([P, 2, P]), in1=cs,
-                                    op=ALU.mult)
-            ts[i] = t
+        def rope_k23(i):
+            k23 = work.tile([P, H, NP, 2], F32, name=f"k23_{i}", tag="k23", align_bytes=64)
+            kind = i % KINDS
+            nc.vector.tensor_tensor(
+                out=k23[:], in0=ups[i][:].rearrange("p (f n i) -> p n i f", f=2, n=H),
+                in1=mix[:, NP * kind : NP * (kind + 1), :].unsqueeze(1).to_broadcast([P, H, NP, 2]), op=ALU.mult)
+            k23s[i] = k23
 
-        def tick(i):
-            word = work.tile([P, 1], U32, name=f"tick{i}", tag="tick")
-            nc.gpsimd.tensor_copy(out=word[:], in_=cq[i][0][:, 0:1])
+        def rope_k1(i):
+            k1 = work.tile([P, H, NP], F32, name=f"k1_{i}", tag="k1", align_bytes=64)
+            kind = i % KINDS
+            nc.vector.tensor_tensor(
+                out=k1[:], in0=sps[i][:].rearrange("p (n i) -> p n i", n=H),
+                in1=cos[:, NP * kind : NP * (kind + 1)].unsqueeze(1).to_broadcast([P, H, NP]), op=ALU.mult)
+            k1s[i] = k1
 
-        def u3_copy(i):
-            u3 = work.tile([P, P], F32, name=f"u3_{i}", tag="u3", align_bytes=64)
-            nc.scalar.copy(out=u3[:], in_=ups[i][:, H - 1, :])
-            u3s[i] = u3
+        def rope_add(i):
+            engine = nc.vector if i >= NT - V_ADDS else nc.gpsimd
+            engine.tensor_tensor(
+                out=result(i, 1).rearrange("p n (i e) -> p n i e", e=2),
+                in0=k23s[i][:], in1=k1s[i][:].unsqueeze(3).to_broadcast([P, H, NP, 2]), op=ALU.add)
 
-        def r_transpose(i):
-            rp = psum.tile([P, H, P], F32, name=f"rp{i}", tag="ra")
-            for n in range(H):
-                nc.tensor.matmul(rp[:, n, :], lhsT=ts[i][:, 0, n, :], rhs=ident[:], is_transpose=True,
-                                 start=True, stop=False)
-                nc.tensor.matmul(rp[:, n, :], lhsT=ts[i][:, 1, n, :], rhs=perm[:], is_transpose=True,
-                                 start=False, stop=True)
-            rps[i] = rp
-
-        def r_copy(i):
-            nc.scalar.copy(out=osb[i // 2][:, :, i % 2, DH : 2 * DH], in_=rps[i][:])
-
-        def store(i):
+        def store(i, part):
             c = i // 4
             b, half = c // 2, c % 2
-            if i < NT - 4:
-                if i % 2 == 0:
-                    return
-                j0, j1, k0, k1 = i % 4 - 1, i % 4 + 1, 0, 2
-            else:
-                j0, j1, k0, k1 = i % 4, i % 4 + 1, i % 2, i % 2 + 1
-            for n in range(H):
-                nc.sync.dma_start(
-                    out=out[b, n, half * 512 : (half + 1) * 512, :].rearrange("(p j) d -> p j d", j=4)[:, j0:j1, :],
-                    in_=osb[i // 2][:, n, k0:k1, :])
+            rows = out[b, :, half * 512 : (half + 1) * 512, :].rearrange("n (p j) d -> p n j d", j=4)
+            if i >= NT - HALVES:
+                nc.sync.dma_start(out=rows[:, :, i % 4, part * DH : (part + 1) * DH], in_=result(i, part))
+            elif i >= NT - SINGLE:
+                nc.sync.dma_start(out=rows[:, :, i % 4, :], in_=osb[i, 0][:])
+            elif i % 2 == 1:
+                nc.sync.dma_start(out=rows[:, :, i % 4 - 1 : i % 4 + 1, :].rearrange("p n j d -> p n (j d)"),
+                                  in_=osb[i // 2][:].rearrange("p n j d -> p n (j d)"))
 
         def ok(i):
             return 0 <= i < NT
 
+        def finish(i):
+            rope_add(i)
+            store(i, 1)
+
         def step(s):
-            if ok(s - 1):
-                h_quant(s - 1)
-            if ok(s - 2):
-                c_quant(s - 2)
-                tick(s - 2)
-            widen_to(WT(s))
+            if s < NT + 2:
+                quant_step(s)
+            if s - 4 >= NT - V_ADDS:
+                finish(s - 4)
+            nxt = s + LEAD if s < SPLIT else SPLIT + LEAD + (s - SPLIT) // 2
+            first = s < SPLIT or (s - SPLIT) % 2 == 0
+            if first and ok(nxt + 1):
+                h_transpose(nxt + 1)
+            if first and ok(nxt + 2):
+                cast(nxt + 2, nc.scalar.copy)
             if ok(s):
-                h_transpose(s)
-                h_copy(s)
-            if ok(s - 4):
-                r_transpose(s - 4)
-                r_copy(s - 4)
-                store(s - 4)
-            if ok(s - 3):
-                rope_mul(s - 3)
-            if ok(s - 1):
-                mm1(s - 1)
-                c_copy(s - 1)
-
+                mm1(s)
+                c_copy(s)
             if ok(s - 2):
-                mm2u(s - 2)
-                mm2a(s - 2)
-                u3_copy(s - 2)
+                mm2(s - 2)
                 a_copy(s - 2)
+                if s - 2 >= NT - HALVES:
+                    store(s - 2, 0)
+            if s < SPLIT:
+                h_scale_mul(nxt)
+            elif ok(nxt):
+                h_scale_mul(nxt, (s - SPLIT) % 2, (s - SPLIT) % 2 + 1)
+            if ok(s - 3):
+                rope_k23(s - 3)
+                rope_k1(s - 3)
+                if s - 3 < NT - V_ADDS or s - 3 == NT - 1:
+                    finish(s - 3)
 
-        whole_v(0)
-        widen_to(1)
-        frac_v(0)
-        wcq_copy(A, 0)
-        tables_s(0)
-        widen_to(2)
+        tables_turns(0)
+        tables_turns(1)
+        cast(0, nc.vector.tensor_copy)
+        for stage in (tables_whole, tables_frac):
+            for f in range(2):
+                stage(f)
         h_transpose(0)
-        h_copy(0)
+        tables_sin(0, 0)
+        tables_sin(0, 1)
+        cast(1, nc.scalar.copy)
+        wcq_copy(nc.vector.tensor_copy, 0)
+        wcq_copy(pool_copy, 1)
+        wqr_copy(pool_copy, early_g[:, 0, :], 0)
         h_transpose(1)
-        h_copy(1)
-        wcq_copy(V, 1)
-        wcq_quant(0)
-        wcq_quant(1)
-        h_quant(0)
-        w_copy(A, wqr_g, wqr_raw)
+        h_scale_mul(0)
+        for i in (2, 3):
+            cast(i, nc.scalar.copy)
+            h_transpose(i)
+            h_scale_mul(i - 1)
+        tables_sin(1, 0)
+        tables_sin(1, 1)
+        tables_cos()
+        cast(4, nc.scalar.copy)
+        h_transpose(4)
+        h_scale_mul(3)
+        quant_step(0)
+        quant(wcq_codes[:].rearrange("p g c -> p (g c)"), wcq_sc[:].rearrange("p g c -> p (g c)"),
+              wcq_g[:].rearrange("p g c -> p (g c)"))
+        quant_step(1)
+        quant(w2_codes[:, 0:256], w2_sc[:, 0:256], early_g[:, 0, :])
+        tables_mix()
+        late_g = keep.tile([P, 2, 1024], BF16, name="late_g", tag="late", align_bytes=64)
+        wqr_copy(pool_copy, late_g[:, 0, :], 1)
+        wq_copy(pool_copy, late_g[:, 1, :], 0)
+        cast(5, nc.scalar.copy)
+        h_transpose(5)
+        wq_copy(nc.scalar.copy, early_g[:, 1, :], 1)
+        cast(6, nc.scalar.copy)
         mm1(0)
-        widen_to(3)
-        h_quant(1)
-        c_copy(0)
-        nc.vector.quantize_mx(out=wqr_codes[:].bitcast(FP8X4), scales=wqr_sc[:], in_=wqr_g[:])
-        w_copy(A, wq_g, wq_raw)
-        c_quant(0)
-        whole_v(1)
-        h_transpose(2)
-        h_copy(2)
         mm1(1)
+        h_scale_mul(4)
+        h_transpose(6)
+        h_scale_mul(5)
+        cast(7, nc.scalar.copy)
+        c_copy(0)
         c_copy(1)
-        widen_to(4)
-        frac_v(1)
-        nc.vector.quantize_mx(out=wq_codes[:].bitcast(FP8X4), scales=wq_sc[:], in_=wq_g[:])
-        mm2u(0)
-        mm2a(0)
-        u3_copy(0)
-        a_copy(0)
-        tables_s(1)
-        for s in range(3, NT + 4):
+        h_transpose(7)
+        h_scale_mul(6)
+        cast(8, nc.scalar.copy)
+        quant(w2_codes[:, 768:1024], w2_sc[:, 768:1024], early_g[:, 1, :])
+        quant(w2_codes[:, 256:768], w2_sc[:, 256:768], late_g[:].rearrange("p f c -> p (f c)"))
+        for s in range(2, NT + 3):
             step(s)

@@ -2,7 +2,6 @@ from contextlib import ExitStack
 import math
 
 import concourse.mybir as mybir
-from concourse.masks import make_identity
 
 F32 = mybir.dt.float32
 BF16 = mybir.dt.bfloat16
@@ -20,8 +19,9 @@ NT = B * S // P
 NC = NT // 4
 NP = DH // 2
 LEAD = 5
-V_ADDS = 3
-SINGLE = 6
+V_ADDS = 2
+WIDE = 48
+SINGLE = 8
 HALVES = 2
 SPLIT = NT - 2 * (LEAD - 1) - 1
 KINDS = 8
@@ -58,10 +58,12 @@ def tile_mla_pa_t_kernel(tc, h_bytes, h_scale, w_cq, w_q, w_qr, out):
         load_wcq(0)
         load_h(0, 1, 2)
         nc.sync.dma_start(out=scale[:], in_=h_scale.rearrange("a b (g p t) -> p (a b g) t", g=2, t=4))
+        load_h(0, 2, 3)
         load_wcq(1)
-        load_h(0, 2, 4)
+        load_h(0, 3, 4)
+        load_h(1, 0, 2)
         nc.sync.dma_start(out=wqr_raw[:], in_=w_qr.rearrange("(p j) c -> p j c", j=4))
-        load_h(1, 0, 4)
+        load_h(1, 2, 4)
         nc.sync.dma_start(out=wq_raw[:], in_=w_q.rearrange("(p j) c -> p j c", j=4))
         for c in range(2, NC):
             load_h(c, 0, 4)
@@ -69,62 +71,62 @@ def tile_mla_pa_t_kernel(tc, h_bytes, h_scale, w_cq, w_q, w_qr, out):
         pos = keep.tile([P, KINDS], F32, name="pos")
         nc.gpsimd.iota(pos[:].rearrange("p (c j) -> p c j", c=2), pattern=[[512, 2], [1, 4]],
                        base=0, channel_multiplier=4, allow_small_or_imprecise_dtypes=True)
-        ident = keep.tile([P, P], F32, name="ident", align_bytes=64)
-        make_identity(nc, ident[:])
+        offs = keep.tile([P, P], F32, name="offs", align_bytes=64)
+        nc.gpsimd.iota(offs[:], pattern=[[1, P]], base=0, channel_multiplier=-1,
+                       allow_small_or_imprecise_dtypes=True)
         one = keep.tile([P, 1], F32, name="one")
         nc.vector.memset(one[:], 1.0)
+
+        def constant(dst, value):
+            nc.vector.tensor_scalar(out=dst, in0=one[:], scalar1=value, scalar2=None, op0=ALU.mult)
+
         th = keep.tile([P, NP], F32, name="th")
         for a in range(4):
-            nc.vector.tensor_scalar(out=th[:, a : a + 1], in0=one[:], scalar1=10000.0 ** (-a / NP) / (2.0 * math.pi),
-                                    scalar2=None, op0=ALU.mult)
+            constant(th[:, a : a + 1], 10000.0 ** (-a / NP) / (2.0 * math.pi))
         hpi = keep.tile([P, 1], F32, name="hpi")
-        nc.vector.tensor_scalar(out=hpi[:], in0=one[:], scalar1=math.pi / 2, scalar2=None, op0=ALU.mult)
+        constant(hpi[:], math.pi / 2)
         for w in (4, 16):
             for a in range(1, 4):
                 nc.vector.tensor_scalar(out=th[:, a * w : (a + 1) * w], in0=th[:, 0:w],
                                         scalar1=10000.0 ** (-a * w / NP), scalar2=None, op0=ALU.mult)
-        M = KINDS * NP
-        turns = keep.tile([P, M], F32, name="turns", align_bytes=64)
-        whole = keep.tile([P, M], I32, name="whole", align_bytes=64)
-        frac = keep.tile([P, M], F32, name="frac", align_bytes=64)
-        fabs = keep.tile([P, M], F32, name="fabs", align_bytes=64)
-        sines = keep.tile([P, 2, M], F32, name="sines", tag="late", align_bytes=64)
-        cos = keep.tile([P, M], F32, name="cos", align_bytes=64)
-        mix = keep.tile([P, M, 2], F32, name="mix", align_bytes=64)
+        turns = keep.tile([P, KINDS, NP], F32, name="turns", align_bytes=64)
+        whole = keep.tile([P, KINDS, NP], I32, name="whole", align_bytes=64)
+        frac = keep.tile([P, KINDS, NP], F32, name="frac", align_bytes=64)
+        fabs = keep.tile([P, KINDS, NP], F32, name="fabs", align_bytes=64)
+        sines = keep.tile([P, 2, KINDS, NP], F32, name="sines", align_bytes=64)
+        cos = keep.tile([P, KINDS, NP], F32, name="cos", align_bytes=64)
+        for i0, i1 in ((WIDE, NP), (0, WIDE)):
+            nc.vector.tensor_tensor(out=turns[:, :, i0:i1], in0=pos[:].unsqueeze(2).to_broadcast([P, KINDS, i1 - i0]),
+                                    in1=th[:, i0:i1].unsqueeze(1).to_broadcast([P, KINDS, i1 - i0]), op=ALU.mult)
+        nc.scalar.activation(out=sines[:, 1, :, WIDE:NP], in_=turns[:, :, WIDE:NP], func=ACT.Sin, scale=2.0 * math.pi)
+        ident = keep.tile([P, P], F32, name="ident", align_bytes=64)
+        nc.vector.tensor_scalar(out=ident[:], in0=offs[:], scalar1=0.0, scalar2=None, op0=ALU.is_equal)
+        nc.vector.tensor_copy(out=whole[:], in_=turns[:])
+        nc.vector.tensor_tensor(out=frac[:], in0=turns[:], in1=whole[:], op=ALU.subtract)
 
-        def half_cols(f):
-            return slice(f * M // 2, (f + 1) * M // 2)
-
-        def tables_turns(f):
-            nc.vector.tensor_tensor(out=turns[:, half_cols(f)].rearrange("p (k i) -> p k i", k=4),
-                                    in0=pos[:, 4 * f : 4 * f + 4].unsqueeze(2).to_broadcast([P, 4, NP]),
-                                    in1=th[:].unsqueeze(1).to_broadcast([P, 4, NP]), op=ALU.mult)
-
-        def tables_whole(f):
-            nc.vector.tensor_copy(out=whole[:, half_cols(f)], in_=turns[:, half_cols(f)])
-
-        def tables_frac(f):
-            cols = half_cols(f)
-            nc.vector.tensor_tensor(out=frac[:, cols], in0=turns[:, cols], in1=whole[:, cols], op=ALU.subtract)
-
-        def tables_sin(f, e):
-            nc.scalar.activation(out=sines[:, e, half_cols(f)], in_=frac[:, half_cols(f)], func=ACT.Sin,
-                                 scale=(2.0 * e - 1.0) * 2.0 * math.pi)
-
-        def tables_cos():
+        def tables_sin_cos():
             nc.scalar.activation(out=fabs[:], in_=frac[:], func=ACT.Abs)
+            nc.scalar.activation(out=sines[:, 1, :, 0:WIDE], in_=frac[:, :, 0:WIDE], func=ACT.Sin, scale=2.0 * math.pi)
             nc.scalar.activation(out=cos[:], in_=fabs[:], func=ACT.Sin, scale=-2.0 * math.pi, bias=hpi[:, 0:1])
+            nc.scalar.activation(out=sines[:, 0], in_=frac[:], func=ACT.Sin, scale=-2.0 * math.pi)
 
-        def tables_mix():
-            nc.vector.tensor_tensor(out=mix[:], in0=sines[:].rearrange("p e m -> p m e"),
-                                    in1=cos[:].unsqueeze(2).to_broadcast([P, M, 2]), op=ALU.subtract)
+        mix = {}
+
+        def tables_mix(f, tag):
+            mix[f] = keep.tile([P, 4 * NP, 2], F32, name=f"mix{f}", tag=tag, align_bytes=64)
+            kinds = slice(4 * f, 4 * f + 4)
+            nc.gpsimd.tensor_tensor(
+                out=mix[f][:], in0=sines[:, :, kinds, :].rearrange("p e k i -> p (k i) e"),
+                in1=cos[:, kinds, :].rearrange("p k i -> p (k i)").unsqueeze(2).to_broadcast([P, 4 * NP, 2]),
+                op=ALU.subtract)
 
         wcq_codes = keep.tile([P, 2, CQ], U32, name="wcq_codes", align_bytes=64)
         wcq_sc = keep.tile([P, 2, CQ], U8, name="wcq_sc", align_bytes=64)
         w2_codes = keep.tile([P, 1024], U32, name="w2_codes", align_bytes=64)
         w2_sc = keep.tile([P, 1024], U8, name="w2_sc", align_bytes=64)
         wcq_g = keep.tile([P, 2, 4 * CQ], BF16, name="wcq_g", align_bytes=64)
-        early_g = keep.tile([P, 2, 1024], BF16, name="early_g", align_bytes=64)
+        first_g = keep.tile([P, 1024], BF16, name="first_g", tag="late", align_bytes=64)
+        last_g = keep.tile([P, 1024], BF16, name="last_g", tag="last", align_bytes=64)
 
         def pool_copy(out, in_):
             nc.gpsimd.tensor_scalar(out=out, in0=in_, scalar1=1.0, scalar2=0.0, op0=ALU.mult, op1=ALU.add)
@@ -152,7 +154,8 @@ def tile_mla_pa_t_kernel(tc, h_bytes, h_scale, w_cq, w_q, w_qr, out):
             xb[i] = x
 
         def h_transpose(i):
-            ht = psum.tile([P, 2, 2, P], F32, name=f"ht{i}", tag="ht")
+            tag, bufs = ("m2", 5) if i in (2, 5) else ("ht", 2)
+            ht = psum.tile([P, 2, 2, P], F32, name=f"ht{i}", tag=tag, bufs=bufs)
             words = xb[i][:].bitcast(F32)
             for g in range(2):
                 for u in range(2):
@@ -161,7 +164,7 @@ def tile_mla_pa_t_kernel(tc, h_bytes, h_scale, w_cq, w_q, w_qr, out):
 
         def group(i):
             if i not in grp:
-                grp[i] = work.tile([P, D + CQ], BF16, name=f"g{i}", tag="g", bufs=LEAD + 3, align_bytes=64)
+                grp[i] = work.tile([P, D + CQ], BF16, name=f"g{i}", tag="g", bufs=LEAD + 4, align_bytes=64)
             return grp[i]
 
         def h_scale_mul(i, g0=0, g1=2):
@@ -173,17 +176,17 @@ def tile_mla_pa_t_kernel(tc, h_bytes, h_scale, w_cq, w_q, w_qr, out):
                     [P, g1 - g0, P, 2, 2]),
                 op=ALU.mult)
 
-        def quant_step(s):
-            codes = work.tile([P, 384], U32, name=f"q{s}", tag="q", align_bytes=64)
-            sc = work.tile([P, 384], U8, name=f"qs{s}", tag="qs", align_bytes=64)
-            lo = 0 if s < NT else 256
-            hi = 384 if s >= 2 else 256
+        def quant_step(s, lo, hi):
+            if s not in cq:
+                codes = work.tile([P, 384], U32, name=f"q{s}", tag="q", bufs=5, align_bytes=64)
+                sc = work.tile([P, 384], U8, name=f"qs{s}", tag="qs", bufs=5, align_bytes=64)
+                cq[s] = (codes, sc)
+            codes, sc = cq[s]
             quant(codes[:, lo:hi], sc[:, lo:hi], group(s)[:, 4 * lo : 4 * hi])
-            cq[s] = (codes, sc)
 
         def mm1(i):
             codes, sc = cq[i]
-            tag, bufs = ("m2", 5) if i == 0 else ("cp", 1)
+            tag, bufs = ("m2", 5) if i in (0, 2) else ("cp", 1)
             cp = psum.tile([P, 4, P], F32, name=f"cp{i}", tag=tag, bufs=bufs)
             for t in range(4):
                 for g in range(2):
@@ -208,13 +211,19 @@ def tile_mla_pa_t_kernel(tc, h_bytes, h_scale, w_cq, w_q, w_qr, out):
                                     rhs=w2_codes[:, c0:c1].bitcast(FP8X4), rhs_scale=w2_sc[:, c0:c1],
                                     start=start, stop=stop)
 
-            aps[i] = psum.tile([P, 512], F32, name=f"ap{i}", tag="m2", bufs=5)
-            mm(aps[i][:], 512, 1024, True, True)
+            def mm_a(tag, bufs):
+                aps[i] = psum.tile([P, 512], F32, name=f"ap{i}", tag=tag, bufs=bufs)
+                mm(aps[i][:], 512, 1024, True, True)
+
+            if i < NT - HALVES:
+                mm_a("m2", 5)
             ups[i] = psum.tile([P, 512], F32, name=f"up{i}", tag="m2", bufs=5)
             mm(ups[i][:], 0, 512, True, True)
             sps[i] = psum.tile([P, 256], F32, name=f"sp{i}", tag="m2", bufs=5)
             mm(sps[i][:], 0, 256, True, False)
             mm(sps[i][:], 256, 512, False, True)
+            if i >= NT - HALVES:
+                mm_a("ht", 2)
 
         def result(i, part):
             if i >= NT - HALVES:
@@ -237,7 +246,7 @@ def tile_mla_pa_t_kernel(tc, h_bytes, h_scale, w_cq, w_q, w_qr, out):
             kind = i % KINDS
             nc.vector.tensor_tensor(
                 out=k23[:], in0=ups[i][:].rearrange("p (f n i) -> p n i f", f=2, n=H),
-                in1=mix[:, NP * kind : NP * (kind + 1), :].unsqueeze(1).to_broadcast([P, H, NP, 2]), op=ALU.mult)
+                in1=mix[kind // 4][:, NP * (kind % 4) : NP * (kind % 4 + 1), :].unsqueeze(1).to_broadcast([P, H, NP, 2]), op=ALU.mult)
             k23s[i] = k23
 
         def rope_k1(i):
@@ -245,7 +254,7 @@ def tile_mla_pa_t_kernel(tc, h_bytes, h_scale, w_cq, w_q, w_qr, out):
             kind = i % KINDS
             nc.vector.tensor_tensor(
                 out=k1[:], in0=sps[i][:].rearrange("p (n i) -> p n i", n=H),
-                in1=cos[:, NP * kind : NP * (kind + 1)].unsqueeze(1).to_broadcast([P, H, NP]), op=ALU.mult)
+                in1=cos[:, kind, :].unsqueeze(1).to_broadcast([P, H, NP]), op=ALU.mult)
             k1s[i] = k1
 
         def rope_add(i):
@@ -274,17 +283,15 @@ def tile_mla_pa_t_kernel(tc, h_bytes, h_scale, w_cq, w_q, w_qr, out):
             store(i, 1)
 
         def step(s):
-            if s < NT + 2:
-                quant_step(s)
-            if s - 4 >= NT - V_ADDS:
-                finish(s - 4)
+            if 3 < s < NT + 2:
+                quant_step(s, 0 if s < NT else 256, 384)
             nxt = s + LEAD if s < SPLIT else SPLIT + LEAD + (s - SPLIT) // 2
             first = s < SPLIT or (s - SPLIT) % 2 == 0
             if first and ok(nxt + 1):
                 h_transpose(nxt + 1)
             if first and ok(nxt + 2):
                 cast(nxt + 2, nc.scalar.copy)
-            if ok(s):
+            if 3 < s < NT:
                 mm1(s)
                 c_copy(s)
             if ok(s - 2):
@@ -299,59 +306,62 @@ def tile_mla_pa_t_kernel(tc, h_bytes, h_scale, w_cq, w_q, w_qr, out):
             if ok(s - 3):
                 rope_k23(s - 3)
                 rope_k1(s - 3)
-                if s - 3 < NT - V_ADDS or s - 3 == NT - 1:
+                if s - 3 < NT - V_ADDS:
                     finish(s - 3)
 
-        tables_turns(0)
-        tables_turns(1)
-        cast(0, nc.vector.tensor_copy)
-        for stage in (tables_whole, tables_frac):
-            for f in range(2):
-                stage(f)
+        cast(0, nc.scalar.copy)
         h_transpose(0)
-        tables_sin(0, 0)
-        tables_sin(0, 1)
         cast(1, nc.scalar.copy)
         wcq_copy(nc.vector.tensor_copy, 0)
         wcq_copy(pool_copy, 1)
-        wqr_copy(pool_copy, early_g[:, 0, :], 0)
+        wqr_copy(pool_copy, first_g[:], 0)
         h_transpose(1)
         h_scale_mul(0)
-        for i in (2, 3):
+        for i in (2, 3, 4):
             cast(i, nc.scalar.copy)
             h_transpose(i)
             h_scale_mul(i - 1)
-        tables_sin(1, 0)
-        tables_sin(1, 1)
-        tables_cos()
-        cast(4, nc.scalar.copy)
-        h_transpose(4)
-        h_scale_mul(3)
-        quant_step(0)
+        cast(5, nc.scalar.copy)
+        h_transpose(5)
+        tables_sin_cos()
+        quant_step(0, 0, 256)
         quant(wcq_codes[:].rearrange("p g c -> p (g c)"), wcq_sc[:].rearrange("p g c -> p (g c)"),
               wcq_g[:].rearrange("p g c -> p (g c)"))
-        quant_step(1)
-        quant(w2_codes[:, 0:256], w2_sc[:, 0:256], early_g[:, 0, :])
-        tables_mix()
+        for i in (1, 2, 3):
+            quant_step(i, 0, 256)
+        quant(w2_codes[:, 0:256], w2_sc[:, 0:256], first_g[:])
         late_g = keep.tile([P, 2, 1024], BF16, name="late_g", tag="late", align_bytes=64)
         wqr_copy(pool_copy, late_g[:, 0, :], 1)
         wq_copy(pool_copy, late_g[:, 1, :], 0)
-        cast(5, nc.scalar.copy)
-        h_transpose(5)
-        wq_copy(nc.scalar.copy, early_g[:, 1, :], 1)
+        tables_mix(0, "mix0")
         cast(6, nc.scalar.copy)
-        mm1(0)
-        mm1(1)
         h_scale_mul(4)
+        mm1(0)
         h_transpose(6)
-        h_scale_mul(5)
+        mm1(1)
         cast(7, nc.scalar.copy)
+        h_scale_mul(5)
         c_copy(0)
-        c_copy(1)
         h_transpose(7)
-        h_scale_mul(6)
+        mm1(2)
         cast(8, nc.scalar.copy)
-        quant(w2_codes[:, 768:1024], w2_sc[:, 768:1024], early_g[:, 1, :])
+        h_scale_mul(6)
+        c_copy(1)
+        h_transpose(8)
+        mm1(3)
+        wq_copy(nc.scalar.copy, last_g[:], 1)
+        h_scale_mul(7)
+        c_copy(2)
+        cast(9, nc.scalar.copy)
+        c_copy(3)
         quant(w2_codes[:, 256:768], w2_sc[:, 256:768], late_g[:].rearrange("p f c -> p (f c)"))
-        for s in range(2, NT + 3):
+        quant_step(2, 256, 384)
+        quant_step(3, 256, 384)
+        quant(w2_codes[:, 768:1024], w2_sc[:, 768:1024], last_g[:])
+        tables_mix(1, "last")
+        mm2(0)
+        a_copy(0)
+        for s in range(3, NT + 3):
             step(s)
+        for i in range(NT - V_ADDS, NT):
+            finish(i)

@@ -18,12 +18,14 @@ P = 128
 NT = B * S // P
 NC = NT // 4
 NP = DH // 2
-LEAD = 5
+LEAD = 6
 V_ADDS = 2
-WIDE = 48
+WIDE = 44
 SINGLE = 8
-HALVES = 2
-SPLIT = NT - 2 * (LEAD - 1) - 1
+HALVES = 5
+U_FIRST = 3
+PACE = 3
+SPLIT = -(-(4 * NT - PACE * (NT - 1) - 4 * LEAD) // (4 - PACE))
 KINDS = 8
 
 FLOPS = 2 * B * S * (D * CQ + 2 * CQ * H * DH) + 3 * B * S * H * DH
@@ -89,20 +91,20 @@ def tile_mla_pa_t_kernel(tc, h_bytes, h_scale, w_cq, w_q, w_qr, out):
             for a in range(1, 4):
                 nc.vector.tensor_scalar(out=th[:, a * w : (a + 1) * w], in0=th[:, 0:w],
                                         scalar1=10000.0 ** (-a * w / NP), scalar2=None, op0=ALU.mult)
-        turns = keep.tile([P, KINDS, NP], F32, name="turns", align_bytes=64)
-        whole = keep.tile([P, KINDS, NP], I32, name="whole", align_bytes=64)
+        turns = keep.tile([P, KINDS, WIDE], F32, name="turns", align_bytes=64)
+        whole = keep.tile([P, KINDS, WIDE], I32, name="whole", align_bytes=64)
         frac = keep.tile([P, KINDS, NP], F32, name="frac", align_bytes=64)
         fabs = keep.tile([P, KINDS, NP], F32, name="fabs", align_bytes=64)
         sines = keep.tile([P, 2, KINDS, NP], F32, name="sines", align_bytes=64)
         cos = keep.tile([P, KINDS, NP], F32, name="cos", align_bytes=64)
-        for i0, i1 in ((WIDE, NP), (0, WIDE)):
-            nc.vector.tensor_tensor(out=turns[:, :, i0:i1], in0=pos[:].unsqueeze(2).to_broadcast([P, KINDS, i1 - i0]),
+        for dst, i0, i1 in ((frac[:, :, WIDE:NP], WIDE, NP), (turns[:], 0, WIDE)):
+            nc.vector.tensor_tensor(out=dst, in0=pos[:].unsqueeze(2).to_broadcast([P, KINDS, i1 - i0]),
                                     in1=th[:, i0:i1].unsqueeze(1).to_broadcast([P, KINDS, i1 - i0]), op=ALU.mult)
-        nc.scalar.activation(out=sines[:, 1, :, WIDE:NP], in_=turns[:, :, WIDE:NP], func=ACT.Sin, scale=2.0 * math.pi)
+        nc.scalar.activation(out=sines[:, 1, :, WIDE:NP], in_=frac[:, :, WIDE:NP], func=ACT.Sin, scale=2.0 * math.pi)
         ident = keep.tile([P, P], F32, name="ident", align_bytes=64)
         nc.vector.tensor_scalar(out=ident[:], in0=offs[:], scalar1=0.0, scalar2=None, op0=ALU.is_equal)
         nc.vector.tensor_copy(out=whole[:], in_=turns[:])
-        nc.vector.tensor_tensor(out=frac[:], in0=turns[:], in1=whole[:], op=ALU.subtract)
+        nc.vector.tensor_tensor(out=frac[:, :, 0:WIDE], in0=turns[:], in1=whole[:], op=ALU.subtract)
 
         def tables_sin_cos():
             nc.scalar.activation(out=fabs[:], in_=frac[:], func=ACT.Abs)
@@ -112,10 +114,10 @@ def tile_mla_pa_t_kernel(tc, h_bytes, h_scale, w_cq, w_q, w_qr, out):
 
         mix = {}
 
-        def tables_mix(f, tag):
+        def tables_mix(engine, f, tag):
             mix[f] = keep.tile([P, 4 * NP, 2], F32, name=f"mix{f}", tag=tag, align_bytes=64)
             kinds = slice(4 * f, 4 * f + 4)
-            nc.gpsimd.tensor_tensor(
+            engine.tensor_tensor(
                 out=mix[f][:], in0=sines[:, :, kinds, :].rearrange("p e k i -> p (k i) e"),
                 in1=cos[:, kinds, :].rearrange("p k i -> p (k i)").unsqueeze(2).to_broadcast([P, 4 * NP, 2]),
                 op=ALU.subtract)
@@ -154,7 +156,7 @@ def tile_mla_pa_t_kernel(tc, h_bytes, h_scale, w_cq, w_q, w_qr, out):
             xb[i] = x
 
         def h_transpose(i):
-            tag, bufs = ("m2", 5) if i in (2, 5) else ("ht", 2)
+            tag, bufs = ("m2", 5) if i in (2, 6) else ("ht", 2)
             ht = psum.tile([P, 2, 2, P], F32, name=f"ht{i}", tag=tag, bufs=bufs)
             words = xb[i][:].bitcast(F32)
             for g in range(2):
@@ -167,14 +169,20 @@ def tile_mla_pa_t_kernel(tc, h_bytes, h_scale, w_cq, w_q, w_qr, out):
                 grp[i] = work.tile([P, D + CQ], BF16, name=f"g{i}", tag="g", bufs=LEAD + 4, align_bytes=64)
             return grp[i]
 
-        def h_scale_mul(i, g0=0, g1=2):
+        def h_scale_mul(i, q0=0, q1=4):
             halves = hps[i][:].rearrange("p u g n -> p (u g n)").bitcast(BF16)
-            nc.vector.tensor_tensor(
-                out=group(i)[:, 0:D].rearrange("p (g n u e) -> p g n u e", g=2, u=2, e=2)[:, g0:g1],
-                in0=halves.rearrange("p (u g n e) -> p g n u e", u=2, g=2, e=2)[:, g0:g1],
-                in1=scale[:, g0:g1, :].rearrange("p g (u e) -> p g u e", u=2).unsqueeze(2).to_broadcast(
-                    [P, g1 - g0, P, 2, 2]),
-                op=ALU.mult)
+            src = halves.rearrange("p (u g n e) -> p g n u e", u=2, g=2, e=2)
+            dst = group(i)[:, 0:D].rearrange("p (g n u e) -> p g n u e", g=2, u=2, e=2)
+            while q0 < q1:
+                whole_passes = (q1 - q0) // 2 if q0 % 2 == 0 else 0
+                g0, g1 = q0 // 2, q0 // 2 + max(whole_passes, 1)
+                n0, n1 = (0, P) if whole_passes else (64 * (q0 % 2), 64 * (q0 % 2) + 64)
+                nc.vector.tensor_tensor(
+                    out=dst[:, g0:g1, n0:n1], in0=src[:, g0:g1, n0:n1],
+                    in1=scale[:, g0:g1, :].rearrange("p g (u e) -> p g u e", u=2).unsqueeze(2).to_broadcast(
+                        [P, g1 - g0, n1 - n0, 2, 2]),
+                    op=ALU.mult)
+                q0 = q0 + max(2 * whole_passes, 1)
 
         def quant_step(s, lo, hi):
             if s not in cq:
@@ -215,14 +223,14 @@ def tile_mla_pa_t_kernel(tc, h_bytes, h_scale, w_cq, w_q, w_qr, out):
                 aps[i] = psum.tile([P, 512], F32, name=f"ap{i}", tag=tag, bufs=bufs)
                 mm(aps[i][:], 512, 1024, True, True)
 
-            if i < NT - HALVES:
+            if i < NT - U_FIRST:
                 mm_a("m2", 5)
             ups[i] = psum.tile([P, 512], F32, name=f"up{i}", tag="m2", bufs=5)
             mm(ups[i][:], 0, 512, True, True)
             sps[i] = psum.tile([P, 256], F32, name=f"sp{i}", tag="m2", bufs=5)
             mm(sps[i][:], 0, 256, True, False)
             mm(sps[i][:], 256, 512, False, True)
-            if i >= NT - HALVES:
+            if i >= NT - U_FIRST:
                 mm_a("ht", 2)
 
         def result(i, part):
@@ -282,15 +290,20 @@ def tile_mla_pa_t_kernel(tc, h_bytes, h_scale, w_cq, w_q, w_qr, out):
             rope_add(i)
             store(i, 1)
 
+        def quarters(s):
+            return min(4 * (min(s, SPLIT) + LEAD) + PACE * max(s - SPLIT, 0), 4 * NT)
+
+        def turn(s, done):
+            i = len(hps)
+            if ok(i) and 4 * i < quarters(s + 2) and 4 * (i - 1) <= done:
+                h_transpose(i)
+
         def step(s):
             if 3 < s < NT + 2:
                 quant_step(s, 0 if s < NT else 256, 384)
-            nxt = s + LEAD if s < SPLIT else SPLIT + LEAD + (s - SPLIT) // 2
-            first = s < SPLIT or (s - SPLIT) % 2 == 0
-            if first and ok(nxt + 1):
-                h_transpose(nxt + 1)
-            if first and ok(nxt + 2):
-                cast(nxt + 2, nc.scalar.copy)
+            turn(s, quarters(s))
+            if ok(len(xb)) and 4 * len(xb) < quarters(s + 3):
+                cast(len(xb), nc.scalar.copy)
             if 3 < s < NT:
                 mm1(s)
                 c_copy(s)
@@ -299,10 +312,10 @@ def tile_mla_pa_t_kernel(tc, h_bytes, h_scale, w_cq, w_q, w_qr, out):
                 a_copy(s - 2)
                 if s - 2 >= NT - HALVES:
                     store(s - 2, 0)
-            if s < SPLIT:
-                h_scale_mul(nxt)
-            elif ok(nxt):
-                h_scale_mul(nxt, (s - SPLIT) % 2, (s - SPLIT) % 2 + 1)
+            q0, q1 = quarters(s), quarters(s + 1)
+            for i in range(q0 // 4, -(-q1 // 4)):
+                h_scale_mul(i, max(q0 - 4 * i, 0), min(q1 - 4 * i, 4))
+            turn(s, q1)
             if ok(s - 3):
                 rope_k23(s - 3)
                 rope_k1(s - 3)
@@ -317,48 +330,48 @@ def tile_mla_pa_t_kernel(tc, h_bytes, h_scale, w_cq, w_q, w_qr, out):
         wqr_copy(pool_copy, first_g[:], 0)
         h_transpose(1)
         h_scale_mul(0)
-        for i in (2, 3, 4):
+        for i in range(2, 6):
             cast(i, nc.scalar.copy)
             h_transpose(i)
             h_scale_mul(i - 1)
-        cast(5, nc.scalar.copy)
-        h_transpose(5)
+        cast(6, nc.scalar.copy)
+        h_transpose(6)
         tables_sin_cos()
         quant_step(0, 0, 256)
         quant(wcq_codes[:].rearrange("p g c -> p (g c)"), wcq_sc[:].rearrange("p g c -> p (g c)"),
               wcq_g[:].rearrange("p g c -> p (g c)"))
         for i in (1, 2, 3):
             quant_step(i, 0, 256)
+        tables_mix(nc.vector, 0, "mix0")
         quant(w2_codes[:, 0:256], w2_sc[:, 0:256], first_g[:])
         late_g = keep.tile([P, 2, 1024], BF16, name="late_g", tag="late", align_bytes=64)
         wqr_copy(pool_copy, late_g[:, 0, :], 1)
         wq_copy(pool_copy, late_g[:, 1, :], 0)
-        tables_mix(0, "mix0")
-        cast(6, nc.scalar.copy)
-        h_scale_mul(4)
-        mm1(0)
-        h_transpose(6)
-        mm1(1)
         cast(7, nc.scalar.copy)
         h_scale_mul(5)
-        c_copy(0)
+        mm1(0)
         h_transpose(7)
-        mm1(2)
+        mm1(1)
         cast(8, nc.scalar.copy)
         h_scale_mul(6)
-        c_copy(1)
+        c_copy(0)
         h_transpose(8)
+        mm1(2)
+        cast(9, nc.scalar.copy)
+        h_scale_mul(7)
+        c_copy(1)
+        h_transpose(9)
         mm1(3)
         wq_copy(nc.scalar.copy, last_g[:], 1)
-        h_scale_mul(7)
+        h_scale_mul(8)
         c_copy(2)
-        cast(9, nc.scalar.copy)
+        cast(10, nc.scalar.copy)
         c_copy(3)
         quant(w2_codes[:, 256:768], w2_sc[:, 256:768], late_g[:].rearrange("p f c -> p (f c)"))
         quant_step(2, 256, 384)
         quant_step(3, 256, 384)
         quant(w2_codes[:, 768:1024], w2_sc[:, 768:1024], last_g[:])
-        tables_mix(1, "last")
+        tables_mix(nc.gpsimd, 1, "last")
         mm2(0)
         a_copy(0)
         for s in range(3, NT + 3):

@@ -208,8 +208,8 @@ def tile_mla_pa_t_kernel(tc, h_bytes, h_scale, w_cq, w_q, w_qr, out):
             cps[i] = cp
 
         def c_copy(i):
-            nc.scalar.copy(out=group(i + 2)[:, D : D + CQ].rearrange("p (n t) -> p n t", t=4),
-                           in_=cps[i][:].rearrange("p t n -> p n t"))
+            nc.scalar.copy(out=group(i + 2)[:, D : D + CQ].rearrange("p (m e t) -> p m t e", e=2, t=4),
+                           in_=cps[i][:].rearrange("p t (m e) -> p m t e", e=2))
 
         def mm2(i):
             codes, sc = cq[i + 2]

@@ -18,14 +18,15 @@ P = 128
 NT = B * S // P
 NC = NT // 4
 NP = DH // 2
-LEAD = 6
-V_ADDS = 2
+LEAD = 5
+LAG = 3
+V_ADDS = 3
 WIDE = 44
 SINGLE = 8
 HALVES = 5
 U_FIRST = 3
-PACE = 3
-SPLIT = -(-(4 * NT - PACE * (NT - 1) - 4 * LEAD) // (4 - PACE))
+PERIOD = 4
+FIRST = 5
 KINDS = 8
 
 FLOPS = 2 * B * S * (D * CQ + 2 * CQ * H * DH) + 3 * B * S * H * DH
@@ -148,7 +149,7 @@ def tile_mla_pa_t_kernel(tc, h_bytes, h_scale, w_cq, w_q, w_qr, out):
         def quant(codes, sc, grouped):
             nc.vector.quantize_mx(out=codes.bitcast(FP8X4), scales=sc, in_=grouped)
 
-        xb, hps, grp, cq, cps, ups, aps, sps, k1s, k23s, osb = ({} for k in range(11))
+        xb, hps, grp, cq, cps, ups, aps, sps, k1s, k23s, osb, prods = ({} for k in range(12))
 
         def cast(i, copy):
             x = work.tile([P, D], BF16, name=f"x{i}", tag="x", align_bytes=64)
@@ -166,7 +167,7 @@ def tile_mla_pa_t_kernel(tc, h_bytes, h_scale, w_cq, w_q, w_qr, out):
 
         def group(i):
             if i not in grp:
-                grp[i] = work.tile([P, D + CQ], BF16, name=f"g{i}", tag="g", bufs=LEAD + 4, align_bytes=64)
+                grp[i] = work.tile([P, D + CQ], BF16, name=f"g{i}", tag="g", bufs=LEAD + 5, align_bytes=64)
             return grp[i]
 
         def h_scale_mul(i, q0=0, q1=4):
@@ -186,15 +187,15 @@ def tile_mla_pa_t_kernel(tc, h_bytes, h_scale, w_cq, w_q, w_qr, out):
 
         def quant_step(s, lo, hi):
             if s not in cq:
-                codes = work.tile([P, 384], U32, name=f"q{s}", tag="q", bufs=5, align_bytes=64)
-                sc = work.tile([P, 384], U8, name=f"qs{s}", tag="qs", bufs=5, align_bytes=64)
+                codes = work.tile([P, 384], U32, name=f"q{s}", tag="q", bufs=6, align_bytes=64)
+                sc = work.tile([P, 384], U8, name=f"qs{s}", tag="qs", bufs=6, align_bytes=64)
                 cq[s] = (codes, sc)
             codes, sc = cq[s]
             quant(codes[:, lo:hi], sc[:, lo:hi], group(s)[:, 4 * lo : 4 * hi])
 
         def mm1(i):
             codes, sc = cq[i]
-            tag, bufs = ("m2", 5) if i in (0, 2) else ("cp", 1)
+            tag, bufs = ("m2", 5) if i in (0, 2, 4) else ("cp", 1)
             cp = psum.tile([P, 4, P], F32, name=f"cp{i}", tag=tag, bufs=bufs)
             for t in range(4):
                 for g in range(2):
@@ -207,15 +208,21 @@ def tile_mla_pa_t_kernel(tc, h_bytes, h_scale, w_cq, w_q, w_qr, out):
                         start=(g == 0), stop=(g == 1))
             cps[i] = cp
 
+        def c_place(i):
+            if i < NT - LAG:
+                return i + LAG, 256
+            return (NT, 128) if i == NT - 3 else (i + 2, 256)
+
         def c_copy(i):
-            nc.scalar.copy(out=group(i + 2)[:, D : D + CQ].rearrange("p (m e t) -> p m t e", e=2, t=4),
+            nc.scalar.copy(out=group(c_place(i)[0])[:, 4 * c_place(i)[1] : 4 * c_place(i)[1] + CQ].rearrange("p (m e t) -> p m t e", e=2, t=4),
                            in_=cps[i][:].rearrange("p t (m e) -> p m t e", e=2))
 
         def mm2(i):
-            codes, sc = cq[i + 2]
+            codes, sc = cq[c_place(i)[0]]
+            cols = slice(c_place(i)[1], c_place(i)[1] + P)
 
             def mm(dst, c0, c1, start, stop):
-                nc.tensor.matmul_mx(out=dst, lhsT=codes[:, 256:384].bitcast(FP8X4), lhsT_scale=sc[:, 256:384],
+                nc.tensor.matmul_mx(out=dst, lhsT=codes[:, cols].bitcast(FP8X4), lhsT_scale=sc[:, cols],
                                     rhs=w2_codes[:, c0:c1].bitcast(FP8X4), rhs_scale=w2_sc[:, c0:c1],
                                     start=start, stop=stop)
 
@@ -225,11 +232,11 @@ def tile_mla_pa_t_kernel(tc, h_bytes, h_scale, w_cq, w_q, w_qr, out):
 
             if i < NT - U_FIRST:
                 mm_a("m2", 5)
-            ups[i] = psum.tile([P, 512], F32, name=f"up{i}", tag="m2", bufs=5)
-            mm(ups[i][:], 0, 512, True, True)
             sps[i] = psum.tile([P, 256], F32, name=f"sp{i}", tag="m2", bufs=5)
             mm(sps[i][:], 0, 256, True, False)
             mm(sps[i][:], 256, 512, False, True)
+            ups[i] = psum.tile([P, 512], F32, name=f"up{i}", tag="m2", bufs=5)
+            mm(ups[i][:], 0, 512, True, True)
             if i >= NT - U_FIRST:
                 mm_a("ht", 2)
 
@@ -250,18 +257,20 @@ def tile_mla_pa_t_kernel(tc, h_bytes, h_scale, w_cq, w_q, w_qr, out):
             nc.scalar.copy(out=result(i, 0), in_=aps[i][:].rearrange("p (n d) -> p n d", n=H))
 
         def rope_k23(i):
-            k23 = work.tile([P, H, NP, 2], F32, name=f"k23_{i}", tag="k23", align_bytes=64)
+            if i % 4 == 0:
+                prods[i // 4] = work.tile([P, 4 * 768], F32, name=f"prod{i}", tag="prod", bufs=2, align_bytes=64)
+            k23 = prods[i // 4][:, 768 * (i % 4) : 768 * (i % 4) + 512].rearrange("p (n i e) -> p n i e", n=H, e=2)
             kind = i % KINDS
             nc.vector.tensor_tensor(
-                out=k23[:], in0=ups[i][:].rearrange("p (f n i) -> p n i f", f=2, n=H),
+                out=k23, in0=ups[i][:].rearrange("p (f n i) -> p n i f", f=2, n=H),
                 in1=mix[kind // 4][:, NP * (kind % 4) : NP * (kind % 4 + 1), :].unsqueeze(1).to_broadcast([P, H, NP, 2]), op=ALU.mult)
             k23s[i] = k23
 
         def rope_k1(i):
-            k1 = work.tile([P, H, NP], F32, name=f"k1_{i}", tag="k1", align_bytes=64)
+            k1 = prods[i // 4][:, 768 * (i % 4) + 512 : 768 * (i % 4 + 1)].rearrange("p (n i) -> p n i", n=H)
             kind = i % KINDS
             nc.vector.tensor_tensor(
-                out=k1[:], in0=sps[i][:].rearrange("p (n i) -> p n i", n=H),
+                out=k1, in0=sps[i][:].rearrange("p (n i) -> p n i", n=H),
                 in1=cos[:, kind, :].unsqueeze(1).to_broadcast([P, H, NP]), op=ALU.mult)
             k1s[i] = k1
 
@@ -269,7 +278,7 @@ def tile_mla_pa_t_kernel(tc, h_bytes, h_scale, w_cq, w_q, w_qr, out):
             engine = nc.vector if i >= NT - V_ADDS else nc.gpsimd
             engine.tensor_tensor(
                 out=result(i, 1).rearrange("p n (i e) -> p n i e", e=2),
-                in0=k23s[i][:], in1=k1s[i][:].unsqueeze(3).to_broadcast([P, H, NP, 2]), op=ALU.add)
+                in0=k23s[i], in1=k1s[i].unsqueeze(3).to_broadcast([P, H, NP, 2]), op=ALU.add)
 
         def store(i, part):
             c = i // 4
@@ -291,36 +300,37 @@ def tile_mla_pa_t_kernel(tc, h_bytes, h_scale, w_cq, w_q, w_qr, out):
             store(i, 1)
 
         def quarters(s):
-            return min(4 * (min(s, SPLIT) + LEAD) + PACE * max(s - SPLIT, 0), 4 * NT)
+            short = sum(1 for r in range(FIRST, s) if (r - FIRST) % PERIOD < 2 and (r - FIRST) // PERIOD < LEAD - 1)
+            return min(4 * (s + LEAD) - 2 * short, 4 * NT)
 
         def turn(s, done):
             i = len(hps)
             if ok(i) and 4 * i < quarters(s + 2) and 4 * (i - 1) <= done:
                 h_transpose(i)
 
+        def second(i):
+            mm2(i)
+            a_copy(i)
+            if i >= NT - HALVES:
+                store(i, 0)
+
         def step(s):
-            if 3 < s < NT + 2:
-                quant_step(s, 0 if s < NT else 256, 384)
+            if LAG + 1 < s:
+                quant_step(s, 0, 384)
             turn(s, quarters(s))
             if ok(len(xb)) and 4 * len(xb) < quarters(s + 3):
                 cast(len(xb), nc.scalar.copy)
-            if 3 < s < NT:
+            if LAG + 1 < s:
                 mm1(s)
                 c_copy(s)
-            if ok(s - 2):
-                mm2(s - 2)
-                a_copy(s - 2)
-                if s - 2 >= NT - HALVES:
-                    store(s - 2, 0)
+            second(s - LAG)
             q0, q1 = quarters(s), quarters(s + 1)
             for i in range(q0 // 4, -(-q1 // 4)):
                 h_scale_mul(i, max(q0 - 4 * i, 0), min(q1 - 4 * i, 4))
             turn(s, q1)
-            if ok(s - 3):
-                rope_k23(s - 3)
-                rope_k1(s - 3)
-                if s - 3 < NT - V_ADDS:
-                    finish(s - 3)
+            rope_k23(s - LAG - 1)
+            rope_k1(s - LAG - 1)
+            finish(s - LAG - 1)
 
         cast(0, nc.scalar.copy)
         h_transpose(0)
@@ -340,7 +350,7 @@ def tile_mla_pa_t_kernel(tc, h_bytes, h_scale, w_cq, w_q, w_qr, out):
         quant_step(0, 0, 256)
         quant(wcq_codes[:].rearrange("p g c -> p (g c)"), wcq_sc[:].rearrange("p g c -> p (g c)"),
               wcq_g[:].rearrange("p g c -> p (g c)"))
-        for i in (1, 2, 3):
+        for i in (1, 2, 3, 4):
             quant_step(i, 0, 256)
         tables_mix(nc.vector, 0, "mix0")
         quant(w2_codes[:, 0:256], w2_sc[:, 0:256], first_g[:])
@@ -366,15 +376,30 @@ def tile_mla_pa_t_kernel(tc, h_bytes, h_scale, w_cq, w_q, w_qr, out):
         h_scale_mul(8)
         c_copy(2)
         cast(10, nc.scalar.copy)
+        mm1(4)
         c_copy(3)
         quant(w2_codes[:, 256:768], w2_sc[:, 256:768], late_g[:].rearrange("p f c -> p (f c)"))
-        quant_step(2, 256, 384)
-        quant_step(3, 256, 384)
+        quant_step(LAG, 256, 384)
+        quant_step(LAG + 1, 256, 384)
         quant(w2_codes[:, 768:1024], w2_sc[:, 768:1024], last_g[:])
         tables_mix(nc.gpsimd, 1, "last")
         mm2(0)
+        c_copy(4)
         a_copy(0)
-        for s in range(3, NT + 3):
+        for s in range(LAG + 1, NT):
             step(s)
+        quant_step(NT, 128, 384)
+        second(NT - 3)
+        rope_k23(NT - 4)
+        second(NT - 2)
+        rope_k23(NT - 3)
+        rope_k1(NT - 3)
+        rope_k1(NT - 4)
+        finish(NT - 4)
+        quant_step(NT + 1, 256, 384)
+        second(NT - 1)
+        for i in (NT - 2, NT - 1):
+            rope_k23(i)
+            rope_k1(i)
         for i in range(NT - V_ADDS, NT):
             finish(i)

@@ -18,15 +18,13 @@ P = 128
 NT = B * S // P
 NC = NT // 4
 NP = DH // 2
-LEAD = 5
-LAG = 3
+LEAD = 6
+LAG = 2
 V_ADDS = 3
 WIDE = 44
-SINGLE = 8
 HALVES = 5
 U_FIRST = 3
-PERIOD = 4
-FIRST = 5
+FIRST = LAG + 7
 KINDS = 8
 
 FLOPS = 2 * B * S * (D * CQ + 2 * CQ * H * DH) + 3 * B * S * H * DH
@@ -167,7 +165,7 @@ def tile_mla_pa_t_kernel(tc, h_bytes, h_scale, w_cq, w_q, w_qr, out):
 
         def group(i):
             if i not in grp:
-                grp[i] = work.tile([P, D + CQ], BF16, name=f"g{i}", tag="g", bufs=LEAD + 5, align_bytes=64)
+                grp[i] = work.tile([P, D + CQ], BF16, name=f"g{i}", tag="g", bufs=LEAD + 4, align_bytes=64)
             return grp[i]
 
         def h_scale_mul(i, q0=0, q1=4):
@@ -195,7 +193,7 @@ def tile_mla_pa_t_kernel(tc, h_bytes, h_scale, w_cq, w_q, w_qr, out):
 
         def mm1(i):
             codes, sc = cq[i]
-            tag, bufs = ("m2", 5) if i in (0, 2, 4) else ("cp", 1)
+            tag, bufs = ("m2", 5) if i in (0, 2) else ("cp", 1)
             cp = psum.tile([P, 4, P], F32, name=f"cp{i}", tag=tag, bufs=bufs)
             for t in range(4):
                 for g in range(2):
@@ -209,15 +207,13 @@ def tile_mla_pa_t_kernel(tc, h_bytes, h_scale, w_cq, w_q, w_qr, out):
             cps[i] = cp
 
         def c_place(i):
-            if i < NT - LAG:
-                return i + LAG, 256
-            return (NT, 128) if i == NT - 3 else (i + 2, 256)
+            return i + LAG, 256
 
         def c_copy(i):
             nc.scalar.copy(out=group(c_place(i)[0])[:, 4 * c_place(i)[1] : 4 * c_place(i)[1] + CQ].rearrange("p (m e t) -> p m t e", e=2, t=4),
                            in_=cps[i][:].rearrange("p t (m e) -> p m t e", e=2))
 
-        def mm2(i):
+        def mm2(i, part):
             codes, sc = cq[c_place(i)[0]]
             cols = slice(c_place(i)[1], c_place(i)[1] + P)
 
@@ -230,14 +226,18 @@ def tile_mla_pa_t_kernel(tc, h_bytes, h_scale, w_cq, w_q, w_qr, out):
                 aps[i] = psum.tile([P, 512], F32, name=f"ap{i}", tag=tag, bufs=bufs)
                 mm(aps[i][:], 512, 1024, True, True)
 
-            if i < NT - U_FIRST:
+            if part == "sum":
+                if i % 2 == 0:
+                    sps[i // 2] = psum.tile([P, 2, 256], F32, name=f"sp{i}", tag="m2", bufs=5)
+                mm(sps[i // 2][:, i % 2, :], 0, 256, True, False)
+                mm(sps[i // 2][:, i % 2, :], 256, 512, False, True)
+                return
+            if part == "u":
+                ups[i] = psum.tile([P, 512], F32, name=f"up{i}", tag="m2", bufs=5)
+                mm(ups[i][:], 0, 512, True, True)
+            elif i < NT - U_FIRST:
                 mm_a("m2", 5)
-            sps[i] = psum.tile([P, 256], F32, name=f"sp{i}", tag="m2", bufs=5)
-            mm(sps[i][:], 0, 256, True, False)
-            mm(sps[i][:], 256, 512, False, True)
-            ups[i] = psum.tile([P, 512], F32, name=f"up{i}", tag="m2", bufs=5)
-            mm(ups[i][:], 0, 512, True, True)
-            if i >= NT - U_FIRST:
+            else:
                 mm_a("ht", 2)
 
         def result(i, part):
@@ -245,34 +245,35 @@ def tile_mla_pa_t_kernel(tc, h_bytes, h_scale, w_cq, w_q, w_qr, out):
                 if (i, part) not in osb:
                     osb[i, part] = keep.tile([P, H, DH], F32, name=f"last{i}_{part}", align_bytes=64)
                 return osb[i, part][:]
-            if i >= NT - SINGLE:
-                if (i, 0) not in osb:
-                    osb[i, 0] = keep.tile([P, H, 2 * DH], F32, name=f"single{i}", align_bytes=64)
-                return osb[i, 0][:, :, part * DH : (part + 1) * DH]
-            if i // 2 not in osb:
-                osb[i // 2] = work.tile([P, H, 2, 2 * DH], F32, name=f"o{i}", tag="o", bufs=4, align_bytes=64)
-            return osb[i // 2][:, :, i % 2, part * DH : (part + 1) * DH]
+            if (i, 0) not in osb:
+                osb[i, 0] = work.tile([P, H, 2 * DH], F32, name=f"o{i}", tag="o", bufs=8, align_bytes=64)
+            return osb[i, 0][:, :, part * DH : (part + 1) * DH]
 
         def a_copy(i):
             nc.scalar.copy(out=result(i, 0), in_=aps[i][:].rearrange("p (n d) -> p n d", n=H))
 
-        def rope_k23(i):
-            if i % 4 == 0:
+        def products(i):
+            if i // 4 not in prods:
                 prods[i // 4] = work.tile([P, 4 * 768], F32, name=f"prod{i}", tag="prod", bufs=2, align_bytes=64)
-            k23 = prods[i // 4][:, 768 * (i % 4) : 768 * (i % 4) + 512].rearrange("p (n i e) -> p n i e", n=H, e=2)
+            return prods[i // 4]
+
+        def rope_k23(i):
+            k23 = products(i)[:, 512 * (i % 4) : 512 * (i % 4 + 1)].rearrange("p (n i e) -> p n i e", n=H, e=2)
             kind = i % KINDS
-            nc.vector.tensor_tensor(
-                out=k23, in0=ups[i][:].rearrange("p (f n i) -> p n i f", f=2, n=H),
-                in1=mix[kind // 4][:, NP * (kind % 4) : NP * (kind % 4 + 1), :].unsqueeze(1).to_broadcast([P, H, NP, 2]), op=ALU.mult)
+            table = mix[kind // 4][:, NP * (kind % 4) : NP * (kind % 4 + 1), :]
+            nc.vector.tensor_tensor(out=k23, in0=ups[i][:].rearrange("p (f n i) -> p n i f", f=2, n=H),
+                                    in1=table.unsqueeze(1).to_broadcast([P, H, NP, 2]), op=ALU.mult)
             k23s[i] = k23
 
-        def rope_k1(i):
-            k1 = prods[i // 4][:, 768 * (i % 4) + 512 : 768 * (i % 4 + 1)].rearrange("p (n i) -> p n i", n=H)
+        def rope_k1(i, count):
+            first = 2048 + 256 * (i % 4)
+            k1 = products(i)[:, first : first + 256 * count].rearrange("p (j n i) -> p j n i", j=count, n=H)
             kind = i % KINDS
             nc.vector.tensor_tensor(
-                out=k1, in0=sps[i][:].rearrange("p (n i) -> p n i", n=H),
-                in1=cos[:, kind, :].unsqueeze(1).to_broadcast([P, H, NP]), op=ALU.mult)
-            k1s[i] = k1
+                out=k1, in0=sps[i // 2][:, i % 2 : i % 2 + count, :].rearrange("p j (n i) -> p j n i", n=H),
+                in1=cos[:, kind : kind + count, :].unsqueeze(2).to_broadcast([P, count, H, NP]), op=ALU.mult)
+            for j in range(count):
+                k1s[i + j] = k1[:, j]
 
         def rope_add(i):
             engine = nc.vector if i >= NT - V_ADDS else nc.gpsimd
@@ -286,11 +287,8 @@ def tile_mla_pa_t_kernel(tc, h_bytes, h_scale, w_cq, w_q, w_qr, out):
             rows = out[b, :, half * 512 : (half + 1) * 512, :].rearrange("n (p j) d -> p n j d", j=4)
             if i >= NT - HALVES:
                 nc.sync.dma_start(out=rows[:, :, i % 4, part * DH : (part + 1) * DH], in_=result(i, part))
-            elif i >= NT - SINGLE:
+            else:
                 nc.sync.dma_start(out=rows[:, :, i % 4, :], in_=osb[i, 0][:])
-            elif i % 2 == 1:
-                nc.sync.dma_start(out=rows[:, :, i % 4 - 1 : i % 4 + 1, :].rearrange("p n j d -> p n (j d)"),
-                                  in_=osb[i // 2][:].rearrange("p n j d -> p n (j d)"))
 
         def ok(i):
             return 0 <= i < NT
@@ -300,7 +298,7 @@ def tile_mla_pa_t_kernel(tc, h_bytes, h_scale, w_cq, w_q, w_qr, out):
             store(i, 1)
 
         def quarters(s):
-            short = sum(1 for r in range(FIRST, s) if (r - FIRST) % PERIOD < 2 and (r - FIRST) // PERIOD < LEAD - 1)
+            short = len([r for r in range(FIRST, s, 2)][: 2 * (LEAD - 1)])
             return min(4 * (s + LEAD) - 2 * short, 4 * NT)
 
         def turn(s, done):
@@ -309,7 +307,7 @@ def tile_mla_pa_t_kernel(tc, h_bytes, h_scale, w_cq, w_q, w_qr, out):
                 h_transpose(i)
 
         def second(i):
-            mm2(i)
+            mm2(i, "a")
             a_copy(i)
             if i >= NT - HALVES:
                 store(i, 0)
@@ -317,19 +315,26 @@ def tile_mla_pa_t_kernel(tc, h_bytes, h_scale, w_cq, w_q, w_qr, out):
         def step(s):
             if LAG + 1 < s:
                 quant_step(s, 0, 384)
+            if s > LAG + 1:
+                mm2(s - LAG, "sum")
             turn(s, quarters(s))
+            if s == NT - 1:
+                mm2(s - LAG, "u")
             if ok(len(xb)) and 4 * len(xb) < quarters(s + 3):
                 cast(len(xb), nc.scalar.copy)
             if LAG + 1 < s:
                 mm1(s)
                 c_copy(s)
             second(s - LAG)
+            if s < NT - 1:
+                mm2(s - LAG, "u")
             q0, q1 = quarters(s), quarters(s + 1)
             for i in range(q0 // 4, -(-q1 // 4)):
                 h_scale_mul(i, max(q0 - 4 * i, 0), min(q1 - 4 * i, 4))
             turn(s, q1)
             rope_k23(s - LAG - 1)
-            rope_k1(s - LAG - 1)
+            if (s - LAG - 1) % 2 == 0:
+                rope_k1(s - LAG - 1, 2)
             finish(s - LAG - 1)
 
         cast(0, nc.scalar.copy)
@@ -350,7 +355,7 @@ def tile_mla_pa_t_kernel(tc, h_bytes, h_scale, w_cq, w_q, w_qr, out):
         quant_step(0, 0, 256)
         quant(wcq_codes[:].rearrange("p g c -> p (g c)"), wcq_sc[:].rearrange("p g c -> p (g c)"),
               wcq_g[:].rearrange("p g c -> p (g c)"))
-        for i in (1, 2, 3, 4):
+        for i in (1, 2, 3):
             quant_step(i, 0, 256)
         tables_mix(nc.vector, 0, "mix0")
         quant(w2_codes[:, 0:256], w2_sc[:, 0:256], first_g[:])
@@ -376,30 +381,32 @@ def tile_mla_pa_t_kernel(tc, h_bytes, h_scale, w_cq, w_q, w_qr, out):
         h_scale_mul(8)
         c_copy(2)
         cast(10, nc.scalar.copy)
-        mm1(4)
         c_copy(3)
         quant(w2_codes[:, 256:768], w2_sc[:, 256:768], late_g[:].rearrange("p f c -> p (f c)"))
         quant_step(LAG, 256, 384)
         quant_step(LAG + 1, 256, 384)
         quant(w2_codes[:, 768:1024], w2_sc[:, 768:1024], last_g[:])
         tables_mix(nc.gpsimd, 1, "last")
-        mm2(0)
-        c_copy(4)
+        mm2(0, "sum")
+        mm2(1, "sum")
+        mm2(0, "a")
+        mm2(0, "u")
         a_copy(0)
         for s in range(LAG + 1, NT):
             step(s)
-        quant_step(NT, 128, 384)
-        second(NT - 3)
-        rope_k23(NT - 4)
+        quant_step(NT, 256, 384)
+        mm2(NT - 2, "u")
+        mm2(NT - 2, "sum")
         second(NT - 2)
         rope_k23(NT - 3)
-        rope_k1(NT - 3)
-        rope_k1(NT - 4)
-        finish(NT - 4)
+        rope_k23(NT - 2)
+        rope_k1(NT - 2, 1)
         quant_step(NT + 1, 256, 384)
+        finish(NT - 3)
+        finish(NT - 2)
+        mm2(NT - 1, "u")
+        mm2(NT - 1, "sum")
         second(NT - 1)
-        for i in (NT - 2, NT - 1):
-            rope_k23(i)
-            rope_k1(i)
-        for i in range(NT - V_ADDS, NT):
-            finish(i)
+        rope_k23(NT - 1)
+        rope_k1(NT - 1, 1)
+        finish(NT - 1)

@@ -18,13 +18,16 @@ P = 128
 NT = B * S // P
 NC = NT // 4
 NP = DH // 2
-LEAD = 6
+N1 = 6
+N2 = 4
+LEAD = N1 + N2 - 3
 LAG = 2
 V_ADDS = 3
-WIDE = 44
-HALVES = 5
+WIDE = 48
+VT = 1
+HALVES = 6
 U_FIRST = 3
-FIRST = LAG + 7
+FIRST = LAG + 3
 KINDS = 8
 
 FLOPS = 2 * B * S * (D * CQ + 2 * CQ * H * DH) + 3 * B * S * H * DH
@@ -56,8 +59,8 @@ def tile_mla_pa_t_kernel(tc, h_bytes, h_scale, w_cq, w_q, w_qr, out):
                               in_=w_cq[g * 512 : (g + 1) * 512, :].rearrange("(p j) c -> p j c", j=4))
 
         load_h(0, 0, 1)
-        load_wcq(0)
         load_h(0, 1, 2)
+        load_wcq(0)
         nc.sync.dma_start(out=scale[:], in_=h_scale.rearrange("a b (g p t) -> p (a b g) t", g=2, t=4))
         load_h(0, 2, 3)
         load_wcq(1)
@@ -82,28 +85,35 @@ def tile_mla_pa_t_kernel(tc, h_bytes, h_scale, w_cq, w_q, w_qr, out):
             nc.vector.tensor_scalar(out=dst, in0=one[:], scalar1=value, scalar2=None, op0=ALU.mult)
 
         th = keep.tile([P, NP], F32, name="th")
-        for a in range(4):
+        for a in range(NP - 4, NP):
             constant(th[:, a : a + 1], 10000.0 ** (-a / NP) / (2.0 * math.pi))
         hpi = keep.tile([P, 1], F32, name="hpi")
         constant(hpi[:], math.pi / 2)
-        for w in (4, 16):
+
+        def spread(w):
             for a in range(1, 4):
-                nc.vector.tensor_scalar(out=th[:, a * w : (a + 1) * w], in0=th[:, 0:w],
-                                        scalar1=10000.0 ** (-a * w / NP), scalar2=None, op0=ALU.mult)
+                nc.vector.tensor_scalar(out=th[:, NP - (a + 1) * w : NP - a * w], in0=th[:, NP - w : NP],
+                                        scalar1=10000.0 ** (a * w / NP), scalar2=None, op0=ALU.mult)
+
         turns = keep.tile([P, KINDS, WIDE], F32, name="turns", align_bytes=64)
-        whole = keep.tile([P, KINDS, WIDE], I32, name="whole", align_bytes=64)
+        whole = keep.tile([P, KINDS, WIDE], I32, name="whole", tag="wide", align_bytes=64)
         frac = keep.tile([P, KINDS, NP], F32, name="frac", align_bytes=64)
         fabs = keep.tile([P, KINDS, NP], F32, name="fabs", align_bytes=64)
         sines = keep.tile([P, 2, KINDS, NP], F32, name="sines", align_bytes=64)
         cos = keep.tile([P, KINDS, NP], F32, name="cos", align_bytes=64)
-        for dst, i0, i1 in ((frac[:, :, WIDE:NP], WIDE, NP), (turns[:], 0, WIDE)):
+
+        def angles(dst, i0, i1):
             nc.vector.tensor_tensor(out=dst, in0=pos[:].unsqueeze(2).to_broadcast([P, KINDS, i1 - i0]),
                                     in1=th[:, i0:i1].unsqueeze(1).to_broadcast([P, KINDS, i1 - i0]), op=ALU.mult)
-        nc.scalar.activation(out=sines[:, 1, :, WIDE:NP], in_=frac[:, :, WIDE:NP], func=ACT.Sin, scale=2.0 * math.pi)
+
+        spread(4)
         ident = keep.tile([P, P], F32, name="ident", align_bytes=64)
         nc.vector.tensor_scalar(out=ident[:], in0=offs[:], scalar1=0.0, scalar2=None, op0=ALU.is_equal)
+        angles(frac[:, :, WIDE:NP], WIDE, NP)
+        nc.scalar.activation(out=sines[:, 1, :, WIDE:NP], in_=frac[:, :, WIDE:NP], func=ACT.Sin, scale=2.0 * math.pi)
+        spread(16)
+        angles(turns[:], 0, WIDE)
         nc.vector.tensor_copy(out=whole[:], in_=turns[:])
-        nc.vector.tensor_tensor(out=frac[:, :, 0:WIDE], in0=turns[:], in1=whole[:], op=ALU.subtract)
 
         def tables_sin_cos():
             nc.scalar.activation(out=fabs[:], in_=frac[:], func=ACT.Abs)
@@ -121,20 +131,20 @@ def tile_mla_pa_t_kernel(tc, h_bytes, h_scale, w_cq, w_q, w_qr, out):
                 in1=cos[:, kinds, :].rearrange("p k i -> p (k i)").unsqueeze(2).to_broadcast([P, 4 * NP, 2]),
                 op=ALU.subtract)
 
-        wcq_codes = keep.tile([P, 2, CQ], U32, name="wcq_codes", align_bytes=64)
-        wcq_sc = keep.tile([P, 2, CQ], U8, name="wcq_sc", align_bytes=64)
+        wcq_codes = keep.tile([P, 2 * CQ], U32, name="wcq_codes", align_bytes=64)
+        wcq_sc = keep.tile([P, 2 * CQ], U8, name="wcq_sc", align_bytes=64)
         w2_codes = keep.tile([P, 1024], U32, name="w2_codes", align_bytes=64)
         w2_sc = keep.tile([P, 1024], U8, name="w2_sc", align_bytes=64)
-        wcq_g = keep.tile([P, 2, 4 * CQ], BF16, name="wcq_g", align_bytes=64)
+        wcq_v = keep.tile([P, VT * CQ], BF16, name="wcq_v", align_bytes=64)
         first_g = keep.tile([P, 1024], BF16, name="first_g", tag="late", align_bytes=64)
         last_g = keep.tile([P, 1024], BF16, name="last_g", tag="last", align_bytes=64)
 
         def pool_copy(out, in_):
             nc.gpsimd.tensor_scalar(out=out, in0=in_, scalar1=1.0, scalar2=0.0, op0=ALU.mult, op1=ALU.add)
 
-        def wcq_copy(copy, g):
-            copy(out=wcq_g[:, g, :].rearrange("p (t m j) -> p t m j", t=4, j=4),
-                 in_=wcq_raw[g][:].rearrange("p j (m t) -> p t m j", t=4))
+        def wcq_copy(copy, dst, g, t0, t1):
+            copy(out=dst.rearrange("p (t m j) -> p t m j", m=P, j=4),
+                 in_=wcq_raw[g][:].rearrange("p j (m t) -> p t m j", t=4)[:, t0:t1])
 
         def wqr_copy(copy, dst, f):
             copy(out=dst.rearrange("p (m j) -> p m j", j=4),
@@ -155,8 +165,7 @@ def tile_mla_pa_t_kernel(tc, h_bytes, h_scale, w_cq, w_q, w_qr, out):
             xb[i] = x
 
         def h_transpose(i):
-            tag, bufs = ("m2", 5) if i in (2, 6) else ("ht", 2)
-            ht = psum.tile([P, 2, 2, P], F32, name=f"ht{i}", tag=tag, bufs=bufs)
+            ht = psum.tile([P, 2, 2, P], F32, name=f"ht{i}", tag="ht", bufs=3)
             words = xb[i][:].bitcast(F32)
             for g in range(2):
                 for u in range(2):
@@ -193,15 +202,15 @@ def tile_mla_pa_t_kernel(tc, h_bytes, h_scale, w_cq, w_q, w_qr, out):
 
         def mm1(i):
             codes, sc = cq[i]
-            tag, bufs = ("m2", 5) if i in (0, 2) else ("cp", 1)
+            tag, bufs = ("u", 2) if i in (0, 2) else ("cp", 1)
             cp = psum.tile([P, 4, P], F32, name=f"cp{i}", tag=tag, bufs=bufs)
             for t in range(4):
                 for g in range(2):
                     cols = slice(g * P, (g + 1) * P)
                     nc.tensor.matmul_mx(
                         out=cp[:, t, :],
-                        lhsT=wcq_codes[:, g, t * P : (t + 1) * P].bitcast(FP8X4),
-                        lhsT_scale=wcq_sc[:, g, t * P : (t + 1) * P],
+                        lhsT=wcq_codes[:, (4 * g + t) * P : (4 * g + t + 1) * P].bitcast(FP8X4),
+                        lhsT_scale=wcq_sc[:, (4 * g + t) * P : (4 * g + t + 1) * P],
                         rhs=codes[:, cols].bitcast(FP8X4), rhs_scale=sc[:, cols],
                         start=(g == 0), stop=(g == 1))
             cps[i] = cp
@@ -228,17 +237,17 @@ def tile_mla_pa_t_kernel(tc, h_bytes, h_scale, w_cq, w_q, w_qr, out):
 
             if part == "sum":
                 if i % 2 == 0:
-                    sps[i // 2] = psum.tile([P, 2, 256], F32, name=f"sp{i}", tag="m2", bufs=5)
+                    sps[i // 2] = psum.tile([P, 2, 256], F32, name=f"sp{i}", tag="sum", bufs=1)
                 mm(sps[i // 2][:, i % 2, :], 0, 256, True, False)
                 mm(sps[i // 2][:, i % 2, :], 256, 512, False, True)
                 return
             if part == "u":
-                ups[i] = psum.tile([P, 512], F32, name=f"up{i}", tag="m2", bufs=5)
+                ups[i] = psum.tile([P, 512], F32, name=f"up{i}", tag="u", bufs=2)
                 mm(ups[i][:], 0, 512, True, True)
             elif i < NT - U_FIRST:
-                mm_a("m2", 5)
+                mm_a("a", 1)
             else:
-                mm_a("ht", 2)
+                mm_a("ht", 3)
 
         def result(i, part):
             if i >= NT - HALVES:
@@ -303,7 +312,7 @@ def tile_mla_pa_t_kernel(tc, h_bytes, h_scale, w_cq, w_q, w_qr, out):
 
         def turn(s, done):
             i = len(hps)
-            if ok(i) and 4 * i < quarters(s + 2) and 4 * (i - 1) <= done:
+            if ok(i) and 4 * i < quarters(s + 2) and 4 * (i - 2) <= done:
                 h_transpose(i)
 
         def second(i):
@@ -317,17 +326,17 @@ def tile_mla_pa_t_kernel(tc, h_bytes, h_scale, w_cq, w_q, w_qr, out):
                 quant_step(s, 0, 384)
             if s > LAG + 1:
                 mm2(s - LAG, "sum")
+            mm2(s - LAG, "u")
             turn(s, quarters(s))
-            if s == NT - 1:
-                mm2(s - LAG, "u")
             if ok(len(xb)) and 4 * len(xb) < quarters(s + 3):
                 cast(len(xb), nc.scalar.copy)
+            if s == NT - 1:
+                second(s - LAG)
             if LAG + 1 < s:
                 mm1(s)
                 c_copy(s)
-            second(s - LAG)
             if s < NT - 1:
-                mm2(s - LAG, "u")
+                second(s - LAG)
             q0, q1 = quarters(s), quarters(s + 1)
             for i in range(q0 // 4, -(-q1 // 4)):
                 h_scale_mul(i, max(q0 - 4 * i, 0), min(q1 - 4 * i, 4))
@@ -337,51 +346,47 @@ def tile_mla_pa_t_kernel(tc, h_bytes, h_scale, w_cq, w_q, w_qr, out):
                 rope_k1(s - LAG - 1, 2)
             finish(s - LAG - 1)
 
-        cast(0, nc.scalar.copy)
-        h_transpose(0)
-        cast(1, nc.scalar.copy)
-        wcq_copy(nc.vector.tensor_copy, 0)
-        wcq_copy(pool_copy, 1)
+        nc.vector.tensor_tensor(out=frac[:, :, 0:WIDE], in0=turns[:], in1=whole[:], op=ALU.subtract)
+        wcq_copy(nc.vector.tensor_copy, wcq_v[:], 0, 0, VT)
+        wcq_p = keep.tile([P, (8 - VT) * CQ], BF16, name="wcq_p", tag="wide", align_bytes=64)
+        rest = (4 - VT) * CQ
+        wcq_copy(pool_copy, wcq_p[:, 0:rest], 0, VT, 4)
+        wcq_copy(pool_copy, wcq_p[:, rest:], 1, 0, 4)
         wqr_copy(pool_copy, first_g[:], 0)
-        h_transpose(1)
-        h_scale_mul(0)
-        for i in range(2, 6):
+        for i in range(2):
             cast(i, nc.scalar.copy)
             h_transpose(i)
-            h_scale_mul(i - 1)
-        cast(6, nc.scalar.copy)
-        h_transpose(6)
+        for i in range(N1):
+            cast(i + 2, nc.scalar.copy)
+            h_transpose(i + 2)
+            h_scale_mul(i)
         tables_sin_cos()
         quant_step(0, 0, 256)
-        quant(wcq_codes[:].rearrange("p g c -> p (g c)"), wcq_sc[:].rearrange("p g c -> p (g c)"),
-              wcq_g[:].rearrange("p g c -> p (g c)"))
+        quant(wcq_codes[:, 0 : VT * P], wcq_sc[:, 0 : VT * P], wcq_v[:])
+        quant(wcq_codes[:, VT * P : CQ], wcq_sc[:, VT * P : CQ], wcq_p[:, 0:rest])
+        quant(wcq_codes[:, CQ:], wcq_sc[:, CQ:], wcq_p[:, rest:])
         for i in (1, 2, 3):
             quant_step(i, 0, 256)
-        tables_mix(nc.vector, 0, "mix0")
         quant(w2_codes[:, 0:256], w2_sc[:, 0:256], first_g[:])
         late_g = keep.tile([P, 2, 1024], BF16, name="late_g", tag="late", align_bytes=64)
         wqr_copy(pool_copy, late_g[:, 0, :], 1)
         wq_copy(pool_copy, late_g[:, 1, :], 0)
-        cast(7, nc.scalar.copy)
-        h_scale_mul(5)
-        mm1(0)
-        h_transpose(7)
-        mm1(1)
-        cast(8, nc.scalar.copy)
-        h_scale_mul(6)
-        c_copy(0)
-        h_transpose(8)
-        mm1(2)
-        cast(9, nc.scalar.copy)
-        h_scale_mul(7)
-        c_copy(1)
-        h_transpose(9)
-        mm1(3)
-        wq_copy(nc.scalar.copy, last_g[:], 1)
-        h_scale_mul(8)
-        c_copy(2)
-        cast(10, nc.scalar.copy)
-        c_copy(3)
+        tables_mix(nc.gpsimd, 0, "mix0")
+        for k in range(N2):
+            if k < N2 - 1:
+                cast(N1 + k + 2, nc.scalar.copy)
+            else:
+                wq_copy(nc.scalar.copy, last_g[:], 1)
+            if 1 <= k:
+                c_copy(k - 1)
+            if k < 4:
+                mm1(k)
+            if k < N2 - 1:
+                h_transpose(N1 + k + 2)
+            h_scale_mul(N1 + k)
+        cast(N1 + N2 + 1, nc.scalar.copy)
+        if N2 == 4:
+            c_copy(3)
         quant(w2_codes[:, 256:768], w2_sc[:, 256:768], late_g[:].rearrange("p f c -> p (f c)"))
         quant_step(LAG, 256, 384)
         quant_step(LAG + 1, 256, 384)
@@ -389,8 +394,8 @@ def tile_mla_pa_t_kernel(tc, h_bytes, h_scale, w_cq, w_q, w_qr, out):
         tables_mix(nc.gpsimd, 1, "last")
         mm2(0, "sum")
         mm2(1, "sum")
-        mm2(0, "a")
         mm2(0, "u")
+        mm2(0, "a")
         a_copy(0)
         for s in range(LAG + 1, NT):
             step(s)

@@ -18,16 +18,19 @@ P = 128
 NT = B * S // P
 NC = NT // 4
 NP = DH // 2
-N1 = 6
+N1 = 5
 N2 = 4
 LEAD = N1 + N2 - 3
 LAG = 2
 V_ADDS = 3
 WIDE = 48
-VT = 1
-HALVES = 6
+VT = 3
+RUN = 1
+SINGLE = 8
+CUTS = (0, 1, 3, 6, 8)
 U_FIRST = 3
-FIRST = LAG + 3
+FIRST = 6
+PERIOD = 4
 KINDS = 8
 
 FLOPS = 2 * B * S * (D * CQ + 2 * CQ * H * DH) + 3 * B * S * H * DH
@@ -157,10 +160,10 @@ def tile_mla_pa_t_kernel(tc, h_bytes, h_scale, w_cq, w_q, w_qr, out):
         def quant(codes, sc, grouped):
             nc.vector.quantize_mx(out=codes.bitcast(FP8X4), scales=sc, in_=grouped)
 
-        xb, hps, grp, cq, cps, ups, aps, sps, k1s, k23s, osb, prods = ({} for k in range(12))
+        xb, hps, grp, cq, cps, ups, aps, sps, k1s, k23s, osb, prods, written = ({} for k in range(13))
 
         def cast(i, copy):
-            x = work.tile([P, D], BF16, name=f"x{i}", tag="x", align_bytes=64)
+            x = work.tile([P, D], BF16, name=f"x{i}", tag="x", bufs=4, align_bytes=64)
             copy(out=x[:], in_=hb[i // 4][:, i % 4, :].bitcast(E4M3))
             xb[i] = x
 
@@ -202,7 +205,7 @@ def tile_mla_pa_t_kernel(tc, h_bytes, h_scale, w_cq, w_q, w_qr, out):
 
         def mm1(i):
             codes, sc = cq[i]
-            tag, bufs = ("u", 2) if i in (0, 2) else ("cp", 1)
+            tag, bufs = ("m2", 4) if i in (0, 2) else ("cp", 1)
             cp = psum.tile([P, 4, P], F32, name=f"cp{i}", tag=tag, bufs=bufs)
             for t in range(4):
                 for g in range(2):
@@ -236,27 +239,37 @@ def tile_mla_pa_t_kernel(tc, h_bytes, h_scale, w_cq, w_q, w_qr, out):
                 mm(aps[i][:], 512, 1024, True, True)
 
             if part == "sum":
-                if i % 2 == 0:
-                    sps[i // 2] = psum.tile([P, 2, 256], F32, name=f"sp{i}", tag="sum", bufs=1)
-                mm(sps[i // 2][:, i % 2, :], 0, 256, True, False)
-                mm(sps[i // 2][:, i % 2, :], 256, 512, False, True)
+                sps[i] = psum.tile([P, 256], F32, name=f"sp{i}", tag="m2", bufs=4)
+                mm(sps[i][:], 0, 256, True, False)
+                mm(sps[i][:], 256, 512, False, True)
                 return
             if part == "u":
-                ups[i] = psum.tile([P, 512], F32, name=f"up{i}", tag="u", bufs=2)
+                ups[i] = psum.tile([P, 512], F32, name=f"up{i}", tag="m2", bufs=4)
                 mm(ups[i][:], 0, 512, True, True)
             elif i < NT - U_FIRST:
-                mm_a("a", 1)
+                mm_a("m2", 4)
             else:
                 mm_a("ht", 3)
 
+        def piece(i, part):
+            n = 2 * (i % 4) + part
+            if i < NT - SINGLE:
+                return n // 4 * 4, 4
+            if i < NT - 4:
+                return n // 2 * 2, 2
+            first = max(cut for cut in CUTS if cut <= n)
+            return first, CUTS[CUTS.index(first) + 1] - first
+
         def result(i, part):
-            if i >= NT - HALVES:
-                if (i, part) not in osb:
-                    osb[i, part] = keep.tile([P, H, DH], F32, name=f"last{i}_{part}", align_bytes=64)
-                return osb[i, part][:]
-            if (i, 0) not in osb:
-                osb[i, 0] = work.tile([P, H, 2 * DH], F32, name=f"o{i}", tag="o", bufs=8, align_bytes=64)
-            return osb[i, 0][:, :, part * DH : (part + 1) * DH]
+            first, count = piece(i, part)
+            key = (i // 4, first)
+            if key not in osb:
+                if i < NT - SINGLE:
+                    osb[key] = work.tile([P, H, count * DH], F32, name=f"o{i}", tag="o", bufs=4, align_bytes=64)
+                else:
+                    osb[key] = keep.tile([P, H, count * DH], F32, name=f"last{i}_{part}", align_bytes=64)
+            n = 2 * (i % 4) + part - first
+            return osb[key][:, :, n * DH : (n + 1) * DH]
 
         def a_copy(i):
             nc.scalar.copy(out=result(i, 0), in_=aps[i][:].rearrange("p (n d) -> p n d", n=H))
@@ -274,15 +287,12 @@ def tile_mla_pa_t_kernel(tc, h_bytes, h_scale, w_cq, w_q, w_qr, out):
                                     in1=table.unsqueeze(1).to_broadcast([P, H, NP, 2]), op=ALU.mult)
             k23s[i] = k23
 
-        def rope_k1(i, count):
+        def rope_k1(i):
             first = 2048 + 256 * (i % 4)
-            k1 = products(i)[:, first : first + 256 * count].rearrange("p (j n i) -> p j n i", j=count, n=H)
-            kind = i % KINDS
-            nc.vector.tensor_tensor(
-                out=k1, in0=sps[i // 2][:, i % 2 : i % 2 + count, :].rearrange("p j (n i) -> p j n i", n=H),
-                in1=cos[:, kind : kind + count, :].unsqueeze(2).to_broadcast([P, count, H, NP]), op=ALU.mult)
-            for j in range(count):
-                k1s[i + j] = k1[:, j]
+            k1 = products(i)[:, first : first + 256].rearrange("p (n i) -> p n i", n=H)
+            nc.vector.tensor_tensor(out=k1, in0=sps[i][:].rearrange("p (n i) -> p n i", n=H),
+                                    in1=cos[:, i % KINDS, :].unsqueeze(1).to_broadcast([P, H, NP]), op=ALU.mult)
+            k1s[i] = k1
 
         def rope_add(i):
             engine = nc.vector if i >= NT - V_ADDS else nc.gpsimd
@@ -291,13 +301,13 @@ def tile_mla_pa_t_kernel(tc, h_bytes, h_scale, w_cq, w_q, w_qr, out):
                 in0=k23s[i], in1=k1s[i].unsqueeze(3).to_broadcast([P, H, NP, 2]), op=ALU.add)
 
         def store(i, part):
-            c = i // 4
-            b, half = c // 2, c % 2
-            rows = out[b, :, half * 512 : (half + 1) * 512, :].rearrange("n (p j) d -> p n j d", j=4)
-            if i >= NT - HALVES:
-                nc.sync.dma_start(out=rows[:, :, i % 4, part * DH : (part + 1) * DH], in_=result(i, part))
-            else:
-                nc.sync.dma_start(out=rows[:, :, i % 4, :], in_=osb[i, 0][:])
+            first, count = piece(i, part)
+            key = (i // 4, first)
+            written[key] = written.get(key, 0) + 1
+            if written[key] == count:
+                b, half = i // 8, i // 4 % 2
+                rows = out[b, :, half * 512 : (half + 1) * 512, :].rearrange("n (p j) d -> p n (j d)", j=4)
+                nc.sync.dma_start(out=rows[:, :, first * DH : (first + count) * DH], in_=osb[key][:])
 
         def ok(i):
             return 0 <= i < NT
@@ -307,43 +317,41 @@ def tile_mla_pa_t_kernel(tc, h_bytes, h_scale, w_cq, w_q, w_qr, out):
             store(i, 1)
 
         def quarters(s):
-            short = len([r for r in range(FIRST, s, 2)][: 2 * (LEAD - 1)])
+            short = len([r for r in range(FIRST, s) if (r - FIRST) % PERIOD < 2][: 2 * (LEAD - 1)])
             return min(4 * (s + LEAD) - 2 * short, 4 * NT)
 
         def turn(s, done):
-            i = len(hps)
-            if ok(i) and 4 * i < quarters(s + 2) and 4 * (i - 2) <= done:
-                h_transpose(i)
+            ahead = 3 if s % 2 == RUN else 2
+            while ok(len(hps)) and 4 * len(hps) < quarters(s + ahead) and 4 * (len(hps) - 2) <= done:
+                h_transpose(len(hps))
 
         def second(i):
             mm2(i, "a")
             a_copy(i)
-            if i >= NT - HALVES:
-                store(i, 0)
+            store(i, 0)
 
         def step(s):
             if LAG + 1 < s:
                 quant_step(s, 0, 384)
-            if s > LAG + 1:
-                mm2(s - LAG, "sum")
-            mm2(s - LAG, "u")
+            mm2(s - LAG - 1, "sum")
             turn(s, quarters(s))
-            if ok(len(xb)) and 4 * len(xb) < quarters(s + 3):
+            if ok(len(xb)) and 4 * len(xb) < quarters(s + 4):
                 cast(len(xb), nc.scalar.copy)
             if s == NT - 1:
+                mm2(s - LAG, "u")
                 second(s - LAG)
             if LAG + 1 < s:
                 mm1(s)
                 c_copy(s)
             if s < NT - 1:
                 second(s - LAG)
+                mm2(s - LAG, "u")
             q0, q1 = quarters(s), quarters(s + 1)
             for i in range(q0 // 4, -(-q1 // 4)):
                 h_scale_mul(i, max(q0 - 4 * i, 0), min(q1 - 4 * i, 4))
             turn(s, q1)
             rope_k23(s - LAG - 1)
-            if (s - LAG - 1) % 2 == 0:
-                rope_k1(s - LAG - 1, 2)
+            rope_k1(s - LAG - 1)
             finish(s - LAG - 1)
 
         nc.vector.tensor_tensor(out=frac[:, :, 0:WIDE], in0=turns[:], in1=whole[:], op=ALU.subtract)
@@ -371,7 +379,6 @@ def tile_mla_pa_t_kernel(tc, h_bytes, h_scale, w_cq, w_q, w_qr, out):
         late_g = keep.tile([P, 2, 1024], BF16, name="late_g", tag="late", align_bytes=64)
         wqr_copy(pool_copy, late_g[:, 0, :], 1)
         wq_copy(pool_copy, late_g[:, 1, :], 0)
-        tables_mix(nc.gpsimd, 0, "mix0")
         for k in range(N2):
             if k < N2 - 1:
                 cast(N1 + k + 2, nc.scalar.copy)
@@ -385,27 +392,29 @@ def tile_mla_pa_t_kernel(tc, h_bytes, h_scale, w_cq, w_q, w_qr, out):
                 h_transpose(N1 + k + 2)
             h_scale_mul(N1 + k)
         cast(N1 + N2 + 1, nc.scalar.copy)
-        if N2 == 4:
-            c_copy(3)
+        c_copy(3)
+        cast(N1 + N2 + 2, nc.scalar.copy)
         quant(w2_codes[:, 256:768], w2_sc[:, 256:768], late_g[:].rearrange("p f c -> p (f c)"))
+        tables_mix(nc.vector, 0, "mix0")
         quant_step(LAG, 256, 384)
         quant_step(LAG + 1, 256, 384)
         quant(w2_codes[:, 768:1024], w2_sc[:, 768:1024], last_g[:])
         tables_mix(nc.gpsimd, 1, "last")
-        mm2(0, "sum")
-        mm2(1, "sum")
-        mm2(0, "u")
         mm2(0, "a")
+        mm2(0, "u")
         a_copy(0)
+        store(0, 0)
         for s in range(LAG + 1, NT):
             step(s)
         quant_step(NT, 256, 384)
+        mm2(NT - 3, "sum")
         mm2(NT - 2, "u")
-        mm2(NT - 2, "sum")
         second(NT - 2)
         rope_k23(NT - 3)
+        rope_k1(NT - 3)
+        mm2(NT - 2, "sum")
         rope_k23(NT - 2)
-        rope_k1(NT - 2, 1)
+        rope_k1(NT - 2)
         quant_step(NT + 1, 256, 384)
         finish(NT - 3)
         finish(NT - 2)
@@ -413,5 +422,5 @@ def tile_mla_pa_t_kernel(tc, h_bytes, h_scale, w_cq, w_q, w_qr, out):
         mm2(NT - 1, "sum")
         second(NT - 1)
         rope_k23(NT - 1)
-        rope_k1(NT - 1, 1)
+        rope_k1(NT - 1)
         finish(NT - 1)

@@ -19,18 +19,16 @@ NT = B * S // P
 NC = NT // 4
 NP = DH // 2
 N1 = 5
-N2 = 4
+N2 = 3
 LEAD = N1 + N2 - 3
 LAG = 2
 V_ADDS = 3
 WIDE = 48
-VT = 3
 RUN = 1
-SINGLE = 8
-CUTS = (0, 1, 3, 6, 8)
+CUTS = (0, 1, 3, 5, 7, 9, 11, 14, 16)
 U_FIRST = 3
-FIRST = 6
-PERIOD = 4
+FIRST = 4
+PERIOD = 8
 KINDS = 8
 
 FLOPS = 2 * B * S * (D * CQ + 2 * CQ * H * DH) + 3 * B * S * H * DH
@@ -47,10 +45,9 @@ def tile_mla_pa_t_kernel(tc, h_bytes, h_scale, w_cq, w_q, w_qr, out):
         hb = [keep.tile([P, 4, D], U8, name=f"hb{c}", align_bytes=64) for c in range(NC)]
 
         def load_h(c, j0, j1):
-            b, half = c // 2, c % 2
-            nc.sync.dma_start(
-                out=hb[c][:, j0:j1, :],
-                in_=h_bytes[b, half * 512 : (half + 1) * 512, :].rearrange("(p j) k -> p j k", j=4)[:, j0:j1, :])
+            first = 4 * (c % 2)
+            nc.sync.dma_start(out=hb[c][:, j0:j1, :],
+                              in_=h_bytes[c // 2].rearrange("(p j) k -> p j k", j=KINDS)[:, first + j0 : first + j1, :])
 
         scale = keep.tile([P, 2, 4], F32, name="scale")
         wcq_raw = [keep.tile([P, 4, CQ], BF16, name=f"wcq_raw{g}", align_bytes=64) for g in range(2)]
@@ -76,8 +73,8 @@ def tile_mla_pa_t_kernel(tc, h_bytes, h_scale, w_cq, w_q, w_qr, out):
             load_h(c, 0, 4)
 
         pos = keep.tile([P, KINDS], F32, name="pos")
-        nc.gpsimd.iota(pos[:].rearrange("p (c j) -> p c j", c=2), pattern=[[512, 2], [1, 4]],
-                       base=0, channel_multiplier=4, allow_small_or_imprecise_dtypes=True)
+        nc.gpsimd.iota(pos[:], pattern=[[1, KINDS]], base=0, channel_multiplier=KINDS,
+                       allow_small_or_imprecise_dtypes=True)
         offs = keep.tile([P, P], F32, name="offs", align_bytes=64)
         nc.gpsimd.iota(offs[:], pattern=[[1, P]], base=0, channel_multiplier=-1,
                        allow_small_or_imprecise_dtypes=True)
@@ -99,24 +96,30 @@ def tile_mla_pa_t_kernel(tc, h_bytes, h_scale, w_cq, w_q, w_qr, out):
                                         scalar1=10000.0 ** (a * w / NP), scalar2=None, op0=ALU.mult)
 
         turns = keep.tile([P, KINDS, WIDE], F32, name="turns", align_bytes=64)
-        whole = keep.tile([P, KINDS, WIDE], I32, name="whole", tag="wide", align_bytes=64)
+        whole = keep.tile([P, KINDS, WIDE], I32, name="whole", align_bytes=64)
         frac = keep.tile([P, KINDS, NP], F32, name="frac", align_bytes=64)
         fabs = keep.tile([P, KINDS, NP], F32, name="fabs", align_bytes=64)
         sines = keep.tile([P, 2, KINDS, NP], F32, name="sines", align_bytes=64)
         cos = keep.tile([P, KINDS, NP], F32, name="cos", align_bytes=64)
 
-        def angles(dst, i0, i1):
-            nc.vector.tensor_tensor(out=dst, in0=pos[:].unsqueeze(2).to_broadcast([P, KINDS, i1 - i0]),
-                                    in1=th[:, i0:i1].unsqueeze(1).to_broadcast([P, KINDS, i1 - i0]), op=ALU.mult)
+        def angles(dst, k0, k1, i0, i1):
+            shape = [P, k1 - k0, i1 - i0]
+            nc.vector.tensor_tensor(out=dst, in0=pos[:, k0:k1].unsqueeze(2).to_broadcast(shape),
+                                    in1=th[:, i0:i1].unsqueeze(1).to_broadcast(shape), op=ALU.mult)
 
         spread(4)
         ident = keep.tile([P, P], F32, name="ident", align_bytes=64)
         nc.vector.tensor_scalar(out=ident[:], in0=offs[:], scalar1=0.0, scalar2=None, op0=ALU.is_equal)
-        angles(frac[:, :, WIDE:NP], WIDE, NP)
+        angles(frac[:, :, WIDE:NP], 0, KINDS, WIDE, NP)
         nc.scalar.activation(out=sines[:, 1, :, WIDE:NP], in_=frac[:, :, WIDE:NP], func=ACT.Sin, scale=2.0 * math.pi)
         spread(16)
-        angles(turns[:], 0, WIDE)
-        nc.vector.tensor_copy(out=whole[:], in_=turns[:])
+        halves = [slice(0, 4), slice(4, KINDS)]
+        for ks in halves:
+            angles(turns[:, ks], ks.start, ks.stop, 0, WIDE)
+        for ks in halves:
+            nc.vector.tensor_copy(out=whole[:, ks], in_=turns[:, ks])
+        for ks in halves:
+            nc.vector.tensor_tensor(out=frac[:, ks, 0:WIDE], in0=turns[:, ks], in1=whole[:, ks], op=ALU.subtract)
 
         def tables_sin_cos():
             nc.scalar.activation(out=fabs[:], in_=frac[:], func=ACT.Abs)
@@ -138,24 +141,23 @@ def tile_mla_pa_t_kernel(tc, h_bytes, h_scale, w_cq, w_q, w_qr, out):
         wcq_sc = keep.tile([P, 2 * CQ], U8, name="wcq_sc", align_bytes=64)
         w2_codes = keep.tile([P, 1024], U32, name="w2_codes", align_bytes=64)
         w2_sc = keep.tile([P, 1024], U8, name="w2_sc", align_bytes=64)
-        wcq_v = keep.tile([P, VT * CQ], BF16, name="wcq_v", align_bytes=64)
+        wcq_g = keep.tile([P, 8 * CQ], BF16, name="wcq_g", align_bytes=64)
         first_g = keep.tile([P, 1024], BF16, name="first_g", tag="late", align_bytes=64)
-        last_g = keep.tile([P, 1024], BF16, name="last_g", tag="last", align_bytes=64)
+        last_g = keep.tile([P, 1536], BF16, name="last_g", tag="last", align_bytes=64)
 
         def pool_copy(out, in_):
             nc.gpsimd.tensor_scalar(out=out, in0=in_, scalar1=1.0, scalar2=0.0, op0=ALU.mult, op1=ALU.add)
 
-        def wcq_copy(copy, dst, g, t0, t1):
-            copy(out=dst.rearrange("p (t m j) -> p t m j", m=P, j=4),
-                 in_=wcq_raw[g][:].rearrange("p j (m t) -> p t m j", t=4)[:, t0:t1])
+        def wcq_copy(copy, g):
+            copy(out=wcq_g[:, 4 * CQ * g : 4 * CQ * (g + 1)].rearrange("p (t m j) -> p t m j", m=P, j=4),
+                 in_=wcq_raw[g][:].rearrange("p j (m t) -> p t m j", t=4))
 
         def wqr_copy(copy, dst, f):
             copy(out=dst.rearrange("p (m j) -> p m j", j=4),
                  in_=wqr_raw[:].rearrange("p j (m e) -> p e m j", e=2)[:, 1 - f])
 
-        def wq_copy(copy, dst, f):
-            copy(out=dst.rearrange("p (n j) -> p n j", j=4),
-                 in_=wq_raw[:, :, 256 * f : 256 * (f + 1)].rearrange("p j n -> p n j"))
+        def wq_copy(copy, dst, n0, n1):
+            copy(out=dst.rearrange("p (n j) -> p n j", j=4), in_=wq_raw[:, :, n0:n1].rearrange("p j n -> p n j"))
 
         def quant(codes, sc, grouped):
             nc.vector.quantize_mx(out=codes.bitcast(FP8X4), scales=sc, in_=grouped)
@@ -246,29 +248,28 @@ def tile_mla_pa_t_kernel(tc, h_bytes, h_scale, w_cq, w_q, w_qr, out):
             if part == "u":
                 ups[i] = psum.tile([P, 512], F32, name=f"up{i}", tag="m2", bufs=4)
                 mm(ups[i][:], 0, 512, True, True)
+            elif i == 0:
+                mm_a("cp", 1)
             elif i < NT - U_FIRST:
                 mm_a("m2", 4)
             else:
                 mm_a("ht", 3)
 
         def piece(i, part):
-            n = 2 * (i % 4) + part
-            if i < NT - SINGLE:
-                return n // 4 * 4, 4
-            if i < NT - 4:
-                return n // 2 * 2, 2
-            first = max(cut for cut in CUTS if cut <= n)
-            return first, CUTS[CUTS.index(first) + 1] - first
+            n = 2 * (i % KINDS) + part
+            cuts = CUTS if i >= NT - KINDS else range(0, 2 * KINDS + 1, 4)
+            first = max(cut for cut in cuts if cut <= n)
+            return first, cuts[cuts.index(first) + 1] - first
 
         def result(i, part):
             first, count = piece(i, part)
-            key = (i // 4, first)
+            key = (i // KINDS, first)
             if key not in osb:
-                if i < NT - SINGLE:
+                if i < NT - KINDS:
                     osb[key] = work.tile([P, H, count * DH], F32, name=f"o{i}", tag="o", bufs=4, align_bytes=64)
                 else:
                     osb[key] = keep.tile([P, H, count * DH], F32, name=f"last{i}_{part}", align_bytes=64)
-            n = 2 * (i % 4) + part - first
+            n = 2 * (i % KINDS) + part - first
             return osb[key][:, :, n * DH : (n + 1) * DH]
 
         def a_copy(i):
@@ -302,11 +303,10 @@ def tile_mla_pa_t_kernel(tc, h_bytes, h_scale, w_cq, w_q, w_qr, out):
 
         def store(i, part):
             first, count = piece(i, part)
-            key = (i // 4, first)
+            key = (i // KINDS, first)
             written[key] = written.get(key, 0) + 1
             if written[key] == count:
-                b, half = i // 8, i // 4 % 2
-                rows = out[b, :, half * 512 : (half + 1) * 512, :].rearrange("n (p j) d -> p n (j d)", j=4)
+                rows = out[i // KINDS].rearrange("n (p j) d -> p n (j d)", j=KINDS)
                 nc.sync.dma_start(out=rows[:, :, first * DH : (first + count) * DH], in_=osb[key][:])
 
         def ok(i):
@@ -333,7 +333,8 @@ def tile_mla_pa_t_kernel(tc, h_bytes, h_scale, w_cq, w_q, w_qr, out):
         def step(s):
             if LAG + 1 < s:
                 quant_step(s, 0, 384)
-            mm2(s - LAG - 1, "sum")
+            if s > LAG + 1:
+                mm2(s - LAG - 1, "sum")
             turn(s, quarters(s))
             if ok(len(xb)) and 4 * len(xb) < quarters(s + 4):
                 cast(len(xb), nc.scalar.copy)
@@ -354,12 +355,8 @@ def tile_mla_pa_t_kernel(tc, h_bytes, h_scale, w_cq, w_q, w_qr, out):
             rope_k1(s - LAG - 1)
             finish(s - LAG - 1)
 
-        nc.vector.tensor_tensor(out=frac[:, :, 0:WIDE], in0=turns[:], in1=whole[:], op=ALU.subtract)
-        wcq_copy(nc.vector.tensor_copy, wcq_v[:], 0, 0, VT)
-        wcq_p = keep.tile([P, (8 - VT) * CQ], BF16, name="wcq_p", tag="wide", align_bytes=64)
-        rest = (4 - VT) * CQ
-        wcq_copy(pool_copy, wcq_p[:, 0:rest], 0, VT, 4)
-        wcq_copy(pool_copy, wcq_p[:, rest:], 1, 0, 4)
+        wcq_copy(nc.vector.tensor_copy, 0)
+        wcq_copy(pool_copy, 1)
         wqr_copy(pool_copy, first_g[:], 0)
         for i in range(2):
             cast(i, nc.scalar.copy)
@@ -370,20 +367,19 @@ def tile_mla_pa_t_kernel(tc, h_bytes, h_scale, w_cq, w_q, w_qr, out):
             h_scale_mul(i)
         tables_sin_cos()
         quant_step(0, 0, 256)
-        quant(wcq_codes[:, 0 : VT * P], wcq_sc[:, 0 : VT * P], wcq_v[:])
-        quant(wcq_codes[:, VT * P : CQ], wcq_sc[:, VT * P : CQ], wcq_p[:, 0:rest])
-        quant(wcq_codes[:, CQ:], wcq_sc[:, CQ:], wcq_p[:, rest:])
+        quant(wcq_codes[:], wcq_sc[:], wcq_g[:])
         for i in (1, 2, 3):
             quant_step(i, 0, 256)
+        wq_copy(nc.vector.tensor_copy, last_g[:, 0:512], 128, 256)
         quant(w2_codes[:, 0:256], w2_sc[:, 0:256], first_g[:])
-        late_g = keep.tile([P, 2, 1024], BF16, name="late_g", tag="late", align_bytes=64)
-        wqr_copy(pool_copy, late_g[:, 0, :], 1)
-        wq_copy(pool_copy, late_g[:, 1, :], 0)
+        late_g = keep.tile([P, 1536], BF16, name="late_g", tag="late", align_bytes=64)
+        wqr_copy(pool_copy, late_g[:, 0:1024], 1)
+        wq_copy(pool_copy, late_g[:, 1024:1536], 0, 128)
         for k in range(N2):
             if k < N2 - 1:
                 cast(N1 + k + 2, nc.scalar.copy)
             else:
-                wq_copy(nc.scalar.copy, last_g[:], 1)
+                wq_copy(nc.scalar.copy, last_g[:, 512:1536], 256, 512)
             if 1 <= k:
                 c_copy(k - 1)
             if k < 4:
@@ -391,19 +387,21 @@ def tile_mla_pa_t_kernel(tc, h_bytes, h_scale, w_cq, w_q, w_qr, out):
             if k < N2 - 1:
                 h_transpose(N1 + k + 2)
             h_scale_mul(N1 + k)
+        for k in range(N2, 4):
+            mm1(k)
+            c_copy(k - 1)
         cast(N1 + N2 + 1, nc.scalar.copy)
         c_copy(3)
         cast(N1 + N2 + 2, nc.scalar.copy)
-        quant(w2_codes[:, 256:768], w2_sc[:, 256:768], late_g[:].rearrange("p f c -> p (f c)"))
-        tables_mix(nc.vector, 0, "mix0")
+        quant(w2_codes[:, 256:640], w2_sc[:, 256:640], late_g[:])
         quant_step(LAG, 256, 384)
         quant_step(LAG + 1, 256, 384)
-        quant(w2_codes[:, 768:1024], w2_sc[:, 768:1024], last_g[:])
+        tables_mix(nc.vector, 0, "mix0")
+        quant(w2_codes[:, 640:1024], w2_sc[:, 640:1024], last_g[:])
         tables_mix(nc.gpsimd, 1, "last")
-        mm2(0, "a")
         mm2(0, "u")
-        a_copy(0)
-        store(0, 0)
+        mm2(0, "sum")
+        second(0)
         for s in range(LAG + 1, NT):
             step(s)
         quant_step(NT, 256, 384)

@@ -16,20 +16,13 @@ ACT = mybir.ActivationFunctionType
 B, S, D, H, DH, CQ = 4, 1024, 1024, 4, 128, 512
 P = 128
 NT = B * S // P
-NC = NT // 4
+NW = NT // 2
 NP = DH // 2
-N1 = 5
-N2 = 3
-LEAD = N1 + N2 - 3
-LAG = 2
-V_ADDS = 3
-WIDE = 48
-RUN = 1
-CUTS = (0, 1, 3, 5, 7, 9, 11, 14, 16)
-U_FIRST = 3
-FIRST = 4
-PERIOD = 8
 KINDS = 8
+WIDE = 48
+POOL_TOKENS = 48
+LAST_TOKENS = 8
+LAST_CUTS = (0, 4, 5, 7, 9, 11, 13, 15, 16)
 
 FLOPS = 2 * B * S * (D * CQ + 2 * CQ * H * DH) + 3 * B * S * H * DH
 
@@ -38,16 +31,19 @@ def tile_mla_pa_t_kernel(tc, h_bytes, h_scale, w_cq, w_q, w_qr, out):
     nc = tc.nc
     with ExitStack() as ctx:
         keep = ctx.enter_context(tc.tile_pool(name="keep", bufs=1))
-        work = ctx.enter_context(tc.tile_pool(name="work", bufs=3))
+        work = ctx.enter_context(tc.tile_pool(name="work", bufs=2))
         psum = ctx.enter_context(tc.psum_pool(name="psum", bufs=2))
         ctx.enter_context(tc.manual_schedule())
 
-        hb = [keep.tile([P, 4, D], U8, name=f"hb{c}", align_bytes=64) for c in range(NC)]
+        hb = {}
 
-        def load_h(c, j0, j1):
-            first = 4 * (c % 2)
-            nc.sync.dma_start(out=hb[c][:, j0:j1, :],
-                              in_=h_bytes[c // 2].rearrange("(p j) k -> p j k", j=KINDS)[:, first + j0 : first + j1, :])
+        def load_h(i0, i1):
+            rows = keep.tile([P, i1 - i0, D], U8, name=f"hb{i0}", align_bytes=64)
+            first = i0 % KINDS
+            nc.sync.dma_start(out=rows[:],
+                              in_=h_bytes[i0 // KINDS].rearrange("(p j) k -> p j k", j=KINDS)[:, first : first + i1 - i0, :])
+            for i in range(i0, i1):
+                hb[i] = rows[:, i - i0, :]
 
         scale = keep.tile([P, 2, 4], F32, name="scale")
         wcq_raw = [keep.tile([P, 4, CQ], BF16, name=f"wcq_raw{g}", align_bytes=64) for g in range(2)]
@@ -58,19 +54,18 @@ def tile_mla_pa_t_kernel(tc, h_bytes, h_scale, w_cq, w_q, w_qr, out):
             nc.sync.dma_start(out=wcq_raw[g][:],
                               in_=w_cq[g * 512 : (g + 1) * 512, :].rearrange("(p j) c -> p j c", j=4))
 
-        load_h(0, 0, 1)
-        load_h(0, 1, 2)
+        load_h(0, 1)
+        load_h(1, 2)
         load_wcq(0)
         nc.sync.dma_start(out=scale[:], in_=h_scale.rearrange("a b (g p t) -> p (a b g) t", g=2, t=4))
-        load_h(0, 2, 3)
+        load_h(2, 4)
         load_wcq(1)
-        load_h(0, 3, 4)
-        load_h(1, 0, 2)
         nc.sync.dma_start(out=wqr_raw[:], in_=w_qr.rearrange("(p j) c -> p j c", j=4))
-        load_h(1, 2, 4)
+        load_h(4, 6)
         nc.sync.dma_start(out=wq_raw[:], in_=w_q.rearrange("(p j) c -> p j c", j=4))
-        for c in range(2, NC):
-            load_h(c, 0, 4)
+        load_h(6, 8)
+        for i in range(8, NT, 4):
+            load_h(i, i + 4)
 
         pos = keep.tile([P, KINDS], F32, name="pos")
         nc.gpsimd.iota(pos[:], pattern=[[1, KINDS]], base=0, channel_multiplier=KINDS,
@@ -121,11 +116,13 @@ def tile_mla_pa_t_kernel(tc, h_bytes, h_scale, w_cq, w_q, w_qr, out):
         for ks in halves:
             nc.vector.tensor_tensor(out=frac[:, ks, 0:WIDE], in0=turns[:, ks], in1=whole[:, ks], op=ALU.subtract)
 
-        def tables_sin_cos():
-            nc.scalar.activation(out=fabs[:], in_=frac[:], func=ACT.Abs)
+        def tables_sin():
             nc.scalar.activation(out=sines[:, 1, :, 0:WIDE], in_=frac[:, :, 0:WIDE], func=ACT.Sin, scale=2.0 * math.pi)
-            nc.scalar.activation(out=cos[:], in_=fabs[:], func=ACT.Sin, scale=-2.0 * math.pi, bias=hpi[:, 0:1])
             nc.scalar.activation(out=sines[:, 0], in_=frac[:], func=ACT.Sin, scale=-2.0 * math.pi)
+
+        def tables_cos():
+            nc.scalar.activation(out=fabs[:], in_=frac[:], func=ACT.Abs)
+            nc.scalar.activation(out=cos[:], in_=fabs[:], func=ACT.Sin, scale=-2.0 * math.pi, bias=hpi[:, 0:1])
 
         mix = {}
 
@@ -141,16 +138,14 @@ def tile_mla_pa_t_kernel(tc, h_bytes, h_scale, w_cq, w_q, w_qr, out):
         wcq_sc = keep.tile([P, 2 * CQ], U8, name="wcq_sc", align_bytes=64)
         w2_codes = keep.tile([P, 1024], U32, name="w2_codes", align_bytes=64)
         w2_sc = keep.tile([P, 1024], U8, name="w2_sc", align_bytes=64)
-        wcq_g = keep.tile([P, 8 * CQ], BF16, name="wcq_g", align_bytes=64)
-        first_g = keep.tile([P, 1024], BF16, name="first_g", tag="late", align_bytes=64)
-        last_g = keep.tile([P, 1536], BF16, name="last_g", tag="last", align_bytes=64)
+        wcq_g = keep.tile([P, 8 * CQ], BF16, name="wcq_g", tag="wg", align_bytes=64)
 
         def pool_copy(out, in_):
             nc.gpsimd.tensor_scalar(out=out, in0=in_, scalar1=1.0, scalar2=0.0, op0=ALU.mult, op1=ALU.add)
 
-        def wcq_copy(copy, g):
-            copy(out=wcq_g[:, 4 * CQ * g : 4 * CQ * (g + 1)].rearrange("p (t m j) -> p t m j", m=P, j=4),
-                 in_=wcq_raw[g][:].rearrange("p j (m t) -> p t m j", t=4))
+        def wcq_copy(copy, g, t0, t1):
+            copy(out=wcq_g[:, CQ * (4 * g + t0) : CQ * (4 * g + t1)].rearrange("p (t m j) -> p t m j", m=P, j=4),
+                 in_=wcq_raw[g][:].rearrange("p j (m t) -> p t m j", t=4)[:, t0:t1])
 
         def wqr_copy(copy, dst, f):
             copy(out=dst.rearrange("p (m j) -> p m j", j=4),
@@ -162,263 +157,319 @@ def tile_mla_pa_t_kernel(tc, h_bytes, h_scale, w_cq, w_q, w_qr, out):
         def quant(codes, sc, grouped):
             nc.vector.quantize_mx(out=codes.bitcast(FP8X4), scales=sc, in_=grouped)
 
-        xb, hps, grp, cq, cps, ups, aps, sps, k1s, k23s, osb, prods, written = ({} for k in range(13))
+        xb, hps, hg, cg, hq, cq, cps, ups, aps, sps, osb, prods, stage, written = ({} for k in range(14))
 
-        def cast(i, copy):
-            x = work.tile([P, D], BF16, name=f"x{i}", tag="x", bufs=4, align_bytes=64)
-            copy(out=x[:], in_=hb[i // 4][:, i % 4, :].bitcast(E4M3))
-            xb[i] = x
+        def cast(i):
+            xb[i] = work.tile([P, D], BF16, name=f"x{i}", tag="x", bufs=4, align_bytes=64)
+            nc.scalar.copy(out=xb[i][:], in_=hb[i].bitcast(E4M3))
 
-        def h_transpose(i):
-            ht = psum.tile([P, 2, 2, P], F32, name=f"ht{i}", tag="ht", bufs=3)
+        def h_transpose(i, tag="ht", bufs=2):
+            hps[i] = psum.tile([P, 2, 2, P], F32, name=f"ht{i}", tag=tag, bufs=bufs)
             words = xb[i][:].bitcast(F32)
             for g in range(2):
                 for u in range(2):
-                    nc.tensor.transpose(ht[:, u, g, :], words[:, 256 * g + u : 256 * (g + 1) : 2], ident[:])
-            hps[i] = ht
+                    nc.tensor.transpose(hps[i][:, u, g, :], words[:, 256 * g + u : 256 * (g + 1) : 2], ident[:])
 
-        def group(i):
-            if i not in grp:
-                grp[i] = work.tile([P, D + CQ], BF16, name=f"g{i}", tag="g", bufs=LEAD + 4, align_bytes=64)
-            return grp[i]
+        def h_group(i):
+            if i // 2 not in hg:
+                hg[i // 2] = work.tile([P, 2 * D], BF16, name=f"hg{i // 2}", tag="hg", bufs=1, align_bytes=64)
+            return hg[i // 2][:, D * (i % 2) : D * (i % 2 + 1)]
 
-        def h_scale_mul(i, q0=0, q1=4):
+        def h_scale_mul(i, n0, n1):
             halves = hps[i][:].rearrange("p u g n -> p (u g n)").bitcast(BF16)
             src = halves.rearrange("p (u g n e) -> p g n u e", u=2, g=2, e=2)
-            dst = group(i)[:, 0:D].rearrange("p (g n u e) -> p g n u e", g=2, u=2, e=2)
-            while q0 < q1:
-                whole_passes = (q1 - q0) // 2 if q0 % 2 == 0 else 0
-                g0, g1 = q0 // 2, q0 // 2 + max(whole_passes, 1)
-                n0, n1 = (0, P) if whole_passes else (64 * (q0 % 2), 64 * (q0 % 2) + 64)
+            dst = h_group(i).rearrange("p (g n u e) -> p g n u e", g=2, u=2, e=2)
+            for g0, g1 in ((0, 2),) if n1 - n0 == P else ((0, 1), (1, 2)):
                 nc.vector.tensor_tensor(
                     out=dst[:, g0:g1, n0:n1], in0=src[:, g0:g1, n0:n1],
                     in1=scale[:, g0:g1, :].rearrange("p g (u e) -> p g u e", u=2).unsqueeze(2).to_broadcast(
                         [P, g1 - g0, n1 - n0, 2, 2]),
                     op=ALU.mult)
-                q0 = q0 + max(2 * whole_passes, 1)
 
-        def quant_step(s, lo, hi):
-            if s not in cq:
-                codes = work.tile([P, 384], U32, name=f"q{s}", tag="q", bufs=6, align_bytes=64)
-                sc = work.tile([P, 384], U8, name=f"qs{s}", tag="qs", bufs=6, align_bytes=64)
-                cq[s] = (codes, sc)
-            codes, sc = cq[s]
-            quant(codes[:, lo:hi], sc[:, lo:hi], group(s)[:, 4 * lo : 4 * hi])
+        def h_stage(i, n):
+            stage[i] = work.tile([P, 2, n, 2], F32, name=f"st{i}", tag="st", bufs=2, align_bytes=64)
+            nc.scalar.copy(out=stage[i][:], in_=hps[i][:, :, :, 0:n].rearrange("p u g n -> p g n u"))
 
-        def mm1(i):
-            codes, sc = cq[i]
-            tag, bufs = ("m2", 4) if i in (0, 2) else ("cp", 1)
-            cp = psum.tile([P, 4, P], F32, name=f"cp{i}", tag=tag, bufs=bufs)
+        def h_scale_pool(i, n):
+            src = stage[i][:].rearrange("p g n u -> p (g n u)").bitcast(BF16).rearrange("p (g n t) -> p g n t", g=2, t=4)
+            nc.gpsimd.tensor_tensor(
+                out=h_group(i).rearrange("p (g n t) -> p g n t", g=2, t=4)[:, :, 0:n], in0=src,
+                in1=scale[:].unsqueeze(2).to_broadcast([P, 2, n, 4]), op=ALU.mult)
+
+        def h_quant(w, parts=1):
+            codes = work.tile([P, 512], U32, name=f"hq{w}", tag="hq", bufs=2, align_bytes=64)
+            sc = work.tile([P, 512], U8, name=f"hs{w}", tag="hs", bufs=2, align_bytes=64)
+            for c in range(0, 512, 512 // parts):
+                cols = slice(c, c + 512 // parts)
+                quant(codes[:, cols], sc[:, cols], hg[w][:, 4 * cols.start : 4 * cols.stop])
+            hq[w] = (codes, sc)
+
+        def mm1(i, tag="m", bufs=3):
+            codes, sc = hq[i // 2]
+            cps[i] = psum.tile([P, 4, P], F32, name=f"cp{i}", tag=tag, bufs=bufs)
             for t in range(4):
                 for g in range(2):
-                    cols = slice(g * P, (g + 1) * P)
+                    cols = slice((2 * (i % 2) + g) * P, (2 * (i % 2) + g + 1) * P)
                     nc.tensor.matmul_mx(
-                        out=cp[:, t, :],
+                        out=cps[i][:, t, :],
                         lhsT=wcq_codes[:, (4 * g + t) * P : (4 * g + t + 1) * P].bitcast(FP8X4),
                         lhsT_scale=wcq_sc[:, (4 * g + t) * P : (4 * g + t + 1) * P],
                         rhs=codes[:, cols].bitcast(FP8X4), rhs_scale=sc[:, cols],
                         start=(g == 0), stop=(g == 1))
-            cps[i] = cp
-
-        def c_place(i):
-            return i + LAG, 256
 
         def c_copy(i):
-            nc.scalar.copy(out=group(c_place(i)[0])[:, 4 * c_place(i)[1] : 4 * c_place(i)[1] + CQ].rearrange("p (m e t) -> p m t e", e=2, t=4),
+            if i // 2 not in cg:
+                cg[i // 2] = work.tile([P, 2 * CQ], BF16, name=f"cg{i // 2}", tag="cg", bufs=2, align_bytes=64)
+            dst = cg[i // 2][:, CQ * (i % 2) : CQ * (i % 2 + 1)]
+            nc.scalar.copy(out=dst.rearrange("p (m e t) -> p m t e", e=2, t=4),
                            in_=cps[i][:].rearrange("p t (m e) -> p m t e", e=2))
 
-        def mm2(i, part):
-            codes, sc = cq[c_place(i)[0]]
-            cols = slice(c_place(i)[1], c_place(i)[1] + P)
+        def c_quant(i0, i1):
+            w = i0 // 2
+            if w not in cq:
+                cq[w] = (work.tile([P, 2 * P], U32, name=f"cq{w}", tag="cq", bufs=2, align_bytes=64),
+                         work.tile([P, 2 * P], U8, name=f"cs{w}", tag="cs", bufs=2, align_bytes=64))
+            codes, sc = cq[w]
+            lo, hi = P * (i0 - 2 * w), P * (i1 - 2 * w)
+            quant(codes[:, lo:hi], sc[:, lo:hi], cg[w][:, 4 * lo : 4 * hi])
 
-            def mm(dst, c0, c1, start, stop):
-                nc.tensor.matmul_mx(out=dst, lhsT=codes[:, cols].bitcast(FP8X4), lhsT_scale=sc[:, cols],
-                                    rhs=w2_codes[:, c0:c1].bitcast(FP8X4), rhs_scale=w2_sc[:, c0:c1],
-                                    start=start, stop=stop)
+        def mm2(i, dst, c0, c1, start, stop):
+            codes, sc = cq[i // 2]
+            cols = slice(P * (i % 2), P * (i % 2 + 1))
+            nc.tensor.matmul_mx(out=dst, lhsT=codes[:, cols].bitcast(FP8X4), lhsT_scale=sc[:, cols],
+                                rhs=w2_codes[:, c0:c1].bitcast(FP8X4), rhs_scale=w2_sc[:, c0:c1],
+                                start=start, stop=stop)
 
-            def mm_a(tag, bufs):
-                aps[i] = psum.tile([P, 512], F32, name=f"ap{i}", tag=tag, bufs=bufs)
-                mm(aps[i][:], 512, 1024, True, True)
+        def mm_u(i, tag="u"):
+            ups[i] = psum.tile([P, 512], F32, name=f"up{i}", tag=tag, bufs=2)
+            mm2(i, ups[i][:], 0, 512, True, True)
 
-            if part == "sum":
-                sps[i] = psum.tile([P, 256], F32, name=f"sp{i}", tag="m2", bufs=4)
-                mm(sps[i][:], 0, 256, True, False)
-                mm(sps[i][:], 256, 512, False, True)
-                return
-            if part == "u":
-                ups[i] = psum.tile([P, 512], F32, name=f"up{i}", tag="m2", bufs=4)
-                mm(ups[i][:], 0, 512, True, True)
-            elif i == 0:
-                mm_a("cp", 1)
-            elif i < NT - U_FIRST:
-                mm_a("m2", 4)
+        def mm_sum(i, tag=None, bufs=2):
+            if tag:
+                sps[i] = psum.tile([P, 256], F32, name=f"sp{i}", tag=tag, bufs=bufs)[:]
             else:
-                mm_a("ht", 3)
+                if i % 2 == 0:
+                    sps[i, "pair"] = psum.tile([P, 512], F32, name=f"sp{i}", tag="sum", bufs=1)
+                sps[i] = sps[i - i % 2, "pair"][:, 256 * (i % 2) : 256 * (i % 2 + 1)]
+            mm2(i, sps[i], 0, 256, True, False)
+            mm2(i, sps[i], 256, 512, False, True)
+
+        def mm_a(i):
+            aps[i] = psum.tile([P, 512], F32, name=f"ap{i}", tag="m", bufs=3)
+            mm2(i, aps[i][:], 512, 1024, True, True)
 
         def piece(i, part):
             n = 2 * (i % KINDS) + part
-            cuts = CUTS if i >= NT - KINDS else range(0, 2 * KINDS + 1, 4)
+            cuts = LAST_CUTS if i >= NT - KINDS else range(0, 2 * KINDS + 1, 4)
             first = max(cut for cut in cuts if cut <= n)
-            return first, cuts[cuts.index(first) + 1] - first
-
-        def result(i, part):
-            first, count = piece(i, part)
+            count = cuts[cuts.index(first) + 1] - first
             key = (i // KINDS, first)
             if key not in osb:
-                if i < NT - KINDS:
-                    osb[key] = work.tile([P, H, count * DH], F32, name=f"o{i}", tag="o", bufs=4, align_bytes=64)
+                if count == 4:
+                    osb[key] = work.tile([P, H, count * DH], F32, name=f"o{i}", tag="o", bufs=3, align_bytes=64)
                 else:
                     osb[key] = keep.tile([P, H, count * DH], F32, name=f"last{i}_{part}", align_bytes=64)
-            n = 2 * (i % KINDS) + part - first
+            return key, count
+
+        def half(i, part):
+            key = piece(i, part)[0]
+            n = 2 * (i % KINDS) + part - key[1]
             return osb[key][:, :, n * DH : (n + 1) * DH]
 
-        def a_copy(i):
-            nc.scalar.copy(out=result(i, 0), in_=aps[i][:].rearrange("p (n d) -> p n d", n=H))
+        def store(i, part):
+            key, count = piece(i, part)
+            written[key] = written.get(key, 0) + 1
+            if written[key] == count:
+                rows = out[key[0]].rearrange("n (p j) d -> p n (j d)", j=KINDS)
+                nc.sync.dma_start(out=rows[:, :, key[1] * DH : (key[1] + count) * DH], in_=osb[key][:])
 
-        def products(i):
-            if i // 4 not in prods:
-                prods[i // 4] = work.tile([P, 4 * 768], F32, name=f"prod{i}", tag="prod", bufs=2, align_bytes=64)
-            return prods[i // 4]
+        def a_copy(i):
+            nc.scalar.copy(out=half(i, 0), in_=aps[i][:].rearrange("p (n d) -> p n d", n=H))
+            store(i, 0)
+
+        def products(w):
+            if w not in prods:
+                prods[w] = work.tile([P, 2 * 768], F32, name=f"prod{w}", tag="prod", bufs=2, align_bytes=64)
+            return prods[w]
 
         def rope_k23(i):
-            k23 = products(i)[:, 512 * (i % 4) : 512 * (i % 4 + 1)].rearrange("p (n i e) -> p n i e", n=H, e=2)
+            k23 = products(i // 2)[:, 512 * (i % 2) : 512 * (i % 2 + 1)].rearrange("p (n i e) -> p n i e", n=H, e=2)
             kind = i % KINDS
             table = mix[kind // 4][:, NP * (kind % 4) : NP * (kind % 4 + 1), :]
             nc.vector.tensor_tensor(out=k23, in0=ups[i][:].rearrange("p (f n i) -> p n i f", f=2, n=H),
                                     in1=table.unsqueeze(1).to_broadcast([P, H, NP, 2]), op=ALU.mult)
-            k23s[i] = k23
 
         def rope_k1(i):
-            first = 2048 + 256 * (i % 4)
-            k1 = products(i)[:, first : first + 256].rearrange("p (n i) -> p n i", n=H)
-            nc.vector.tensor_tensor(out=k1, in0=sps[i][:].rearrange("p (n i) -> p n i", n=H),
+            first = 1024 + 256 * (i % 2)
+            nc.vector.tensor_tensor(out=products(i // 2)[:, first : first + 256].rearrange("p (n i) -> p n i", n=H),
+                                    in0=sps[i].rearrange("p (n i) -> p n i", n=H),
                                     in1=cos[:, i % KINDS, :].unsqueeze(1).to_broadcast([P, H, NP]), op=ALU.mult)
-            k1s[i] = k1
 
-        def rope_add(i):
-            engine = nc.vector if i >= NT - V_ADDS else nc.gpsimd
+        def rope_k1_pair(w):
+            kind = 2 * w % KINDS
+            nc.vector.tensor_tensor(out=products(w)[:, 1024:1536].rearrange("p (j n i) -> p j n i", j=2, n=H),
+                                    in0=sps[2 * w, "pair"][:].rearrange("p (j n i) -> p j n i", j=2, n=H),
+                                    in1=cos[:, kind : kind + 2, :].unsqueeze(2).to_broadcast([P, 2, H, NP]),
+                                    op=ALU.mult)
+
+        def rope_add_pair(w):
+            nc.gpsimd.tensor_tensor(
+                out=osb[piece(2 * w, 1)[0]][:].rearrange("p n (j f i e) -> p f j n i e", j=2, f=2, e=2)[:, 1],
+                in0=products(w)[:, 0:1024].rearrange("p (j n i e) -> p j n i e", j=2, n=H, e=2),
+                in1=products(w)[:, 1024:1536].rearrange("p (j n i) -> p j n i", j=2, n=H).unsqueeze(4).to_broadcast(
+                    [P, 2, H, NP, 2]),
+                op=ALU.add)
+            store(2 * w, 1)
+            store(2 * w + 1, 1)
+
+        def rope_add(engine, i):
+            first = 1024 + 256 * (i % 2)
             engine.tensor_tensor(
-                out=result(i, 1).rearrange("p n (i e) -> p n i e", e=2),
-                in0=k23s[i], in1=k1s[i].unsqueeze(3).to_broadcast([P, H, NP, 2]), op=ALU.add)
-
-        def store(i, part):
-            first, count = piece(i, part)
-            key = (i // KINDS, first)
-            written[key] = written.get(key, 0) + 1
-            if written[key] == count:
-                rows = out[i // KINDS].rearrange("n (p j) d -> p n (j d)", j=KINDS)
-                nc.sync.dma_start(out=rows[:, :, first * DH : (first + count) * DH], in_=osb[key][:])
-
-        def ok(i):
-            return 0 <= i < NT
-
-        def finish(i):
-            rope_add(i)
+                out=half(i, 1).rearrange("p n (i e) -> p n i e", e=2),
+                in0=products(i // 2)[:, 512 * (i % 2) : 512 * (i % 2 + 1)].rearrange("p (n i e) -> p n i e", n=H, e=2),
+                in1=products(i // 2)[:, first : first + 256].rearrange("p (n i) -> p n i", n=H).unsqueeze(3).to_broadcast(
+                    [P, H, NP, 2]),
+                op=ALU.add)
             store(i, 1)
 
-        def quarters(s):
-            short = len([r for r in range(FIRST, s) if (r - FIRST) % PERIOD < 2][: 2 * (LEAD - 1)])
-            return min(4 * (s + LEAD) - 2 * short, 4 * NT)
-
-        def turn(s, done):
-            ahead = 3 if s % 2 == RUN else 2
-            while ok(len(hps)) and 4 * len(hps) < quarters(s + ahead) and 4 * (len(hps) - 2) <= done:
-                h_transpose(len(hps))
-
         def second(i):
-            mm2(i, "a")
+            mm_a(i)
             a_copy(i)
-            store(i, 0)
 
-        def step(s):
-            if LAG + 1 < s:
-                quant_step(s, 0, 384)
-            if s > LAG + 1:
-                mm2(s - LAG - 1, "sum")
-            turn(s, quarters(s))
-            if ok(len(xb)) and 4 * len(xb) < quarters(s + 4):
-                cast(len(xb), nc.scalar.copy)
-            if s == NT - 1:
-                mm2(s - LAG, "u")
-                second(s - LAG)
-            if LAG + 1 < s:
-                mm1(s)
-                c_copy(s)
-            if s < NT - 1:
-                second(s - LAG)
-                mm2(s - LAG, "u")
-            q0, q1 = quarters(s), quarters(s + 1)
-            for i in range(q0 // 4, -(-q1 // 4)):
-                h_scale_mul(i, max(q0 - 4 * i, 0), min(q1 - 4 * i, 4))
-            turn(s, q1)
-            rope_k23(s - LAG - 1)
-            rope_k1(s - LAG - 1)
-            finish(s - LAG - 1)
+        def window(w):
+            a, b = 2 * w, 2 * w + 1
+            if w == 2:
+                quant(w2_codes[:, 512:1024], w2_sc[:, 512:1024], wq_g[:])
+            h_quant(w)
+            c_quant(a - 2, a)
+            h_scale_pool(a + 2, POOL_TOKENS)
+            cast(a + 4)
+            cast(b + 4)
+            if w == 2:
+                second(0)
+                second(1)
+            mm1(a)
+            c_copy(a)
+            mm_u(a - 2)
+            mm_u(b - 2)
+            rope_add_pair(w - 2)
+            mm1(b)
+            c_copy(b)
+            mm_sum(a - 2)
+            mm_sum(b - 2)
+            h_scale_mul(b + 2, 0, P)
+            h_scale_mul(a + 2, POOL_TOKENS, P)
+            second(a - 2)
+            h_transpose(a + 4)
+            h_stage(a + 4, POOL_TOKENS if w + 3 < NW else LAST_TOKENS)
+            h_transpose(b + 4)
+            second(b - 2)
+            rope_k23(a - 2)
+            rope_k23(b - 2)
+            rope_k1_pair(w - 1)
 
-        wcq_copy(nc.vector.tensor_copy, 0)
-        wcq_copy(pool_copy, 1)
-        wqr_copy(pool_copy, first_g[:], 0)
+        wcq_copy(nc.vector.tensor_copy, 0, 0, 4)
+        wcq_copy(pool_copy, 1, 0, 2)
         for i in range(2):
-            cast(i, nc.scalar.copy)
+            cast(i)
             h_transpose(i)
-        for i in range(N1):
-            cast(i + 2, nc.scalar.copy)
-            h_transpose(i + 2)
-            h_scale_mul(i)
-        tables_sin_cos()
-        quant_step(0, 0, 256)
+        tables_sin()
+        for i in range(2):
+            cast(i + 2)
+            h_transpose(i + 2, "u", 2)
+            h_scale_mul(i, 0, P)
+        wcq_copy(nc.scalar.copy, 1, 2, 4)
+        tables_cos()
+        h_quant(0, 2)
         quant(wcq_codes[:], wcq_sc[:], wcq_g[:])
-        for i in (1, 2, 3):
-            quant_step(i, 0, 256)
-        wq_copy(nc.vector.tensor_copy, last_g[:, 0:512], 128, 256)
-        quant(w2_codes[:, 0:256], w2_sc[:, 0:256], first_g[:])
-        late_g = keep.tile([P, 1536], BF16, name="late_g", tag="late", align_bytes=64)
-        wqr_copy(pool_copy, late_g[:, 0:1024], 1)
-        wq_copy(pool_copy, late_g[:, 1024:1536], 0, 128)
-        for k in range(N2):
-            if k < N2 - 1:
-                cast(N1 + k + 2, nc.scalar.copy)
-            else:
-                wq_copy(nc.scalar.copy, last_g[:, 512:1536], 256, 512)
-            if 1 <= k:
-                c_copy(k - 1)
-            if k < 4:
-                mm1(k)
-            if k < N2 - 1:
-                h_transpose(N1 + k + 2)
-            h_scale_mul(N1 + k)
-        for k in range(N2, 4):
-            mm1(k)
-            c_copy(k - 1)
-        cast(N1 + N2 + 1, nc.scalar.copy)
+        wqr_g = keep.tile([P, 2048], BF16, name="wqr_g", tag="wg", align_bytes=64)
+        wqr_copy(pool_copy, wqr_g[:, 0:1024], 0)
+        cast(4)
+        cast(5)
+        wqr_copy(nc.scalar.copy, wqr_g[:, 1024:2048], 1)
+        mm1(0)
+        c_copy(0)
+        mm1(1)
+        c_copy(1)
+        for i in (2, 3):
+            h_transpose(i + 2)
+            h_scale_mul(i, 0, P)
+        h_quant(1, 2)
+        quant(w2_codes[:, 0:512], w2_sc[:, 0:512], wqr_g[:])
+        c_quant(0, 2)
+        tables_mix(nc.gpsimd, 0, "wg")
+        wq_g = keep.tile([P, 2048], BF16, name="wq_g", align_bytes=64)
+        wq_copy(pool_copy, wq_g[:, 0:768], 0, 192)
+        tables_mix(nc.gpsimd, 1, "mix1")
+        cast(6)
+        cast(7)
+        mm1(2)
+        c_copy(2)
+        wq_copy(nc.scalar.copy, wq_g[:, 768:1280], 192, 320)
+        mm_u(0)
+        mm_u(1)
+        mm1(3)
         c_copy(3)
-        cast(N1 + N2 + 2, nc.scalar.copy)
-        quant(w2_codes[:, 256:640], w2_sc[:, 256:640], late_g[:])
-        quant_step(LAG, 256, 384)
-        quant_step(LAG + 1, 256, 384)
-        tables_mix(nc.vector, 0, "mix0")
-        quant(w2_codes[:, 640:1024], w2_sc[:, 640:1024], last_g[:])
-        tables_mix(nc.gpsimd, 1, "last")
-        mm2(0, "u")
-        mm2(0, "sum")
-        second(0)
-        for s in range(LAG + 1, NT):
-            step(s)
-        quant_step(NT, 256, 384)
-        mm2(NT - 3, "sum")
-        mm2(NT - 2, "u")
-        second(NT - 2)
-        rope_k23(NT - 3)
-        rope_k1(NT - 3)
-        mm2(NT - 2, "sum")
-        rope_k23(NT - 2)
-        rope_k1(NT - 2)
-        quant_step(NT + 1, 256, 384)
-        finish(NT - 3)
-        finish(NT - 2)
-        mm2(NT - 1, "u")
-        mm2(NT - 1, "sum")
-        second(NT - 1)
-        rope_k23(NT - 1)
-        rope_k1(NT - 1)
-        finish(NT - 1)
+        mm_sum(0)
+        mm_sum(1)
+        wq_copy(nc.scalar.copy, wq_g[:, 1280:2048], 320, 512)
+        for i in (4, 5):
+            h_scale_mul(i, 0, P)
+            h_transpose(i + 2)
+        h_stage(6, POOL_TOKENS)
+        rope_k23(0)
+        rope_k23(1)
+        rope_k1_pair(0)
+        for w in range(2, NW - 2):
+            window(w)
+        a = NT - 6
+        h_quant(NW - 2)
+        c_quant(a, a + 2)
+        h_scale_pool(a + 4, LAST_TOKENS)
+        rope_add_pair(NW - 4)
+        mm1(a + 2)
+        c_copy(a + 2)
+        mm1(a + 3)
+        c_copy(a + 3)
+        mm_u(a)
+        mm_sum(a, "sum", 1)
+        mm_u(a + 1)
+        second(a)
+        second(a + 1)
+        h_scale_mul(a + 5, 0, P)
+        h_scale_mul(a + 4, LAST_TOKENS, P)
+        mm_sum(a + 1, "ht")
+        rope_k23(a)
+        c_quant(a + 2, a + 4)
+        rope_k1(a)
+        h_quant(NW - 1)
+        rope_add(nc.gpsimd, a)
+        mm_u(a + 2)
+        mm_sum(a + 2, "sum", 1)
+        mm_u(a + 3, "ht")
+        mm1(a + 4)
+        c_copy(a + 4)
+        mm1(a + 5)
+        c_copy(a + 5)
+        rope_k23(a + 1)
+        rope_k1(a + 1)
+        rope_add(nc.gpsimd, a + 1)
+        mm_sum(a + 3, "ht")
+        second(a + 2)
+        second(a + 3)
+        for i in (a + 2, a + 3):
+            rope_k23(i)
+            rope_k1(i)
+        c_quant(a + 4, a + 6)
+        rope_add(nc.vector, a + 2)
+        rope_add(nc.vector, a + 3)
+        for i in (a + 4, a + 5):
+            mm_u(i)
+            mm_sum(i, "ht")
+            second(i)
+        rope_k23(a + 4)
+        rope_k1(a + 4)
+        rope_k23(a + 5)
+        rope_add(nc.vector, a + 4)
+        rope_k1(a + 5)
+        rope_add(nc.vector, a + 5)

@@ -20,9 +20,10 @@ NW = NT // 2
 NP = DH // 2
 KINDS = 8
 WIDE = 48
-POOL_TOKENS = 48
-LAST_TOKENS = 8
-LAST_CUTS = (0, 4, 5, 7, 9, 11, 13, 15, 16)
+POOL_TOKENS = 128
+LAST_TOKENS = 16
+CUTS = (0, 1, 5, 9, 13, 16)
+LAST_CUTS = (0, 1, 5, 7, 9, 11, 13, 15, 16)
 
 FLOPS = 2 * B * S * (D * CQ + 2 * CQ * H * DH) + 3 * B * S * H * DH
 
@@ -175,26 +176,27 @@ def tile_mla_pa_t_kernel(tc, h_bytes, h_scale, w_cq, w_q, w_qr, out):
                 hg[i // 2] = work.tile([P, 2 * D], BF16, name=f"hg{i // 2}", tag="hg", bufs=1, align_bytes=64)
             return hg[i // 2][:, D * (i % 2) : D * (i % 2 + 1)]
 
-        def h_scale_mul(i, n0, n1):
+        def h_scale_mul(i, n0):
             halves = hps[i][:].rearrange("p u g n -> p (u g n)").bitcast(BF16)
             src = halves.rearrange("p (u g n e) -> p g n u e", u=2, g=2, e=2)
             dst = h_group(i).rearrange("p (g n u e) -> p g n u e", g=2, u=2, e=2)
-            for g0, g1 in ((0, 2),) if n1 - n0 == P else ((0, 1), (1, 2)):
-                nc.vector.tensor_tensor(
-                    out=dst[:, g0:g1, n0:n1], in0=src[:, g0:g1, n0:n1],
-                    in1=scale[:, g0:g1, :].rearrange("p g (u e) -> p g u e", u=2).unsqueeze(2).to_broadcast(
-                        [P, g1 - g0, n1 - n0, 2, 2]),
-                    op=ALU.mult)
+            for g0, g1, n in ((0, 2, 0),) if n0 == 0 else ((0, 1, n0), (1, 2, 0)):
+                if n < P:
+                    nc.vector.tensor_tensor(
+                        out=dst[:, g0:g1, n:P], in0=src[:, g0:g1, n:P],
+                        in1=scale[:, g0:g1, :].rearrange("p g (u e) -> p g u e", u=2).unsqueeze(2).to_broadcast(
+                            [P, g1 - g0, P - n, 2, 2]),
+                        op=ALU.mult)
 
         def h_stage(i, n):
-            stage[i] = work.tile([P, 2, n, 2], F32, name=f"st{i}", tag="st", bufs=2, align_bytes=64)
-            nc.scalar.copy(out=stage[i][:], in_=hps[i][:, :, :, 0:n].rearrange("p u g n -> p g n u"))
+            stage[i] = work.tile([P, n, 2], F32, name=f"st{i}", tag="st", bufs=2, align_bytes=64)
+            nc.scalar.copy(out=stage[i][:], in_=hps[i][:, :, 0, 0:n].rearrange("p u n -> p n u"))
 
         def h_scale_pool(i, n):
-            src = stage[i][:].rearrange("p g n u -> p (g n u)").bitcast(BF16).rearrange("p (g n t) -> p g n t", g=2, t=4)
+            src = stage[i][:].rearrange("p n u -> p (n u)").bitcast(BF16).rearrange("p (n t) -> p n t", t=4)
             nc.gpsimd.tensor_tensor(
-                out=h_group(i).rearrange("p (g n t) -> p g n t", g=2, t=4)[:, :, 0:n], in0=src,
-                in1=scale[:].unsqueeze(2).to_broadcast([P, 2, n, 4]), op=ALU.mult)
+                out=h_group(i)[:, 0 : 4 * n].rearrange("p (n t) -> p n t", t=4), in0=src,
+                in1=scale[:, 0:1, :].to_broadcast([P, n, 4]), op=ALU.mult)
 
         def h_quant(w, parts=1):
             codes = work.tile([P, 512], U32, name=f"hq{w}", tag="hq", bufs=2, align_bytes=64)
@@ -260,13 +262,13 @@ def tile_mla_pa_t_kernel(tc, h_bytes, h_scale, w_cq, w_q, w_qr, out):
 
         def piece(i, part):
             n = 2 * (i % KINDS) + part
-            cuts = LAST_CUTS if i >= NT - KINDS else range(0, 2 * KINDS + 1, 4)
+            cuts = LAST_CUTS if i >= NT - KINDS else CUTS
             first = max(cut for cut in cuts if cut <= n)
             count = cuts[cuts.index(first) + 1] - first
             key = (i // KINDS, first)
             if key not in osb:
-                if count == 4:
-                    osb[key] = work.tile([P, H, count * DH], F32, name=f"o{i}", tag="o", bufs=3, align_bytes=64)
+                if count > 2:
+                    osb[key] = work.tile([P, H, 4 * DH], F32, name=f"o{i}", tag="o", bufs=3, align_bytes=64)
                 else:
                     osb[key] = keep.tile([P, H, count * DH], F32, name=f"last{i}_{part}", align_bytes=64)
             return key, count
@@ -281,7 +283,7 @@ def tile_mla_pa_t_kernel(tc, h_bytes, h_scale, w_cq, w_q, w_qr, out):
             written[key] = written.get(key, 0) + 1
             if written[key] == count:
                 rows = out[key[0]].rearrange("n (p j) d -> p n (j d)", j=KINDS)
-                nc.sync.dma_start(out=rows[:, :, key[1] * DH : (key[1] + count) * DH], in_=osb[key][:])
+                nc.sync.dma_start(out=rows[:, :, key[1] * DH : (key[1] + count) * DH], in_=osb[key][:, :, 0 : count * DH])
 
         def a_copy(i):
             nc.scalar.copy(out=half(i, 0), in_=aps[i][:].rearrange("p (n d) -> p n d", n=H))
@@ -289,7 +291,7 @@ def tile_mla_pa_t_kernel(tc, h_bytes, h_scale, w_cq, w_q, w_qr, out):
 
         def products(w):
             if w not in prods:
-                prods[w] = work.tile([P, 2 * 768], F32, name=f"prod{w}", tag="prod", bufs=2, align_bytes=64)
+                prods[w] = work.tile([P, 2 * 768], F32, name=f"prod{w}", tag="prod", bufs=3, align_bytes=64)
             return prods[w]
 
         def rope_k23(i):
@@ -313,8 +315,9 @@ def tile_mla_pa_t_kernel(tc, h_bytes, h_scale, w_cq, w_q, w_qr, out):
                                     op=ALU.mult)
 
         def rope_add_pair(w):
+            key = piece(2 * w, 1)[0]
             nc.gpsimd.tensor_tensor(
-                out=osb[piece(2 * w, 1)[0]][:].rearrange("p n (j f i e) -> p f j n i e", j=2, f=2, e=2)[:, 1],
+                out=osb[key][:].rearrange("p n (j f i e) -> p f j n i e", j=2, f=2, e=2)[:, 1 - key[1] % 2],
                 in0=products(w)[:, 0:1024].rearrange("p (j n i e) -> p j n i e", j=2, n=H, e=2),
                 in1=products(w)[:, 1024:1536].rearrange("p (j n i) -> p j n i", j=2, n=H).unsqueeze(4).to_broadcast(
                     [P, 2, H, NP, 2]),
@@ -357,8 +360,8 @@ def tile_mla_pa_t_kernel(tc, h_bytes, h_scale, w_cq, w_q, w_qr, out):
             c_copy(b)
             mm_sum(a - 2)
             mm_sum(b - 2)
-            h_scale_mul(b + 2, 0, P)
-            h_scale_mul(a + 2, POOL_TOKENS, P)
+            h_scale_mul(b + 2, 0)
+            h_scale_mul(a + 2, POOL_TOKENS)
             second(a - 2)
             h_transpose(a + 4)
             h_stage(a + 4, POOL_TOKENS if w + 3 < NW else LAST_TOKENS)
@@ -377,7 +380,7 @@ def tile_mla_pa_t_kernel(tc, h_bytes, h_scale, w_cq, w_q, w_qr, out):
         for i in range(2):
             cast(i + 2)
             h_transpose(i + 2, "u", 2)
-            h_scale_mul(i, 0, P)
+            h_scale_mul(i, 0)
         wcq_copy(nc.scalar.copy, 1, 2, 4)
         tables_cos()
         h_quant(0, 2)
@@ -393,7 +396,7 @@ def tile_mla_pa_t_kernel(tc, h_bytes, h_scale, w_cq, w_q, w_qr, out):
         c_copy(1)
         for i in (2, 3):
             h_transpose(i + 2)
-            h_scale_mul(i, 0, P)
+            h_scale_mul(i, 0)
         h_quant(1, 2)
         quant(w2_codes[:, 0:512], w2_sc[:, 0:512], wqr_g[:])
         c_quant(0, 2)
@@ -414,7 +417,7 @@ def tile_mla_pa_t_kernel(tc, h_bytes, h_scale, w_cq, w_q, w_qr, out):
         mm_sum(1)
         wq_copy(nc.scalar.copy, wq_g[:, 1280:2048], 320, 512)
         for i in (4, 5):
-            h_scale_mul(i, 0, P)
+            h_scale_mul(i, 0)
             h_transpose(i + 2)
         h_stage(6, POOL_TOKENS)
         rope_k23(0)
@@ -429,15 +432,15 @@ def tile_mla_pa_t_kernel(tc, h_bytes, h_scale, w_cq, w_q, w_qr, out):
         rope_add_pair(NW - 4)
         mm1(a + 2)
         c_copy(a + 2)
+        second(a)
+        mm_u(a)
         mm1(a + 3)
         c_copy(a + 3)
-        mm_u(a)
         mm_sum(a, "sum", 1)
         mm_u(a + 1)
-        second(a)
         second(a + 1)
-        h_scale_mul(a + 5, 0, P)
-        h_scale_mul(a + 4, LAST_TOKENS, P)
+        h_scale_mul(a + 5, 0)
+        h_scale_mul(a + 4, LAST_TOKENS)
         mm_sum(a + 1, "ht")
         rope_k23(a)
         c_quant(a + 2, a + 4)
@@ -445,17 +448,17 @@ def tile_mla_pa_t_kernel(tc, h_bytes, h_scale, w_cq, w_q, w_qr, out):
         h_quant(NW - 1)
         rope_add(nc.gpsimd, a)
         mm_u(a + 2)
+        second(a + 2)
         mm_sum(a + 2, "sum", 1)
-        mm_u(a + 3, "ht")
         mm1(a + 4)
         c_copy(a + 4)
+        mm_u(a + 3, "ht")
         mm1(a + 5)
         c_copy(a + 5)
         rope_k23(a + 1)
         rope_k1(a + 1)
         rope_add(nc.gpsimd, a + 1)
         mm_sum(a + 3, "ht")
-        second(a + 2)
         second(a + 3)
         for i in (a + 2, a + 3):
             rope_k23(i)

@@ -20,8 +20,9 @@ NW = NT // 2
 NP = DH // 2
 KINDS = 8
 WIDE = 48
-POOL_TOKENS = 128
+POOL_TOKENS = 92
 LAST_TOKENS = 16
+WQ_POOL = 320
 CUTS = (0, 1, 5, 9, 13, 16)
 LAST_CUTS = (0, 1, 5, 7, 9, 11, 13, 15, 16)
 
@@ -59,8 +60,8 @@ def tile_mla_pa_t_kernel(tc, h_bytes, h_scale, w_cq, w_q, w_qr, out):
         load_h(1, 2)
         load_wcq(0)
         nc.sync.dma_start(out=scale[:], in_=h_scale.rearrange("a b (g p t) -> p (a b g) t", g=2, t=4))
-        load_h(2, 4)
         load_wcq(1)
+        load_h(2, 4)
         nc.sync.dma_start(out=wqr_raw[:], in_=w_qr.rearrange("(p j) c -> p j c", j=4))
         load_h(4, 6)
         nc.sync.dma_start(out=wq_raw[:], in_=w_q.rearrange("(p j) c -> p j c", j=4))
@@ -117,13 +118,15 @@ def tile_mla_pa_t_kernel(tc, h_bytes, h_scale, w_cq, w_q, w_qr, out):
         for ks in halves:
             nc.vector.tensor_tensor(out=frac[:, ks, 0:WIDE], in0=turns[:, ks], in1=whole[:, ks], op=ALU.subtract)
 
-        def tables_sin():
-            nc.scalar.activation(out=sines[:, 1, :, 0:WIDE], in_=frac[:, :, 0:WIDE], func=ACT.Sin, scale=2.0 * math.pi)
-            nc.scalar.activation(out=sines[:, 0], in_=frac[:], func=ACT.Sin, scale=-2.0 * math.pi)
+        def table_sin(ks):
+            nc.scalar.activation(out=sines[:, 1, ks, 0:WIDE], in_=frac[:, ks, 0:WIDE], func=ACT.Sin, scale=2.0 * math.pi)
+            nc.scalar.activation(out=sines[:, 0, ks], in_=frac[:, ks], func=ACT.Sin, scale=-2.0 * math.pi)
 
-        def tables_cos():
-            nc.scalar.activation(out=fabs[:], in_=frac[:], func=ACT.Abs)
-            nc.scalar.activation(out=cos[:], in_=fabs[:], func=ACT.Sin, scale=-2.0 * math.pi, bias=hpi[:, 0:1])
+        def table_abs(ks):
+            nc.scalar.activation(out=fabs[:, ks], in_=frac[:, ks], func=ACT.Abs)
+
+        def table_cos(ks):
+            nc.scalar.activation(out=cos[:, ks], in_=fabs[:, ks], func=ACT.Sin, scale=-2.0 * math.pi, bias=hpi[:, 0:1])
 
         mix = {}
 
@@ -149,11 +152,12 @@ def tile_mla_pa_t_kernel(tc, h_bytes, h_scale, w_cq, w_q, w_qr, out):
                  in_=wcq_raw[g][:].rearrange("p j (m t) -> p t m j", t=4)[:, t0:t1])
 
         def wqr_copy(copy, dst, f):
-            copy(out=dst.rearrange("p (m j) -> p m j", j=4),
-                 in_=wqr_raw[:].rearrange("p j (m e) -> p e m j", e=2)[:, 1 - f])
+            copy(out=dst.rearrange("p (c m j) -> p c m j", c=2, j=4),
+                 in_=wqr_raw[:].rearrange("p j (c m e) -> p e c m j", c=2, e=2)[:, 1 - f])
 
         def wq_copy(copy, dst, n0, n1):
-            copy(out=dst.rearrange("p (n j) -> p n j", j=4), in_=wq_raw[:, :, n0:n1].rearrange("p j n -> p n j"))
+            copy(out=dst.rearrange("p (c n j) -> p c n j", c=2, j=4),
+                 in_=wq_raw[:, :, n0:n1].rearrange("p j (c n) -> p c n j", c=2))
 
         def quant(codes, sc, grouped):
             nc.vector.quantize_mx(out=codes.bitcast(FP8X4), scales=sc, in_=grouped)
@@ -176,17 +180,25 @@ def tile_mla_pa_t_kernel(tc, h_bytes, h_scale, w_cq, w_q, w_qr, out):
                 hg[i // 2] = work.tile([P, 2 * D], BF16, name=f"hg{i // 2}", tag="hg", bufs=1, align_bytes=64)
             return hg[i // 2][:, D * (i % 2) : D * (i % 2 + 1)]
 
+        scale_rows = keep.tile([P, 2 * P - LAST_TOKENS, 4], F32, name="scale_rows", align_bytes=64)
+
+        def spread_scale(g):
+            rows = scale_rows[:, 0 : P - LAST_TOKENS] if g == 0 else scale_rows[:, P - LAST_TOKENS :]
+            nc.scalar.copy(out=rows, in_=scale[:, g : g + 1, :].to_broadcast(rows.shape))
+
         def h_scale_mul(i, n0):
             halves = hps[i][:].rearrange("p u g n -> p (u g n)").bitcast(BF16)
             src = halves.rearrange("p (u g n e) -> p g n u e", u=2, g=2, e=2)
             dst = h_group(i).rearrange("p (g n u e) -> p g n u e", g=2, u=2, e=2)
-            for g0, g1, n in ((0, 2, 0),) if n0 == 0 else ((0, 1, n0), (1, 2, 0)):
-                if n < P:
-                    nc.vector.tensor_tensor(
-                        out=dst[:, g0:g1, n:P], in0=src[:, g0:g1, n:P],
-                        in1=scale[:, g0:g1, :].rearrange("p g (u e) -> p g u e", u=2).unsqueeze(2).to_broadcast(
-                            [P, g1 - g0, P - n, 2, 2]),
-                        op=ALU.mult)
+            if n0 == 0 or n0 == P:
+                g0 = n0 // P
+                factor = scale[:, g0:2, :].rearrange("p g (u e) -> p g u e", u=2).unsqueeze(2).to_broadcast(
+                    [P, 2 - g0, P, 2, 2])
+                nc.vector.tensor_tensor(out=dst[:, g0:2], in0=src[:, g0:2], in1=factor, op=ALU.mult)
+            else:
+                nc.vector.tensor_tensor(
+                    out=dst.rearrange("p g n u e -> p (g n) u e")[:, n0:], in0=src.rearrange("p g n u e -> p (g n) u e")[:, n0:],
+                    in1=scale_rows[:, n0 - LAST_TOKENS :].rearrange("p n (u e) -> p n u e", u=2), op=ALU.mult)
 
         def h_stage(i, n):
             stage[i] = work.tile([P, n, 2], F32, name=f"st{i}", tag="st", bufs=2, align_bytes=64)
@@ -221,7 +233,8 @@ def tile_mla_pa_t_kernel(tc, h_bytes, h_scale, w_cq, w_q, w_qr, out):
 
         def c_copy(i):
             if i // 2 not in cg:
-                cg[i // 2] = work.tile([P, 2 * CQ], BF16, name=f"cg{i // 2}", tag="cg", bufs=2, align_bytes=64)
+                pool, tag, bufs = (keep, "mix0", 1) if i < 2 else (work, "cg", 2)
+                cg[i // 2] = pool.tile([P, 2 * CQ], BF16, name=f"cg{i // 2}", tag=tag, bufs=bufs, align_bytes=64)
             dst = cg[i // 2][:, CQ * (i % 2) : CQ * (i % 2 + 1)]
             nc.scalar.copy(out=dst.rearrange("p (m e t) -> p m t e", e=2, t=4),
                            in_=cps[i][:].rearrange("p t (m e) -> p m t e", e=2))
@@ -341,18 +354,25 @@ def tile_mla_pa_t_kernel(tc, h_bytes, h_scale, w_cq, w_q, w_qr, out):
 
         def window(w):
             a, b = 2 * w, 2 * w + 1
+            share = POOL_TOKENS if w > 2 else 0
+            h_quant(w)
             if w == 2:
                 quant(w2_codes[:, 512:1024], w2_sc[:, 512:1024], wq_g[:])
-            h_quant(w)
             c_quant(a - 2, a)
-            h_scale_pool(a + 2, POOL_TOKENS)
+            if w == 2:
+                tables_mix(nc.gpsimd, 1, "mix1")
+            else:
+                h_scale_pool(a + 2, share)
             cast(a + 4)
             cast(b + 4)
             if w == 2:
-                second(0)
-                second(1)
+                spread_scale(1)
+                spread_scale(0)
             mm1(a)
             c_copy(a)
+            if w == 2:
+                second(0)
+                second(1)
             mm_u(a - 2)
             mm_u(b - 2)
             rope_add_pair(w - 2)
@@ -361,10 +381,11 @@ def tile_mla_pa_t_kernel(tc, h_bytes, h_scale, w_cq, w_q, w_qr, out):
             mm_sum(a - 2)
             mm_sum(b - 2)
             h_scale_mul(b + 2, 0)
-            h_scale_mul(a + 2, POOL_TOKENS)
-            second(a - 2)
+            h_scale_mul(a + 2, share)
+            mm_a(a - 2)
             h_transpose(a + 4)
             h_stage(a + 4, POOL_TOKENS if w + 3 < NW else LAST_TOKENS)
+            a_copy(a - 2)
             h_transpose(b + 4)
             second(b - 2)
             rope_k23(a - 2)
@@ -376,50 +397,52 @@ def tile_mla_pa_t_kernel(tc, h_bytes, h_scale, w_cq, w_q, w_qr, out):
         for i in range(2):
             cast(i)
             h_transpose(i)
-        tables_sin()
+        table_abs(halves[0])
+        table_sin(halves[0])
+        table_cos(halves[0])
+        wcq_copy(nc.scalar.copy, 1, 2, 4)
         for i in range(2):
             cast(i + 2)
             h_transpose(i + 2, "u", 2)
             h_scale_mul(i, 0)
-        wcq_copy(nc.scalar.copy, 1, 2, 4)
-        tables_cos()
         h_quant(0, 2)
         quant(wcq_codes[:], wcq_sc[:], wcq_g[:])
         wqr_g = keep.tile([P, 2048], BF16, name="wqr_g", tag="wg", align_bytes=64)
         wqr_copy(pool_copy, wqr_g[:, 0:1024], 0)
         cast(4)
         cast(5)
+        h_transpose(4)
         wqr_copy(nc.scalar.copy, wqr_g[:, 1024:2048], 1)
         mm1(0)
         c_copy(0)
         mm1(1)
         c_copy(1)
+        h_transpose(5)
         for i in (2, 3):
-            h_transpose(i + 2)
             h_scale_mul(i, 0)
         h_quant(1, 2)
         quant(w2_codes[:, 0:512], w2_sc[:, 0:512], wqr_g[:])
         c_quant(0, 2)
-        tables_mix(nc.gpsimd, 0, "wg")
-        wq_g = keep.tile([P, 2048], BF16, name="wq_g", align_bytes=64)
-        wq_copy(pool_copy, wq_g[:, 0:768], 0, 192)
-        tables_mix(nc.gpsimd, 1, "mix1")
+        tables_mix(nc.gpsimd, 0, "mix0")
+        wq_g = keep.tile([P, 2048], BF16, name="wq_g", tag="mix1", align_bytes=64)
+        wq_copy(pool_copy, wq_g[:, 0 : 4 * WQ_POOL], 0, WQ_POOL)
         cast(6)
         cast(7)
         mm1(2)
         c_copy(2)
-        wq_copy(nc.scalar.copy, wq_g[:, 768:1280], 192, 320)
         mm_u(0)
         mm_u(1)
-        mm1(3)
-        c_copy(3)
         mm_sum(0)
         mm_sum(1)
-        wq_copy(nc.scalar.copy, wq_g[:, 1280:2048], 320, 512)
+        mm1(3)
+        wq_copy(nc.scalar.copy, wq_g[:, 4 * WQ_POOL :], WQ_POOL, H * DH)
+        c_copy(3)
+        table_abs(halves[1])
+        table_sin(halves[1])
+        table_cos(halves[1])
         for i in (4, 5):
             h_scale_mul(i, 0)
             h_transpose(i + 2)
-        h_stage(6, POOL_TOKENS)
         rope_k23(0)
         rope_k23(1)
         rope_k1_pair(0)

@@ -20,7 +20,7 @@ NW = NT // 2
 NP = DH // 2
 KINDS = 8
 WIDE = 48
-POOL_TOKENS = 92
+POOL_TOKENS = 104
 LAST_TOKENS = 16
 WQ_POOL = 320
 CUTS = (0, 1, 5, 9, 13, 16)
@@ -45,7 +45,7 @@ def tile_mla_pa_t_kernel(tc, h_bytes, h_scale, w_cq, w_q, w_qr, out):
             nc.sync.dma_start(out=rows[:],
                               in_=h_bytes[i0 // KINDS].rearrange("(p j) k -> p j k", j=KINDS)[:, first : first + i1 - i0, :])
             for i in range(i0, i1):
-                hb[i] = rows[:, i - i0, :]
+                hb[i] = (rows, i - i0)
 
         scale = keep.tile([P, 2, 4], F32, name="scale")
         wcq_raw = [keep.tile([P, 4, CQ], BF16, name=f"wcq_raw{g}", align_bytes=64) for g in range(2)]
@@ -164,13 +164,16 @@ def tile_mla_pa_t_kernel(tc, h_bytes, h_scale, w_cq, w_q, w_qr, out):
 
         xb, hps, hg, cg, hq, cq, cps, ups, aps, sps, osb, prods, stage, written = ({} for k in range(14))
 
-        def cast(i):
-            xb[i] = work.tile([P, D], BF16, name=f"x{i}", tag="x", bufs=4, align_bytes=64)
-            nc.scalar.copy(out=xb[i][:], in_=hb[i].bitcast(E4M3))
+        def cast(i, count=1):
+            x = work.tile([P, count * D], BF16, name=f"x{i}", tag="x", bufs=3, align_bytes=64)
+            rows, j = hb[i]
+            nc.scalar.copy(out=x[:], in_=rows[:, j : j + count, :].rearrange("p j k -> p (j k)").bitcast(E4M3))
+            for c in range(count):
+                xb[i + c] = x[:, c * D : (c + 1) * D]
 
         def h_transpose(i, tag="ht", bufs=2):
             hps[i] = psum.tile([P, 2, 2, P], F32, name=f"ht{i}", tag=tag, bufs=bufs)
-            words = xb[i][:].bitcast(F32)
+            words = xb[i].bitcast(F32)
             for g in range(2):
                 for u in range(2):
                     nc.tensor.transpose(hps[i][:, u, g, :], words[:, 256 * g + u : 256 * (g + 1) : 2], ident[:])
@@ -236,8 +239,7 @@ def tile_mla_pa_t_kernel(tc, h_bytes, h_scale, w_cq, w_q, w_qr, out):
                 pool, tag, bufs = (keep, "mix0", 1) if i < 2 else (work, "cg", 2)
                 cg[i // 2] = pool.tile([P, 2 * CQ], BF16, name=f"cg{i // 2}", tag=tag, bufs=bufs, align_bytes=64)
             dst = cg[i // 2][:, CQ * (i % 2) : CQ * (i % 2 + 1)]
-            nc.scalar.copy(out=dst.rearrange("p (m e t) -> p m t e", e=2, t=4),
-                           in_=cps[i][:].rearrange("p t (m e) -> p m t e", e=2))
+            nc.scalar.copy(out=dst.rearrange("p (n t) -> p n t", t=4), in_=cps[i][:].rearrange("p t n -> p n t"))
 
         def c_quant(i0, i1):
             w = i0 // 2
@@ -363,8 +365,7 @@ def tile_mla_pa_t_kernel(tc, h_bytes, h_scale, w_cq, w_q, w_qr, out):
                 tables_mix(nc.gpsimd, 1, "mix1")
             else:
                 h_scale_pool(a + 2, share)
-            cast(a + 4)
-            cast(b + 4)
+            cast(a + 4, 2)
             if w == 2:
                 spread_scale(1)
                 spread_scale(0)
@@ -426,8 +427,7 @@ def tile_mla_pa_t_kernel(tc, h_bytes, h_scale, w_cq, w_q, w_qr, out):
         tables_mix(nc.gpsimd, 0, "mix0")
         wq_g = keep.tile([P, 2048], BF16, name="wq_g", tag="mix1", align_bytes=64)
         wq_copy(pool_copy, wq_g[:, 0 : 4 * WQ_POOL], 0, WQ_POOL)
-        cast(6)
-        cast(7)
+        cast(6, 2)
         mm1(2)
         c_copy(2)
         mm_u(0)

@@ -20,7 +20,7 @@ NW = NT // 2
 NP = DH // 2
 KINDS = 8
 WIDE = 48
-POOL_TOKENS = 104
+POOL_TOKENS = 100
 LAST_TOKENS = 16
 WQ_POOL = 320
 CUTS = (0, 1, 5, 9, 13, 16)
@@ -162,7 +162,7 @@ def tile_mla_pa_t_kernel(tc, h_bytes, h_scale, w_cq, w_q, w_qr, out):
         def quant(codes, sc, grouped):
             nc.vector.quantize_mx(out=codes.bitcast(FP8X4), scales=sc, in_=grouped)
 
-        xb, hps, hg, cg, hq, cq, cps, ups, aps, sps, osb, prods, stage, written = ({} for k in range(14))
+        xb, hps, hg, cg, hq, cq, cps, ups, aps, sps, osb, prods, k1s, stage, written = ({} for k in range(15))
 
         def cast(i, count=1):
             x = work.tile([P, count * D], BF16, name=f"x{i}", tag="x", bufs=3, align_bytes=64)
@@ -204,7 +204,7 @@ def tile_mla_pa_t_kernel(tc, h_bytes, h_scale, w_cq, w_q, w_qr, out):
                     in1=scale_rows[:, n0 - LAST_TOKENS :].rearrange("p n (u e) -> p n u e", u=2), op=ALU.mult)
 
         def h_stage(i, n):
-            stage[i] = work.tile([P, n, 2], F32, name=f"st{i}", tag="st", bufs=2, align_bytes=64)
+            stage[i] = keep.tile([P, n, 2], F32, name=f"st{i}", tag=f"ring{i // 2 % 3}", align_bytes=64)
             nc.scalar.copy(out=stage[i][:], in_=hps[i][:, :, 0, 0:n].rearrange("p u n -> p n u"))
 
         def h_scale_pool(i, n):
@@ -306,8 +306,13 @@ def tile_mla_pa_t_kernel(tc, h_bytes, h_scale, w_cq, w_q, w_qr, out):
 
         def products(w):
             if w not in prods:
-                prods[w] = work.tile([P, 2 * 768], F32, name=f"prod{w}", tag="prod", bufs=3, align_bytes=64)
+                prods[w] = work.tile([P, 2 * 512], F32, name=f"prod{w}", tag="prod", bufs=3, align_bytes=64)
             return prods[w]
+
+        def shared(w):
+            if w not in k1s:
+                k1s[w] = keep.tile([P, 2 * 256], F32, name=f"k1_{w}", tag=f"ring{(w + 2) % 3}", align_bytes=64)
+            return k1s[w]
 
         def rope_k23(i):
             k23 = products(i // 2)[:, 512 * (i % 2) : 512 * (i % 2 + 1)].rearrange("p (n i e) -> p n i e", n=H, e=2)
@@ -317,14 +322,14 @@ def tile_mla_pa_t_kernel(tc, h_bytes, h_scale, w_cq, w_q, w_qr, out):
                                     in1=table.unsqueeze(1).to_broadcast([P, H, NP, 2]), op=ALU.mult)
 
         def rope_k1(i):
-            first = 1024 + 256 * (i % 2)
-            nc.vector.tensor_tensor(out=products(i // 2)[:, first : first + 256].rearrange("p (n i) -> p n i", n=H),
+            first = 256 * (i % 2)
+            nc.vector.tensor_tensor(out=shared(i // 2)[:, first : first + 256].rearrange("p (n i) -> p n i", n=H),
                                     in0=sps[i].rearrange("p (n i) -> p n i", n=H),
                                     in1=cos[:, i % KINDS, :].unsqueeze(1).to_broadcast([P, H, NP]), op=ALU.mult)
 
         def rope_k1_pair(w):
             kind = 2 * w % KINDS
-            nc.vector.tensor_tensor(out=products(w)[:, 1024:1536].rearrange("p (j n i) -> p j n i", j=2, n=H),
+            nc.vector.tensor_tensor(out=shared(w)[:].rearrange("p (j n i) -> p j n i", j=2, n=H),
                                     in0=sps[2 * w, "pair"][:].rearrange("p (j n i) -> p j n i", j=2, n=H),
                                     in1=cos[:, kind : kind + 2, :].unsqueeze(2).to_broadcast([P, 2, H, NP]),
                                     op=ALU.mult)
@@ -333,19 +338,19 @@ def tile_mla_pa_t_kernel(tc, h_bytes, h_scale, w_cq, w_q, w_qr, out):
             key = piece(2 * w, 1)[0]
             nc.gpsimd.tensor_tensor(
                 out=osb[key][:].rearrange("p n (j f i e) -> p f j n i e", j=2, f=2, e=2)[:, 1 - key[1] % 2],
-                in0=products(w)[:, 0:1024].rearrange("p (j n i e) -> p j n i e", j=2, n=H, e=2),
-                in1=products(w)[:, 1024:1536].rearrange("p (j n i) -> p j n i", j=2, n=H).unsqueeze(4).to_broadcast(
+                in0=products(w)[:].rearrange("p (j n i e) -> p j n i e", j=2, n=H, e=2),
+                in1=shared(w)[:].rearrange("p (j n i) -> p j n i", j=2, n=H).unsqueeze(4).to_broadcast(
                     [P, 2, H, NP, 2]),
                 op=ALU.add)
             store(2 * w, 1)
             store(2 * w + 1, 1)
 
         def rope_add(engine, i):
-            first = 1024 + 256 * (i % 2)
+            first = 256 * (i % 2)
             engine.tensor_tensor(
                 out=half(i, 1).rearrange("p n (i e) -> p n i e", e=2),
                 in0=products(i // 2)[:, 512 * (i % 2) : 512 * (i % 2 + 1)].rearrange("p (n i e) -> p n i e", n=H, e=2),
-                in1=products(i // 2)[:, first : first + 256].rearrange("p (n i) -> p n i", n=H).unsqueeze(3).to_broadcast(
+                in1=shared(i // 2)[:, first : first + 256].rearrange("p (n i) -> p n i", n=H).unsqueeze(3).to_broadcast(
                     [P, H, NP, 2]),
                 op=ALU.add)
             store(i, 1)
@@ -375,12 +380,12 @@ def tile_mla_pa_t_kernel(tc, h_bytes, h_scale, w_cq, w_q, w_qr, out):
                 second(0)
                 second(1)
             mm_u(a - 2)
+            mm_sum(a - 2)
+            mm_sum(b - 2)
             mm_u(b - 2)
             rope_add_pair(w - 2)
             mm1(b)
             c_copy(b)
-            mm_sum(a - 2)
-            mm_sum(b - 2)
             h_scale_mul(b + 2, 0)
             h_scale_mul(a + 2, share)
             mm_a(a - 2)
@@ -455,10 +460,10 @@ def tile_mla_pa_t_kernel(tc, h_bytes, h_scale, w_cq, w_q, w_qr, out):
         rope_add_pair(NW - 4)
         mm1(a + 2)
         c_copy(a + 2)
-        second(a)
-        mm_u(a)
         mm1(a + 3)
         c_copy(a + 3)
+        mm_u(a)
+        second(a)
         mm_sum(a, "sum", 1)
         mm_u(a + 1)
         second(a + 1)
@@ -495,7 +500,7 @@ def tile_mla_pa_t_kernel(tc, h_bytes, h_scale, w_cq, w_q, w_qr, out):
             second(i)
         rope_k23(a + 4)
         rope_k1(a + 4)
+        rope_k1(a + 5)
         rope_k23(a + 5)
         rope_add(nc.vector, a + 4)
-        rope_k1(a + 5)
         rope_add(nc.vector, a + 5)

@@ -23,8 +23,7 @@ WIDE = 48
 POOL_TOKENS = 100
 LAST_TOKENS = 16
 WQ_POOL = 320
-CUTS = (0, 1, 5, 9, 13, 16)
-LAST_CUTS = (0, 1, 5, 7, 9, 11, 13, 15, 16)
+SINGLE = 6
 
 FLOPS = 2 * B * S * (D * CQ + 2 * CQ * H * DH) + 3 * B * S * H * DH
 
@@ -162,7 +161,7 @@ def tile_mla_pa_t_kernel(tc, h_bytes, h_scale, w_cq, w_q, w_qr, out):
         def quant(codes, sc, grouped):
             nc.vector.quantize_mx(out=codes.bitcast(FP8X4), scales=sc, in_=grouped)
 
-        xb, hps, hg, cg, hq, cq, cps, ups, aps, sps, osb, prods, k1s, stage, written = ({} for k in range(15))
+        xb, hps, hg, cg, hq, cq, cps, ups, aps, sps, osb, prods, k1s, stage = ({} for k in range(14))
 
         def cast(i, count=1):
             x = work.tile([P, count * D], BF16, name=f"x{i}", tag="x", bufs=3, align_bytes=64)
@@ -275,30 +274,18 @@ def tile_mla_pa_t_kernel(tc, h_bytes, h_scale, w_cq, w_q, w_qr, out):
             aps[i] = psum.tile([P, 512], F32, name=f"ap{i}", tag="m", bufs=3)
             mm2(i, aps[i][:], 512, 1024, True, True)
 
-        def piece(i, part):
-            n = 2 * (i % KINDS) + part
-            cuts = LAST_CUTS if i >= NT - KINDS else CUTS
-            first = max(cut for cut in cuts if cut <= n)
-            count = cuts[cuts.index(first) + 1] - first
-            key = (i // KINDS, first)
-            if key not in osb:
-                if count > 2:
-                    osb[key] = work.tile([P, H, 4 * DH], F32, name=f"o{i}", tag="o", bufs=3, align_bytes=64)
-                else:
-                    osb[key] = keep.tile([P, H, count * DH], F32, name=f"last{i}_{part}", align_bytes=64)
-            return key, count
-
         def half(i, part):
-            key = piece(i, part)[0]
-            n = 2 * (i % KINDS) + part - key[1]
-            return osb[key][:, :, n * DH : (n + 1) * DH]
+            key = (i // 2, "pair") if part == 1 and i < NT - SINGLE else (i, part)
+            if key not in osb:
+                if key[1] == "pair":
+                    osb[key] = keep.tile([P, 2, H, DH], F32, name=f"r{i}", align_bytes=64)
+                else:
+                    osb[key] = work.tile([P, H, DH], F32, name=f"o{i}_{part}", tag="half", bufs=8, align_bytes=64)
+            return osb[key][:, i % 2] if key[1] == "pair" else osb[key][:]
 
         def store(i, part):
-            key, count = piece(i, part)
-            written[key] = written.get(key, 0) + 1
-            if written[key] == count:
-                rows = out[key[0]].rearrange("n (p j) d -> p n (j d)", j=KINDS)
-                nc.sync.dma_start(out=rows[:, :, key[1] * DH : (key[1] + count) * DH], in_=osb[key][:, :, 0 : count * DH])
+            rows = out[i // KINDS].rearrange("n (p j) (f d) -> j f p n d", j=KINDS, f=2)
+            nc.sync.dma_start(out=rows[i % KINDS, part], in_=half(i, part))
 
         def a_copy(i):
             nc.scalar.copy(out=half(i, 0), in_=aps[i][:].rearrange("p (n d) -> p n d", n=H))
@@ -335,9 +322,9 @@ def tile_mla_pa_t_kernel(tc, h_bytes, h_scale, w_cq, w_q, w_qr, out):
                                     op=ALU.mult)
 
         def rope_add_pair(w):
-            key = piece(2 * w, 1)[0]
+            half(2 * w, 1)
             nc.gpsimd.tensor_tensor(
-                out=osb[key][:].rearrange("p n (j f i e) -> p f j n i e", j=2, f=2, e=2)[:, 1 - key[1] % 2],
+                out=osb[w, "pair"][:].rearrange("p j n (i e) -> p j n i e", e=2),
                 in0=products(w)[:].rearrange("p (j n i e) -> p j n i e", j=2, n=H, e=2),
                 in1=shared(w)[:].rearrange("p (j n i) -> p j n i", j=2, n=H).unsqueeze(4).to_broadcast(
                     [P, 2, H, NP, 2]),

@@ -404,12 +404,12 @@ def tile_mla_pa_t_kernel(tc, h_bytes, h_scale, w_cq, w_q, w_qr, out):
         wqr_copy(pool_copy, wqr_g[:, 0:1024], 0)
         cast(4)
         cast(5)
-        h_transpose(4)
         wqr_copy(nc.scalar.copy, wqr_g[:, 1024:2048], 1)
         mm1(0)
         c_copy(0)
         mm1(1)
         c_copy(1)
+        h_transpose(4)
         h_transpose(5)
         for i in (2, 3):
             h_scale_mul(i, 0)

from contextlib import ExitStack
import math

import concourse.mybir as mybir

F32 = mybir.dt.float32
BF16 = mybir.dt.bfloat16
U32 = mybir.dt.uint32
I32 = mybir.dt.int32
U8 = mybir.dt.uint8
E4M3 = mybir.dt.float8_e4m3fn
FP8X4 = mybir.dt.float8_e4m3fn_x4
ALU = mybir.AluOpType
ACT = mybir.ActivationFunctionType

B, S, D, H, DH, CQ = 4, 1024, 1024, 4, 128, 512
P = 128
NT = B * S // P
NW = NT // 2
NP = DH // 2
KINDS = 8
WIDE = 48
POOL_TOKENS = 100
LAST_TOKENS = 16
WQ_POOL = 320
SINGLE = 6

FLOPS = 2 * B * S * (D * CQ + 2 * CQ * H * DH) + 3 * B * S * H * DH


def tile_mla_pa_t_kernel(tc, h_bytes, h_scale, w_cq, w_q, w_qr, out):
    nc = tc.nc
    with ExitStack() as ctx:
        keep = ctx.enter_context(tc.tile_pool(name="keep", bufs=1))
        work = ctx.enter_context(tc.tile_pool(name="work", bufs=2))
        psum = ctx.enter_context(tc.psum_pool(name="psum", bufs=2))
        ctx.enter_context(tc.manual_schedule())

        hb = {}

        def load_h(i0, i1):
            rows = keep.tile([P, i1 - i0, D], U8, name=f"hb{i0}", align_bytes=64)
            first = i0 % KINDS
            nc.sync.dma_start(out=rows[:],
                              in_=h_bytes[i0 // KINDS].rearrange("(p j) k -> p j k", j=KINDS)[:, first : first + i1 - i0, :])
            for i in range(i0, i1):
                hb[i] = (rows, i - i0)

        scale = keep.tile([P, 2, 4], F32, name="scale")
        wcq_raw = [keep.tile([P, 4, CQ], BF16, name=f"wcq_raw{g}", align_bytes=64) for g in range(2)]
        wq_raw = keep.tile([P, 4, H * DH], BF16, name="wq_raw", align_bytes=64)
        wqr_raw = keep.tile([P, 4, H * DH], BF16, name="wqr_raw", align_bytes=64)

        def load_wcq(g):
            nc.sync.dma_start(out=wcq_raw[g][:],
                              in_=w_cq[g * 512 : (g + 1) * 512, :].rearrange("(p j) c -> p j c", j=4))

        load_h(0, 1)
        load_h(1, 2)
        load_wcq(0)
        nc.sync.dma_start(out=scale[:], in_=h_scale.rearrange("a b (g p t) -> p (a b g) t", g=2, t=4))
        load_wcq(1)
        load_h(2, 4)
        nc.sync.dma_start(out=wqr_raw[:], in_=w_qr.rearrange("(p j) c -> p j c", j=4))
        load_h(4, 6)
        nc.sync.dma_start(out=wq_raw[:], in_=w_q.rearrange("(p j) c -> p j c", j=4))
        load_h(6, 8)
        for i in range(8, NT, 4):
            load_h(i, i + 4)

        pos = keep.tile([P, KINDS], F32, name="pos")
        nc.gpsimd.iota(pos[:], pattern=[[1, KINDS]], base=0, channel_multiplier=KINDS,
                       allow_small_or_imprecise_dtypes=True)
        offs = keep.tile([P, P], F32, name="offs", align_bytes=64)
        nc.gpsimd.iota(offs[:], pattern=[[1, P]], base=0, channel_multiplier=-1,
                       allow_small_or_imprecise_dtypes=True)
        one = keep.tile([P, 1], F32, name="one")
        nc.vector.memset(one[:], 1.0)

        def constant(dst, value):
            nc.vector.tensor_scalar(out=dst, in0=one[:], scalar1=value, scalar2=None, op0=ALU.mult)

        th = keep.tile([P, NP], F32, name="th")
        for a in range(NP - 4, NP):
            constant(th[:, a : a + 1], 10000.0 ** (-a / NP) / (2.0 * math.pi))
        hpi = keep.tile([P, 1], F32, name="hpi")
        constant(hpi[:], math.pi / 2)

        def spread(w):
            for a in range(1, 4):
                nc.vector.tensor_scalar(out=th[:, NP - (a + 1) * w : NP - a * w], in0=th[:, NP - w : NP],
                                        scalar1=10000.0 ** (a * w / NP), scalar2=None, op0=ALU.mult)

        turns = keep.tile([P, KINDS, WIDE], F32, name="turns", align_bytes=64)
        whole = keep.tile([P, KINDS, WIDE], I32, name="whole", align_bytes=64)
        frac = keep.tile([P, KINDS, NP], F32, name="frac", align_bytes=64)
        fabs = keep.tile([P, KINDS, NP], F32, name="fabs", align_bytes=64)
        sines = keep.tile([P, 2, KINDS, NP], F32, name="sines", align_bytes=64)
        cos = keep.tile([P, KINDS, NP], F32, name="cos", align_bytes=64)

        def angles(dst, k0, k1, i0, i1):
            shape = [P, k1 - k0, i1 - i0]
            nc.vector.tensor_tensor(out=dst, in0=pos[:, k0:k1].unsqueeze(2).to_broadcast(shape),
                                    in1=th[:, i0:i1].unsqueeze(1).to_broadcast(shape), op=ALU.mult)

        spread(4)
        ident = keep.tile([P, P], F32, name="ident", align_bytes=64)
        nc.vector.tensor_scalar(out=ident[:], in0=offs[:], scalar1=0.0, scalar2=None, op0=ALU.is_equal)
        angles(frac[:, :, WIDE:NP], 0, KINDS, WIDE, NP)
        nc.scalar.activation(out=sines[:, 1, :, WIDE:NP], in_=frac[:, :, WIDE:NP], func=ACT.Sin, scale=2.0 * math.pi)
        spread(16)
        halves = [slice(0, 4), slice(4, KINDS)]
        for ks in halves:
            angles(turns[:, ks], ks.start, ks.stop, 0, WIDE)
        for ks in halves:
            nc.vector.tensor_copy(out=whole[:, ks], in_=turns[:, ks])
        for ks in halves:
            nc.vector.tensor_tensor(out=frac[:, ks, 0:WIDE], in0=turns[:, ks], in1=whole[:, ks], op=ALU.subtract)

        def table_sin(ks):
            nc.scalar.activation(out=sines[:, 1, ks, 0:WIDE], in_=frac[:, ks, 0:WIDE], func=ACT.Sin, scale=2.0 * math.pi)
            nc.scalar.activation(out=sines[:, 0, ks], in_=frac[:, ks], func=ACT.Sin, scale=-2.0 * math.pi)

        def table_abs(ks):
            nc.scalar.activation(out=fabs[:, ks], in_=frac[:, ks], func=ACT.Abs)

        def table_cos(ks):
            nc.scalar.activation(out=cos[:, ks], in_=fabs[:, ks], func=ACT.Sin, scale=-2.0 * math.pi, bias=hpi[:, 0:1])

        mix = {}

        def tables_mix(engine, f, tag):
            mix[f] = keep.tile([P, 4 * NP, 2], F32, name=f"mix{f}", tag=tag, align_bytes=64)
            kinds = slice(4 * f, 4 * f + 4)
            engine.tensor_tensor(
                out=mix[f][:], in0=sines[:, :, kinds, :].rearrange("p e k i -> p (k i) e"),
                in1=cos[:, kinds, :].rearrange("p k i -> p (k i)").unsqueeze(2).to_broadcast([P, 4 * NP, 2]),
                op=ALU.subtract)

        wcq_codes = keep.tile([P, 2 * CQ], U32, name="wcq_codes", align_bytes=64)
        wcq_sc = keep.tile([P, 2 * CQ], U8, name="wcq_sc", align_bytes=64)
        w2_codes = keep.tile([P, 1024], U32, name="w2_codes", align_bytes=64)
        w2_sc = keep.tile([P, 1024], U8, name="w2_sc", align_bytes=64)
        wcq_g = keep.tile([P, 8 * CQ], BF16, name="wcq_g", tag="wg", align_bytes=64)

        def pool_copy(out, in_):
            nc.gpsimd.tensor_scalar(out=out, in0=in_, scalar1=1.0, scalar2=0.0, op0=ALU.mult, op1=ALU.add)

        def wcq_copy(copy, g, t0, t1):
            copy(out=wcq_g[:, CQ * (4 * g + t0) : CQ * (4 * g + t1)].rearrange("p (t m j) -> p t m j", m=P, j=4),
                 in_=wcq_raw[g][:].rearrange("p j (m t) -> p t m j", t=4)[:, t0:t1])

        def wqr_copy(copy, dst, f):
            copy(out=dst.rearrange("p (c m j) -> p c m j", c=2, j=4),
                 in_=wqr_raw[:].rearrange("p j (c m e) -> p e c m j", c=2, e=2)[:, 1 - f])

        def wq_copy(copy, dst, n0, n1):
            copy(out=dst.rearrange("p (c n j) -> p c n j", c=2, j=4),
                 in_=wq_raw[:, :, n0:n1].rearrange("p j (c n) -> p c n j", c=2))

        def quant(codes, sc, grouped):
            nc.vector.quantize_mx(out=codes.bitcast(FP8X4), scales=sc, in_=grouped)

        xb, hps, hg, cg, hq, cq, cps, ups, aps, sps, osb, prods, k1s, stage = ({} for k in range(14))

        def cast(i, count=1):
            x = work.tile([P, count * D], BF16, name=f"x{i}", tag="x", bufs=3, align_bytes=64)
            rows, j = hb[i]
            nc.scalar.copy(out=x[:], in_=rows[:, j : j + count, :].rearrange("p j k -> p (j k)").bitcast(E4M3))
            for c in range(count):
                xb[i + c] = x[:, c * D : (c + 1) * D]

        def h_transpose(i, tag="ht", bufs=2):
            hps[i] = psum.tile([P, 2, 2, P], F32, name=f"ht{i}", tag=tag, bufs=bufs)
            words = xb[i].bitcast(F32)
            for g in range(2):
                for u in range(2):
                    nc.tensor.transpose(hps[i][:, u, g, :], words[:, 256 * g + u : 256 * (g + 1) : 2], ident[:])

        def h_group(i):
            if i // 2 not in hg:
                hg[i // 2] = work.tile([P, 2 * D], BF16, name=f"hg{i // 2}", tag="hg", bufs=1, align_bytes=64)
            return hg[i // 2][:, D * (i % 2) : D * (i % 2 + 1)]

        scale_rows = keep.tile([P, 2 * P - LAST_TOKENS, 4], F32, name="scale_rows", align_bytes=64)

        def spread_scale(g):
            rows = scale_rows[:, 0 : P - LAST_TOKENS] if g == 0 else scale_rows[:, P - LAST_TOKENS :]
            nc.scalar.copy(out=rows, in_=scale[:, g : g + 1, :].to_broadcast(rows.shape))

        def h_scale_mul(i, n0):
            halves = hps[i][:].rearrange("p u g n -> p (u g n)").bitcast(BF16)
            src = halves.rearrange("p (u g n e) -> p g n u e", u=2, g=2, e=2)
            dst = h_group(i).rearrange("p (g n u e) -> p g n u e", g=2, u=2, e=2)
            if n0 == 0 or n0 == P:
                g0 = n0 // P
                factor = scale[:, g0:2, :].rearrange("p g (u e) -> p g u e", u=2).unsqueeze(2).to_broadcast(
                    [P, 2 - g0, P, 2, 2])
                nc.vector.tensor_tensor(out=dst[:, g0:2], in0=src[:, g0:2], in1=factor, op=ALU.mult)
            else:
                nc.vector.tensor_tensor(
                    out=dst.rearrange("p g n u e -> p (g n) u e")[:, n0:], in0=src.rearrange("p g n u e -> p (g n) u e")[:, n0:],
                    in1=scale_rows[:, n0 - LAST_TOKENS :].rearrange("p n (u e) -> p n u e", u=2), op=ALU.mult)

        def h_stage(i, n):
            stage[i] = keep.tile([P, n, 2], F32, name=f"st{i}", tag=f"ring{i // 2 % 3}", align_bytes=64)
            nc.scalar.copy(out=stage[i][:], in_=hps[i][:, :, 0, 0:n].rearrange("p u n -> p n u"))

        def h_scale_pool(i, n):
            src = stage[i][:].rearrange("p n u -> p (n u)").bitcast(BF16).rearrange("p (n t) -> p n t", t=4)
            nc.gpsimd.tensor_tensor(
                out=h_group(i)[:, 0 : 4 * n].rearrange("p (n t) -> p n t", t=4), in0=src,
                in1=scale[:, 0:1, :].to_broadcast([P, n, 4]), op=ALU.mult)

        def h_quant(w, parts=1):
            codes = work.tile([P, 512], U32, name=f"hq{w}", tag="hq", bufs=2, align_bytes=64)
            sc = work.tile([P, 512], U8, name=f"hs{w}", tag="hs", bufs=2, align_bytes=64)
            for c in range(0, 512, 512 // parts):
                cols = slice(c, c + 512 // parts)
                quant(codes[:, cols], sc[:, cols], hg[w][:, 4 * cols.start : 4 * cols.stop])
            hq[w] = (codes, sc)

        def mm1(i, tag="m", bufs=3):
            codes, sc = hq[i // 2]
            cps[i] = psum.tile([P, 4, P], F32, name=f"cp{i}", tag=tag, bufs=bufs)
            for t in range(4):
                for g in range(2):
                    cols = slice((2 * (i % 2) + g) * P, (2 * (i % 2) + g + 1) * P)
                    nc.tensor.matmul_mx(
                        out=cps[i][:, t, :],
                        lhsT=wcq_codes[:, (4 * g + t) * P : (4 * g + t + 1) * P].bitcast(FP8X4),
                        lhsT_scale=wcq_sc[:, (4 * g + t) * P : (4 * g + t + 1) * P],
                        rhs=codes[:, cols].bitcast(FP8X4), rhs_scale=sc[:, cols],
                        start=(g == 0), stop=(g == 1))

        def c_copy(i):
            if i // 2 not in cg:
                pool, tag, bufs = (keep, "mix0", 1) if i < 2 else (work, "cg", 2)
                cg[i // 2] = pool.tile([P, 2 * CQ], BF16, name=f"cg{i // 2}", tag=tag, bufs=bufs, align_bytes=64)
            dst = cg[i // 2][:, CQ * (i % 2) : CQ * (i % 2 + 1)]
            nc.scalar.copy(out=dst.rearrange("p (n t) -> p n t", t=4), in_=cps[i][:].rearrange("p t n -> p n t"))

        def c_quant(i0, i1):
            w = i0 // 2
            if w not in cq:
                cq[w] = (work.tile([P, 2 * P], U32, name=f"cq{w}", tag="cq", bufs=2, align_bytes=64),
                         work.tile([P, 2 * P], U8, name=f"cs{w}", tag="cs", bufs=2, align_bytes=64))
            codes, sc = cq[w]
            lo, hi = P * (i0 - 2 * w), P * (i1 - 2 * w)
            quant(codes[:, lo:hi], sc[:, lo:hi], cg[w][:, 4 * lo : 4 * hi])

        def mm2(i, dst, c0, c1, start, stop):
            codes, sc = cq[i // 2]
            cols = slice(P * (i % 2), P * (i % 2 + 1))
            nc.tensor.matmul_mx(out=dst, lhsT=codes[:, cols].bitcast(FP8X4), lhsT_scale=sc[:, cols],
                                rhs=w2_codes[:, c0:c1].bitcast(FP8X4), rhs_scale=w2_sc[:, c0:c1],
                                start=start, stop=stop)

        def mm_u(i, tag="u"):
            ups[i] = psum.tile([P, 512], F32, name=f"up{i}", tag=tag, bufs=2)
            mm2(i, ups[i][:], 0, 512, True, True)

        def mm_sum(i, tag=None, bufs=2):
            if tag:
                sps[i] = psum.tile([P, 256], F32, name=f"sp{i}", tag=tag, bufs=bufs)[:]
            else:
                if i % 2 == 0:
                    sps[i, "pair"] = psum.tile([P, 512], F32, name=f"sp{i}", tag="sum", bufs=1)
                sps[i] = sps[i - i % 2, "pair"][:, 256 * (i % 2) : 256 * (i % 2 + 1)]
            mm2(i, sps[i], 0, 256, True, False)
            mm2(i, sps[i], 256, 512, False, True)

        def mm_a(i):
            aps[i] = psum.tile([P, 512], F32, name=f"ap{i}", tag="m", bufs=3)
            mm2(i, aps[i][:], 512, 1024, True, True)

        def half(i, part):
            key = (i // 2, "pair") if part == 1 and i < NT - SINGLE else (i, part)
            if key not in osb:
                if key[1] == "pair":
                    osb[key] = keep.tile([P, 2, H, DH], F32, name=f"r{i}", align_bytes=64)
                else:
                    osb[key] = work.tile([P, H, DH], F32, name=f"o{i}_{part}", tag="half", bufs=8, align_bytes=64)
            return osb[key][:, i % 2] if key[1] == "pair" else osb[key][:]

        def store(i, part):
            rows = out[i // KINDS].rearrange("n (p j) (f d) -> j f p n d", j=KINDS, f=2)
            nc.sync.dma_start(out=rows[i % KINDS, part], in_=half(i, part))

        def a_copy(i):
            nc.scalar.copy(out=half(i, 0), in_=aps[i][:].rearrange("p (n d) -> p n d", n=H))
            store(i, 0)

        def products(w):
            if w not in prods:
                prods[w] = work.tile([P, 2 * 512], F32, name=f"prod{w}", tag="prod", bufs=3, align_bytes=64)
            return prods[w]

        def shared(w):
            if w not in k1s:
                k1s[w] = keep.tile([P, 2 * 256], F32, name=f"k1_{w}", tag=f"ring{(w + 2) % 3}", align_bytes=64)
            return k1s[w]

        def rope_k23(i):
            k23 = products(i // 2)[:, 512 * (i % 2) : 512 * (i % 2 + 1)].rearrange("p (n i e) -> p n i e", n=H, e=2)
            kind = i % KINDS
            table = mix[kind // 4][:, NP * (kind % 4) : NP * (kind % 4 + 1), :]
            nc.vector.tensor_tensor(out=k23, in0=ups[i][:].rearrange("p (f n i) -> p n i f", f=2, n=H),
                                    in1=table.unsqueeze(1).to_broadcast([P, H, NP, 2]), op=ALU.mult)

        def rope_k1(i):
            first = 256 * (i % 2)
            nc.vector.tensor_tensor(out=shared(i // 2)[:, first : first + 256].rearrange("p (n i) -> p n i", n=H),
                                    in0=sps[i].rearrange("p (n i) -> p n i", n=H),
                                    in1=cos[:, i % KINDS, :].unsqueeze(1).to_broadcast([P, H, NP]), op=ALU.mult)

        def rope_k1_pair(w):
            kind = 2 * w % KINDS
            nc.vector.tensor_tensor(out=shared(w)[:].rearrange("p (j n i) -> p j n i", j=2, n=H),
                                    in0=sps[2 * w, "pair"][:].rearrange("p (j n i) -> p j n i", j=2, n=H),
                                    in1=cos[:, kind : kind + 2, :].unsqueeze(2).to_broadcast([P, 2, H, NP]),
                                    op=ALU.mult)

        def rope_add_pair(w):
            half(2 * w, 1)
            nc.gpsimd.tensor_tensor(
                out=osb[w, "pair"][:].rearrange("p j n (i e) -> p j n i e", e=2),
                in0=products(w)[:].rearrange("p (j n i e) -> p j n i e", j=2, n=H, e=2),
                in1=shared(w)[:].rearrange("p (j n i) -> p j n i", j=2, n=H).unsqueeze(4).to_broadcast(
                    [P, 2, H, NP, 2]),
                op=ALU.add)
            store(2 * w, 1)
            store(2 * w + 1, 1)

        def rope_add(engine, i):
            first = 256 * (i % 2)
            engine.tensor_tensor(
                out=half(i, 1).rearrange("p n (i e) -> p n i e", e=2),
                in0=products(i // 2)[:, 512 * (i % 2) : 512 * (i % 2 + 1)].rearrange("p (n i e) -> p n i e", n=H, e=2),
                in1=shared(i // 2)[:, first : first + 256].rearrange("p (n i) -> p n i", n=H).unsqueeze(3).to_broadcast(
                    [P, H, NP, 2]),
                op=ALU.add)
            store(i, 1)

        def second(i):
            mm_a(i)
            a_copy(i)

        def window(w):
            a, b = 2 * w, 2 * w + 1
            share = POOL_TOKENS if w > 2 else 0
            h_quant(w)
            if w == 2:
                quant(w2_codes[:, 512:1024], w2_sc[:, 512:1024], wq_g[:])
            c_quant(a - 2, a)
            if w == 2:
                tables_mix(nc.gpsimd, 1, "mix1")
            else:
                h_scale_pool(a + 2, share)
            cast(a + 4, 2)
            if w == 2:
                spread_scale(1)
                spread_scale(0)
            mm1(a)
            c_copy(a)
            if w == 2:
                second(0)
                second(1)
            mm_u(a - 2)
            mm_sum(a - 2)
            mm_sum(b - 2)
            mm_u(b - 2)
            rope_add_pair(w - 2)
            mm1(b)
            c_copy(b)
            h_scale_mul(b + 2, 0)
            h_scale_mul(a + 2, share)
            mm_a(a - 2)
            h_transpose(a + 4)
            h_stage(a + 4, POOL_TOKENS if w + 3 < NW else LAST_TOKENS)
            a_copy(a - 2)
            h_transpose(b + 4)
            second(b - 2)
            rope_k23(a - 2)
            rope_k23(b - 2)
            rope_k1_pair(w - 1)

        wcq_copy(nc.vector.tensor_copy, 0, 0, 4)
        wcq_copy(pool_copy, 1, 0, 2)
        for i in range(2):
            cast(i)
            h_transpose(i)
        table_abs(halves[0])
        table_sin(halves[0])
        table_cos(halves[0])
        wcq_copy(nc.scalar.copy, 1, 2, 4)
        for i in range(2):
            cast(i + 2)
            h_transpose(i + 2, "u", 2)
            h_scale_mul(i, 0)
        h_quant(0, 2)
        quant(wcq_codes[:], wcq_sc[:], wcq_g[:])
        wqr_g = keep.tile([P, 2048], BF16, name="wqr_g", tag="wg", align_bytes=64)
        wqr_copy(pool_copy, wqr_g[:, 0:1024], 0)
        cast(4)
        cast(5)
        wqr_copy(nc.scalar.copy, wqr_g[:, 1024:2048], 1)
        mm1(0)
        c_copy(0)
        mm1(1)
        c_copy(1)
        h_transpose(4)
        h_transpose(5)
        for i in (2, 3):
            h_scale_mul(i, 0)
        h_quant(1, 2)
        quant(w2_codes[:, 0:512], w2_sc[:, 0:512], wqr_g[:])
        c_quant(0, 2)
        tables_mix(nc.gpsimd, 0, "mix0")
        wq_g = keep.tile([P, 2048], BF16, name="wq_g", tag="mix1", align_bytes=64)
        wq_copy(pool_copy, wq_g[:, 0 : 4 * WQ_POOL], 0, WQ_POOL)
        cast(6, 2)
        mm1(2)
        c_copy(2)
        mm_u(0)
        mm_u(1)
        mm_sum(0)
        mm_sum(1)
        mm1(3)
        wq_copy(nc.scalar.copy, wq_g[:, 4 * WQ_POOL :], WQ_POOL, H * DH)
        c_copy(3)
        table_abs(halves[1])
        table_sin(halves[1])
        table_cos(halves[1])
        for i in (4, 5):
            h_scale_mul(i, 0)
            h_transpose(i + 2)
        rope_k23(0)
        rope_k23(1)
        rope_k1_pair(0)
        for w in range(2, NW - 2):
            window(w)
        a = NT - 6
        h_quant(NW - 2)
        c_quant(a, a + 2)
        h_scale_pool(a + 4, LAST_TOKENS)
        rope_add_pair(NW - 4)
        mm1(a + 2)
        c_copy(a + 2)
        mm1(a + 3)
        c_copy(a + 3)
        mm_u(a)
        second(a)
        mm_sum(a, "sum", 1)
        mm_u(a + 1)
        second(a + 1)
        h_scale_mul(a + 5, 0)
        h_scale_mul(a + 4, LAST_TOKENS)
        mm_sum(a + 1, "ht")
        rope_k23(a)
        c_quant(a + 2, a + 4)
        rope_k1(a)
        h_quant(NW - 1)
        rope_add(nc.gpsimd, a)
        mm_u(a + 2)
        second(a + 2)
        mm_sum(a + 2, "sum", 1)
        mm1(a + 4)
        c_copy(a + 4)
        mm_u(a + 3, "ht")
        mm1(a + 5)
        c_copy(a + 5)
        rope_k23(a + 1)
        rope_k1(a + 1)
        rope_add(nc.gpsimd, a + 1)
        mm_sum(a + 3, "ht")
        second(a + 3)
        for i in (a + 2, a + 3):
            rope_k23(i)
            rope_k1(i)
        c_quant(a + 4, a + 6)
        rope_add(nc.vector, a + 2)
        rope_add(nc.vector, a + 3)
        for i in (a + 4, a + 5):
            mm_u(i)
            mm_sum(i, "ht")
            second(i)
        rope_k23(a + 4)
        rope_k1(a + 4)
        rope_k1(a + 5)
        rope_k23(a + 5)
        rope_add(nc.vector, a + 4)
        rope_add(nc.vector, a + 5)
